import numpy as np
import ml_dtypes


def mxq(x, axis, fmt="e4m3"):
    dtype, down = {"e4m3": (ml_dtypes.float8_e4m3fn, 7), "e5m2": (ml_dtypes.float8_e5m2, 14)}[fmt]
    v = np.moveaxis(np.asarray(x, np.float32).astype(ml_dtypes.bfloat16).astype(np.float64), axis, -1)
    blocks = v.reshape(v.shape[:-1] + (-1, 32))
    amax = np.abs(blocks).max(-1, keepdims=True)
    byte = np.maximum(np.where(amax > 0, np.frexp(amax)[1] - 1 + 127, 0) - down, 1)
    scale = np.exp2(byte - 127.0)
    codes = (blocks / scale).astype(np.float32).astype(dtype).astype(np.float64)
    return np.moveaxis((codes * scale).reshape(v.shape), -1, axis)


WIDE = False


def mx_kscale(k):
    if not WIDE:
        return np.ones(k)
    levels = np.array([10, -10, 5, -5, 0])
    a = np.random.permutation(np.resize(levels, k // 512 * 4)).reshape(k // 512, 4)
    idx = np.arange(k)
    return np.exp2(a[idx // 512, idx % 128 // 32])


BF16 = ml_dtypes.bfloat16


def bf(x):
    return np.asarray(x, np.float32).astype(BF16)


def f64(x):
    return np.asarray(x).astype(np.float64)


B, F0, FK, S1, S2, D = 256, 8, 128, 128, 1024, 16
M1 = F0 * FK
M2 = F0 * S1


def setup_inputs():
    u = mx_kscale(M2).reshape(F0, S1)[:, 0]
    t = mx_kscale(M1).reshape(F0, FK)[0]
    w1 = np.random.standard_normal((F0, FK, S1)) / np.sqrt(M1) / u[:, None, None] / t[None, :, None]
    w2 = np.random.standard_normal((F0, S1, S2)) / np.sqrt(M2) / u[:, None, None]
    return {"x": bf(np.random.standard_normal((B, F0, D)) * u[None, :, None]),
            "x1": bf(np.random.standard_normal((B, FK, D)) * t[None, :, None]),
            "w1": bf(w1.reshape(M1, S1)), "b1": bf(np.random.standard_normal(S1) * 0.2),
            "w2": bf(w2.reshape(M2, S2)), "b2": bf(np.random.standard_normal(S2) * 0.2)}


def reference(x, x1, w1, b1, w2, b2):
    x0 = f64(x).transpose(0, 2, 1)
    xk = f64(x1).transpose(0, 2, 1)
    z1 = (x0[:, :, :, None] * xk[:, :, None, :]).reshape(B, D, M1)
    o1 = (mxq(z1, 2, "e4m3") @ mxq(f64(w1), 0, "e4m3")) + f64(b1)
    z2 = (x0[:, :, :, None] * o1[:, :, None, :]).reshape(B, D, M2)
    o2 = (mxq(z2, 2, "e4m3") @ mxq(f64(w2), 0, "e4m3")) + f64(b2)
    return np.concatenate([o1.sum(axis=1), o2.sum(axis=1)], axis=1)

@@ -1,0 +1,283 @@
+from concourse import mybir
+from concourse.masks import make_identity
+
+BF16 = mybir.dt.bfloat16
+F32 = mybir.dt.float32
+U32 = mybir.dt.uint32
+U8 = mybir.dt.uint8
+FP8X4 = mybir.dt.float8_e4m3fn_x4
+MULT = mybir.AluOpType.mult
+ADD = mybir.AluOpType.add
+
+P = 128
+PACK = 4
+B, F0, FK, S1, S2, D = 256, 8, 128, 128, 1024, 16
+PASSES = F0 // PACK
+SAMPLE_TILES = B // P
+D_ROUND = 4
+ROUNDS_PER_TILE = D // D_ROUND
+ROUNDS = SAMPLE_TILES * ROUNDS_PER_TILE
+ROWS = D_ROUND * P
+N2 = 512
+HALVES = S2 // N2
+
+FLOPS = 2 * B * D * (F0 * FK * S1 + F0 * S1 * S2)
+
+
+def tile_cin_pa_t_kernel(tc, x, x1, w1, b1, w2, b2, out):
+    nc = tc.nc
+    with (
+        tc.manual_schedule(),
+        tc.tile_pool(name="keep", bufs=1) as keep,
+        tc.tile_pool(name="raw", bufs=4) as raw_pool,
+        tc.tile_pool(name="two", bufs=2) as two,
+        tc.tile_pool(name="three", bufs=3) as three,
+        tc.psum_pool(name="bank", bufs=1) as bank,
+        tc.psum_pool(name="spread", bufs=3) as spread,
+    ):
+        x_sb = keep.tile([P, SAMPLE_TILES * F0 * D], BF16, name="x_sb")
+        nc.sync.dma_start(
+            out=x_sb.rearrange("p (s f) -> p s f", s=SAMPLE_TILES),
+            in_=x.rearrange("(s b) i d -> b s (i d)", s=SAMPLE_TILES),
+        )
+        x1_sb = [keep.tile([P, FK * D], BF16, name="x1_sb%d" % s) for s in range(SAMPLE_TILES)]
+        nc.sync.dma_start(out=x1_sb[0][:], in_=x1[0:P].rearrange("b j d -> b (j d)"))
+        w1_raw = keep.tile([P, PASSES * PACK * S1], BF16, name="w1_raw")
+        nc.sync.dma_start(
+            out=w1_raw.rearrange("p (g n) -> p g n", n=S1),
+            in_=w1.rearrange("(g p) n -> p g n", p=P),
+        )
+        b1_rows = keep.tile([P, S1], BF16, name="b1_rows")
+        nc.sync.dma_start(out=b1_rows[:], in_=b1.partition_broadcast(P))
+        w2_raw = {}
+        for c in range(PASSES):
+            for h in range(HALVES):
+                w2_raw[c, h] = raw_pool.tile([P, PACK * N2], BF16, name="w2_raw")
+                nc.sync.dma_start(
+                    out=w2_raw[c, h].rearrange("p (t n) -> p t n", t=PACK),
+                    in_=w2[c * PACK * P : (c + 1) * PACK * P, h * N2 : (h + 1) * N2].rearrange(
+                        "(t p) n -> p t n", p=P
+                    ),
+                )
+        nc.sync.dma_start(out=x1_sb[1][:], in_=x1[P : 2 * P].rearrange("b j d -> b (j d)"))
+        b2_rows = keep.tile([P, S2], BF16, name="b2_rows")
+        nc.sync.dma_start(out=b2_rows[:], in_=b2.partition_broadcast(P))
+
+        ident_f = keep.tile([P, P], F32, name="ident_f")
+        make_identity(nc, ident_f[:])
+        ident_b = keep.tile([P, P], BF16, name="ident_b")
+        make_identity(nc, ident_b[:])
+
+        x_fields = keep.tile([P, SAMPLE_TILES * F0 * D], BF16, name="x_fields")
+        for s in range(SAMPLE_TILES):
+            nc.vector.tensor_copy(
+                out=x_fields.rearrange("p (s d c t) -> p s d c t", s=SAMPLE_TILES, d=D, c=PASSES)[:, s],
+                in_=x_sb.rearrange("p (s c t d) -> p s d c t", s=SAMPLE_TILES, d=D, c=PASSES)[:, s],
+            )
+        x_words = x_fields[:].bitcast(F32)
+
+        x_all = {}
+        x1_twice = {}
+        z_in = {}
+        z_codes = {}
+        z_scales = {}
+        o1 = {}
+        sums = {}
+
+        def spread_inputs(r):
+            s, d0 = r // ROUNDS_PER_TILE, (r % ROUNDS_PER_TILE) * D_ROUND
+            x_all[r] = three.tile([P, PASSES * ROWS * 2], F32, name="x_all")
+            for dl in range(D_ROUND):
+                x_bank = spread.tile([P, PACK * P], F32, name="x_bank")
+                for cu in range(PACK):
+                    word = (s * D + d0 + dl) * PACK + cu
+                    nc.tensor.transpose(
+                        x_bank[:, cu * P : (cu + 1) * P],
+                        x_words[:, word : word + 1].to_broadcast([P, P]),
+                        ident_f[:],
+                    )
+                nc.scalar.copy(
+                    out=x_all[r].rearrange("p (c w u) -> p c w u", c=PASSES, u=2)[
+                        :, :, dl * P : (dl + 1) * P, :
+                    ],
+                    in_=x_bank.rearrange("p (c u b) -> p c b u", c=PASSES, u=2),
+                )
+            x1_t = bank.tile([P, ROWS], BF16, name="x1_t")
+            for dl in range(D_ROUND):
+                nc.tensor.transpose(
+                    x1_t[:, dl * P : (dl + 1) * P],
+                    x1_sb[s].rearrange("p (j d) -> p j d", d=D)[:, :, d0 + dl],
+                    ident_b[:],
+                )
+            x1_twice[r] = three.tile([P, ROWS * 2], BF16, name="x1_twice")
+            nc.scalar.copy(
+                out=x1_twice[r].rearrange("p (w e) -> p w e", e=2),
+                in_=x1_t[:].unsqueeze(2).to_broadcast([P, ROWS, 2]),
+            )
+
+        def x_of_pass(r, c):
+            return x_all[r][:].bitcast(BF16)[:, c * ROWS * PACK : (c + 1) * ROWS * PACK]
+
+        def z_of_pass(layer, r, c):
+            return z_in[layer, r][:, c * ROWS * PACK : (c + 1) * ROWS * PACK]
+
+        def new_z(layer, r):
+            z_in[layer, r] = two.tile(
+                [P, PASSES * ROWS * PACK], BF16, name="z%d_in" % layer, align_bytes=64
+            )
+            z_codes[layer, r] = three.tile(
+                [P, PASSES * ROWS], U32, name="z%d_codes" % layer, align_bytes=64
+            )
+            z_scales[layer, r] = three.tile(
+                [P, PASSES * ROWS], U8, name="z%d_scales" % layer, align_bytes=64
+            )
+
+        def multiply1(r, c):
+            nc.vector.tensor_tensor(
+                out=z_of_pass(1, r, c).rearrange("p (w u e) -> p w u e", u=2, e=2),
+                in0=x1_twice[r]
+                .rearrange("p (w e) -> p w e", e=2)
+                .unsqueeze(2)
+                .to_broadcast([P, ROWS, 2, 2]),
+                in1=x_of_pass(r, c).rearrange("p (w u e) -> p w u e", u=2, e=2),
+                op=MULT,
+            )
+
+        def multiply2(r, c):
+            nc.vector.scalar_tensor_tensor(
+                out=z_of_pass(2, r, c).rearrange("p (w t) -> p w t", t=PACK),
+                in0=o1[r][:].unsqueeze(2).to_broadcast([P, ROWS, PACK]),
+                scalar=b1_col[:, 0:1],
+                in1=x_of_pass(r, c).rearrange("p (w t) -> p w t", t=PACK),
+                op0=ADD,
+                op1=MULT,
+            )
+
+        def quantise(layer, r, first_pass, passes):
+            cols = slice(first_pass * ROWS, (first_pass + passes) * ROWS)
+            nc.vector.quantize_mx(
+                out=z_codes[layer, r][:, cols].bitcast(FP8X4),
+                scales=z_scales[layer, r][:, cols],
+                in_=z_in[layer, r][:, first_pass * ROWS * PACK : (first_pass + passes) * ROWS * PACK],
+            )
+
+        def layer1(r):
+            o1[r] = bank.tile([P, ROWS], F32, name="o1")
+            for c in range(PASSES):
+                nc.tensor.matmul_mx(
+                    out=o1[r][:],
+                    lhsT=w1_codes[:, c * S1 : (c + 1) * S1].bitcast(FP8X4),
+                    lhsT_scale=w1_scales[:, c * S1 : (c + 1) * S1],
+                    rhs=z_codes[1, r][:, c * ROWS : (c + 1) * ROWS].bitcast(FP8X4),
+                    rhs_scale=z_scales[1, r][:, c * ROWS : (c + 1) * ROWS],
+                    start=(c == 0),
+                    stop=(c == PASSES - 1),
+                )
+
+        def pooled(r, c):
+            s = r // ROUNDS_PER_TILE
+            if r % ROUNDS_PER_TILE == 0 and c == 0:
+                sums[s] = [bank.tile([P, N2], F32, name="sum_o2_%d" % h) for h in range(HALVES)]
+                sums[s].append(bank.tile([P, S1], F32, name="sum_o1"))
+            first = r % ROUNDS_PER_TILE == 0 and c == 0
+            last = r % ROUNDS_PER_TILE == ROUNDS_PER_TILE - 1 and c == PASSES - 1
+            for h in range(HALVES + 1):
+                layer = 2 if h < HALVES else 1
+                for dl in range(D_ROUND):
+                    block = slice(c * ROWS + dl * P, c * ROWS + (dl + 1) * P)
+                    if layer == 2:
+                        w_cols = slice(c * S2 + h * N2, c * S2 + (h + 1) * N2)
+                        w_codes, w_scales = w2_codes, w2_scales
+                    else:
+                        w_cols = slice(c * S1, (c + 1) * S1)
+                        w_codes, w_scales = w1_codes, w1_scales
+                    nc.tensor.matmul_mx(
+                        out=sums[s][h][:],
+                        lhsT=z_codes[layer, r][:, block].bitcast(FP8X4),
+                        lhsT_scale=z_scales[layer, r][:, block],
+                        rhs=w_codes[:, w_cols].bitcast(FP8X4),
+                        rhs_scale=w_scales[:, w_cols],
+                        start=(first and dl == 0),
+                        stop=(last and dl == D_ROUND - 1),
+                    )
+
+        def finish(s):
+            result = two.tile([P, S1 + S2], F32, name="result")
+            pieces = [(S1 + h * N2, N2, b2_rows[:, h * N2 : (h + 1) * N2]) for h in range(HALVES)]
+            pieces.append((0, S1, b1_rows[:]))
+            for h, (col, width, bias) in enumerate(pieces):
+                nc.vector.scalar_tensor_tensor(
+                    out=result[:, col : col + width],
+                    in0=bias,
+                    scalar=float(D),
+                    in1=sums[s][h][:],
+                    op0=MULT,
+                    op1=ADD,
+                )
+                nc.sync.dma_start(
+                    out=out[s * P : (s + 1) * P, col : col + width], in_=result[:, col : col + width]
+                )
+
+        def regroup(dst, src):
+            nc.vector.tensor_copy(
+                out=dst.rearrange("p (g i t) -> p g t i", i=4, t=PACK),
+                in_=src.rearrange("p (t g i) -> p g t i", i=4, t=PACK),
+            )
+
+        def quantise_weights(codes, scales, grouped):
+            nc.vector.quantize_mx(out=codes.bitcast(FP8X4), scales=scales, in_=grouped)
+
+        spread_inputs(0)
+        spread_inputs(1)
+
+        b1_t = bank.tile([P, ROWS], BF16, name="b1_t", tag="x1_t")
+        nc.tensor.transpose(b1_t[:, 0:P], b1_rows[:], ident_b[:])
+        b1_col = keep.tile([P, 1], F32, name="b1_col")
+        nc.scalar.copy(out=b1_col[:], in_=b1_t[:, 0:1])
+
+        w1_grouped = keep.tile([P, PASSES * S1 * PACK], BF16, name="w1_grouped", align_bytes=64)
+        w1_codes = keep.tile([P, PASSES * S1], U32, name="w1_codes", align_bytes=64)
+        w1_scales = keep.tile([P, PASSES * S1], U8, name="w1_scales", align_bytes=64)
+        w2_codes = keep.tile([P, PASSES * S2], U32, name="w2_codes", align_bytes=64)
+        w2_scales = keep.tile([P, PASSES * S2], U8, name="w2_scales", align_bytes=64)
+        for c in range(PASSES):
+            part = slice(c * S1 * PACK, (c + 1) * S1 * PACK)
+            regroup(w1_grouped[:, part], w1_raw[:, part])
+        jobs = [(w1_codes[:], w1_scales[:], w1_grouped[:])]
+        for c in range(PASSES):
+            for h in range(HALVES):
+                w2_grouped = two.tile([P, N2 * PACK], BF16, name="w2_grouped", align_bytes=64)
+                regroup(w2_grouped[:], w2_raw[c, h][:])
+                cols = slice(c * S2 + h * N2, c * S2 + (h + 1) * N2)
+                jobs.append((w2_codes[:, cols], w2_scales[:, cols], w2_grouped[:]))
+                quantise_weights(*jobs[-2])
+        quantise_weights(*jobs[-1])
+
+        new_z(1, 0)
+        for c in range(PASSES):
+            multiply1(0, c)
+        quantise(1, 0, 0, PASSES)
+        layer1(0)
+
+        for r in range(ROUNDS):
+            ahead = r + 1 < ROUNDS
+            if r + 2 < ROUNDS:
+                spread_inputs(r + 2)
+            new_z(2, r)
+            if ahead:
+                new_z(1, r + 1)
+                multiply1(r + 1, 0)
+            multiply2(r, 0)
+            if ahead:
+                multiply1(r + 1, 1)
+            if r > 0 and r % ROUNDS_PER_TILE == 0:
+                finish(r // ROUNDS_PER_TILE - 1)
+            quantise(2, r, 0, 1)
+            pooled(r, 0)
+            multiply2(r, 1)
+            if ahead:
+                quantise(1, r + 1, 0, PASSES)
+                layer1(r + 1)
+            quantise(2, r, 1, 1)
+            pooled(r, 1)
+        finish(SAMPLE_TILES - 1)

@@ -86,6 +86,11 @@ def tile_cin_pa_t_kernel(tc, x, x1, w1, b1, w2, b2, out):
 
         def spread_inputs(r):
             s, d0 = r // ROUNDS_PER_TILE, (r % ROUNDS_PER_TILE) * D_ROUND
+            x1_by_d = two.tile([P, ROWS], BF16, name="x1_by_d")
+            nc.scalar.copy(
+                out=x1_by_d.rearrange("p (d j) -> p j d", d=D_ROUND),
+                in_=x1_sb[s].rearrange("p (j d) -> p j d", d=D)[:, :, d0 : d0 + D_ROUND],
+            )
             x_all[r] = three.tile([P, PASSES * ROWS * 2], F32, name="x_all")
             for dl in range(D_ROUND):
                 x_bank = spread.tile([P, PACK * P], F32, name="x_bank")
@@ -105,9 +110,7 @@ def tile_cin_pa_t_kernel(tc, x, x1, w1, b1, w2, b2, out):
             x1_t = bank.tile([P, ROWS], BF16, name="x1_t")
             for dl in range(D_ROUND):
                 nc.tensor.transpose(
-                    x1_t[:, dl * P : (dl + 1) * P],
-                    x1_sb[s].rearrange("p (j d) -> p j d", d=D)[:, :, d0 + dl],
-                    ident_b[:],
+                    x1_t[:, dl * P : (dl + 1) * P], x1_by_d[:, dl * P : (dl + 1) * P], ident_b[:]
                 )
             x1_twice[r] = three.tile([P, ROWS * 2], BF16, name="x1_twice")
             nc.scalar.copy(
@@ -218,14 +221,18 @@ def tile_cin_pa_t_kernel(tc, x, x1, w1, b1, w2, b2, out):
                     out=out[s * P : (s + 1) * P, col : col + width], in_=result[:, col : col + width]
                 )
 
-        def regroup(dst, src):
-            nc.vector.tensor_copy(
+        def regroup(copy, dst, src):
+            copy(
                 out=dst.rearrange("p (g i t) -> p g t i", i=4, t=PACK),
                 in_=src.rearrange("p (t g i) -> p g t i", i=4, t=PACK),
             )
 
         def quantise_weights(codes, scales, grouped):
             nc.vector.quantize_mx(out=codes.bitcast(FP8X4), scales=scales, in_=grouped)
+
+        def quantise_w2(c):
+            for h in range(HALVES):
+                quantise_weights(*w2_jobs[c, h])
 
         spread_inputs(0)
         spread_inputs(1)
@@ -242,16 +249,15 @@ def tile_cin_pa_t_kernel(tc, x, x1, w1, b1, w2, b2, out):
         w2_scales = keep.tile([P, PASSES * S2], U8, name="w2_scales", align_bytes=64)
         for c in range(PASSES):
             part = slice(c * S1 * PACK, (c + 1) * S1 * PACK)
-            regroup(w1_grouped[:, part], w1_raw[:, part])
-        jobs = [(w1_codes[:], w1_scales[:], w1_grouped[:])]
+            regroup(nc.vector.tensor_copy, w1_grouped[:, part], w1_raw[:, part])
+        w2_jobs = {}
         for c in range(PASSES):
             for h in range(HALVES):
-                w2_grouped = two.tile([P, N2 * PACK], BF16, name="w2_grouped", align_bytes=64)
-                regroup(w2_grouped[:], w2_raw[c, h][:])
+                w2_grouped = raw_pool.tile([P, N2 * PACK], BF16, name="w2_grouped", align_bytes=64)
+                regroup(nc.vector.tensor_copy if c == 0 else nc.scalar.copy, w2_grouped[:], w2_raw[c, h][:])
                 cols = slice(c * S2 + h * N2, c * S2 + (h + 1) * N2)
-                jobs.append((w2_codes[:, cols], w2_scales[:, cols], w2_grouped[:]))
-                quantise_weights(*jobs[-2])
-        quantise_weights(*jobs[-1])
+                w2_jobs[c, h] = (w2_codes[:, cols], w2_scales[:, cols], w2_grouped[:])
+        quantise_weights(w1_codes[:], w1_scales[:], w1_grouped[:])
 
         new_z(1, 0)
         for c in range(PASSES):
@@ -272,12 +278,16 @@ def tile_cin_pa_t_kernel(tc, x, x1, w1, b1, w2, b2, out):
                 multiply1(r + 1, 1)
             if r > 0 and r % ROUNDS_PER_TILE == 0:
                 finish(r // ROUNDS_PER_TILE - 1)
+            if r == 0:
+                quantise_w2(0)
             quantise(2, r, 0, 1)
             pooled(r, 0)
             multiply2(r, 1)
             if ahead:
                 quantise(1, r + 1, 0, PASSES)
                 layer1(r + 1)
+            if r == 0:
+                quantise_w2(1)
             quantise(2, r, 1, 1)
             pooled(r, 1)
         finish(SAMPLE_TILES - 1)

@@ -6,6 +6,7 @@ F32 = mybir.dt.float32
 U32 = mybir.dt.uint32
 U8 = mybir.dt.uint8
 FP8X4 = mybir.dt.float8_e4m3fn_x4
+IDENTITY = mybir.ActivationFunctionType.Identity
 MULT = mybir.AluOpType.mult
 ADD = mybir.AluOpType.add
 
@@ -18,6 +19,8 @@ D_ROUND = 4
 ROUNDS_PER_TILE = D // D_ROUND
 ROUNDS = SAMPLE_TILES * ROUNDS_PER_TILE
 ROWS = D_ROUND * P
+GP_ROWS = P
+DVE_ROWS = ROWS - GP_ROWS
 N2 = 512
 HALVES = S2 // N2
 
@@ -82,6 +85,7 @@ def tile_cin_pa_t_kernel(tc, x, x1, w1, b1, w2, b2, out):
         z_codes = {}
         z_scales = {}
         o1 = {}
+        o1_gp = {}
         sums = {}
 
         def spread_inputs(r):
@@ -147,13 +151,20 @@ def tile_cin_pa_t_kernel(tc, x, x1, w1, b1, w2, b2, out):
             )
 
         def multiply2(r, c):
+            cut = DVE_ROWS * PACK
             nc.vector.scalar_tensor_tensor(
-                out=z_of_pass(2, r, c).rearrange("p (w t) -> p w t", t=PACK),
-                in0=o1[r][:].unsqueeze(2).to_broadcast([P, ROWS, PACK]),
+                out=z_of_pass(2, r, c)[:, 0:cut].rearrange("p (w t) -> p w t", t=PACK),
+                in0=o1[r][:, 0:DVE_ROWS].unsqueeze(2).to_broadcast([P, DVE_ROWS, PACK]),
                 scalar=b1_col[:, 0:1],
-                in1=x_of_pass(r, c).rearrange("p (w t) -> p w t", t=PACK),
+                in1=x_of_pass(r, c)[:, 0:cut].rearrange("p (w t) -> p w t", t=PACK),
                 op0=ADD,
                 op1=MULT,
+            )
+            nc.gpsimd.tensor_tensor(
+                out=z_of_pass(2, r, c)[:, cut:].rearrange("p (w t) -> p w t", t=PACK),
+                in0=o1_gp[r][:].unsqueeze(2).to_broadcast([P, GP_ROWS, PACK]),
+                in1=x_of_pass(r, c)[:, cut:].rearrange("p (w t) -> p w t", t=PACK),
+                op=MULT,
             )
 
         def quantise(layer, r, first_pass, passes):
@@ -166,16 +177,24 @@ def tile_cin_pa_t_kernel(tc, x, x1, w1, b1, w2, b2, out):
 
         def layer1(r):
             o1[r] = bank.tile([P, ROWS], F32, name="o1")
-            for c in range(PASSES):
-                nc.tensor.matmul_mx(
-                    out=o1[r][:],
-                    lhsT=w1_codes[:, c * S1 : (c + 1) * S1].bitcast(FP8X4),
-                    lhsT_scale=w1_scales[:, c * S1 : (c + 1) * S1],
-                    rhs=z_codes[1, r][:, c * ROWS : (c + 1) * ROWS].bitcast(FP8X4),
-                    rhs_scale=z_scales[1, r][:, c * ROWS : (c + 1) * ROWS],
-                    start=(c == 0),
-                    stop=(c == PASSES - 1),
-                )
+            o1_apart = spread.tile([P, PACK * P], F32, name="o1_apart", tag="x_bank")
+            groups = [(o1[r], 0, 2 * P), (o1[r], 2 * P, P), (o1_apart, DVE_ROWS, GP_ROWS)]
+            for target, row0, rows in groups:
+                col0 = row0 % DVE_ROWS
+                for c in range(PASSES):
+                    nc.tensor.matmul_mx(
+                        out=target[:, col0 : col0 + rows],
+                        lhsT=w1_codes[:, c * S1 : (c + 1) * S1].bitcast(FP8X4),
+                        lhsT_scale=w1_scales[:, c * S1 : (c + 1) * S1],
+                        rhs=z_codes[1, r][:, c * ROWS + row0 : c * ROWS + row0 + rows].bitcast(FP8X4),
+                        rhs_scale=z_scales[1, r][:, c * ROWS + row0 : c * ROWS + row0 + rows],
+                        start=(c == 0),
+                        stop=(c == PASSES - 1),
+                    )
+            o1_gp[r] = two.tile([P, GP_ROWS], F32, name="o1_gp")
+            nc.scalar.activation(
+                out=o1_gp[r][:], in_=o1_apart[:, 0:GP_ROWS], func=IDENTITY, bias=b1_col[:, 0:1]
+            )
 
         def pooled(r, c):
             s = r // ROUNDS_PER_TILE
@@ -272,22 +291,18 @@ def tile_cin_pa_t_kernel(tc, x, x1, w1, b1, w2, b2, out):
             new_z(2, r)
             if ahead:
                 new_z(1, r + 1)
-                multiply1(r + 1, 0)
-            multiply2(r, 0)
-            if ahead:
-                multiply1(r + 1, 1)
+                for c in range(PASSES):
+                    multiply1(r + 1, c)
+            for c in range(PASSES):
+                multiply2(r, c)
             if r > 0 and r % ROUNDS_PER_TILE == 0:
                 finish(r // ROUNDS_PER_TILE - 1)
-            if r == 0:
-                quantise_w2(0)
-            quantise(2, r, 0, 1)
-            pooled(r, 0)
-            multiply2(r, 1)
             if ahead:
                 quantise(1, r + 1, 0, PASSES)
                 layer1(r + 1)
-            if r == 0:
-                quantise_w2(1)
-            quantise(2, r, 1, 1)
-            pooled(r, 1)
+            for c in range(PASSES):
+                if r == 0:
+                    quantise_w2(c)
+                quantise(2, r, c, 1)
+                pooled(r, c)
         finish(SAMPLE_TILES - 1)

@@ -23,6 +23,8 @@ GP_ROWS = P
 DVE_ROWS = ROWS - GP_ROWS
 N2 = 512
 HALVES = S2 // N2
+HALF_P = P // 2
+PE_SPREAD_ROUNDS = 2
 
 FLOPS = 2 * B * D * (F0 * FK * S1 + F0 * S1 * S2)
 
@@ -53,7 +55,8 @@ def tile_cin_pa_t_kernel(tc, x, x1, w1, b1, w2, b2, out):
         b1_rows = keep.tile([P, S1], BF16, name="b1_rows")
         nc.sync.dma_start(out=b1_rows[:], in_=b1.partition_broadcast(P))
         w2_raw = {}
-        for c in range(PASSES):
+
+        def load_w2(c):
             for h in range(HALVES):
                 w2_raw[c, h] = raw_pool.tile([P, PACK * N2], BF16, name="w2_raw")
                 nc.sync.dma_start(
@@ -62,9 +65,8 @@ def tile_cin_pa_t_kernel(tc, x, x1, w1, b1, w2, b2, out):
                         "(t p) n -> p t n", p=P
                     ),
                 )
-        nc.sync.dma_start(out=x1_sb[1][:], in_=x1[P : 2 * P].rearrange("b j d -> b (j d)"))
-        b2_rows = keep.tile([P, S2], BF16, name="b2_rows")
-        nc.sync.dma_start(out=b2_rows[:], in_=b2.partition_broadcast(P))
+
+        load_w2(0)
 
         ident_f = keep.tile([P, P], F32, name="ident_f")
         make_identity(nc, ident_f[:])
@@ -79,7 +81,44 @@ def tile_cin_pa_t_kernel(tc, x, x1, w1, b1, w2, b2, out):
             )
         x_words = x_fields[:].bitcast(F32)
 
-        x_all = {}
+        x_all = [keep.tile([P, PASSES * ROWS * 2], F32, name="x_all%d" % r) for r in range(ROUNDS)]
+        x_blocks = keep.tile([P, 3 * HALF_P], F32, name="x_blocks")
+        for block, u in enumerate((0, 1, 0)):
+            nc.vector.tensor_copy(
+                out=x_blocks[:, block * HALF_P : (block + 1) * HALF_P].rearrange(
+                    "p (a c dl) -> p a c dl", c=PASSES, dl=D_ROUND
+                ),
+                in_=x_words.rearrange("p (a dl c u) -> p u a c dl", dl=D_ROUND, c=PASSES, u=2)[:, u],
+            )
+        x_turned_ps = spread.tile([P, PACK * P], F32, name="x_turned_ps", tag="x_bank")
+        for u in range(2):
+            nc.tensor.transpose(
+                x_turned_ps[:, u * P : (u + 1) * P], x_blocks[:, u * HALF_P : u * HALF_P + P], ident_f[:]
+            )
+        x_turned = keep.tile([P, 2 * P], F32, name="x_turned")
+        nc.vector.tensor_copy(
+            out=x_turned.rearrange("p (b u) -> p b u", u=2),
+            in_=x_turned_ps[:, 0 : 2 * P].rearrange("p (u b) -> p b u", u=2),
+        )
+        round_words = PASSES * ROWS * 2
+        parked = out.rearrange("a n -> (a n)")[0 : ROUNDS * round_words]
+        nc.sync.dma_start(out=parked.rearrange("(p w) -> p w", w=2 * P), in_=x_turned[0:HALF_P, :])
+
+        def load_x_all(r):
+            nc.sync.dma_start(
+                out=x_all[r][:],
+                in_=parked[r * round_words : (r + 1) * round_words].partition_broadcast(P),
+            )
+
+        load_w2(1)
+        load_x_all(2)
+        nc.sync.dma_start(out=x1_sb[1][:], in_=x1[P : 2 * P].rearrange("b j d -> b (j d)"))
+        load_x_all(3)
+        b2_rows = keep.tile([P, S2], BF16, name="b2_rows")
+        nc.sync.dma_start(out=b2_rows[:], in_=b2.partition_broadcast(P))
+        for r in range(4, ROUNDS):
+            load_x_all(r)
+
         x1_twice = {}
         z_in = {}
         z_codes = {}
@@ -95,8 +134,7 @@ def tile_cin_pa_t_kernel(tc, x, x1, w1, b1, w2, b2, out):
                 out=x1_by_d.rearrange("p (d j) -> p j d", d=D_ROUND),
                 in_=x1_sb[s].rearrange("p (j d) -> p j d", d=D)[:, :, d0 : d0 + D_ROUND],
             )
-            x_all[r] = three.tile([P, PASSES * ROWS * 2], F32, name="x_all")
-            for dl in range(D_ROUND):
+            for dl in range(D_ROUND if r < PE_SPREAD_ROUNDS else 0):
                 x_bank = spread.tile([P, PACK * P], F32, name="x_bank")
                 for cu in range(PACK):
                     word = (s * D + d0 + dl) * PACK + cu

@@ -7,6 +7,7 @@ U32 = mybir.dt.uint32
 U8 = mybir.dt.uint8
 FP8X4 = mybir.dt.float8_e4m3fn_x4
 IDENTITY = mybir.ActivationFunctionType.Identity
+COPY = mybir.ActivationFunctionType.Copy
 MULT = mybir.AluOpType.mult
 ADD = mybir.AluOpType.add
 
@@ -19,8 +20,10 @@ D_ROUND = 4
 ROUNDS_PER_TILE = D // D_ROUND
 ROUNDS = SAMPLE_TILES * ROUNDS_PER_TILE
 ROWS = D_ROUND * P
-GP_ROWS = P
-DVE_ROWS = ROWS - GP_ROWS
+DVE_ROWS = 2 * P
+ACT_D = 2
+GP_D = 3
+ROUTED_ROUNDS = ROUNDS - 1
 N2 = 512
 HALVES = S2 // N2
 HALF_P = P // 2
@@ -119,25 +122,28 @@ def tile_cin_pa_t_kernel(tc, x, x1, w1, b1, w2, b2, out):
         for r in range(4, ROUNDS):
             load_x_all(r)
 
+        x_f32 = keep.tile([P, SAMPLE_TILES * F0 * D], F32, name="x_f32")
+        nc.gpsimd.tensor_copy(out=x_f32[:], in_=x_sb[:])
+
+        x1_by_d = {}
+        x1_t = {}
         x1_twice = {}
         z_in = {}
         z_codes = {}
         z_scales = {}
         o1 = {}
         o1_gp = {}
+        o1_turned_ps = {}
+        o1_turned = {}
+        z2_turned = {}
+        z2_back = {}
         sums = {}
 
-        def spread_inputs(r):
-            s, d0 = r // ROUNDS_PER_TILE, (r % ROUNDS_PER_TILE) * D_ROUND
-            x1_by_d = two.tile([P, ROWS], BF16, name="x1_by_d")
-            nc.scalar.copy(
-                out=x1_by_d.rearrange("p (d j) -> p j d", d=D_ROUND),
-                in_=x1_sb[s].rearrange("p (j d) -> p j d", d=D)[:, :, d0 : d0 + D_ROUND],
-            )
-            for dl in range(D_ROUND if r < PE_SPREAD_ROUNDS else 0):
+        def spread_x(r):
+            for dl in range(D_ROUND):
                 x_bank = spread.tile([P, PACK * P], F32, name="x_bank")
                 for cu in range(PACK):
-                    word = (s * D + d0 + dl) * PACK + cu
+                    word = (r * D_ROUND + dl) * PACK + cu
                     nc.tensor.transpose(
                         x_bank[:, cu * P : (cu + 1) * P],
                         x_words[:, word : word + 1].to_broadcast([P, P]),
@@ -149,22 +155,32 @@ def tile_cin_pa_t_kernel(tc, x, x1, w1, b1, w2, b2, out):
                     ],
                     in_=x_bank.rearrange("p (c u b) -> p c b u", c=PASSES, u=2),
                 )
-            x1_t = bank.tile([P, ROWS], BF16, name="x1_t")
+
+        def sort_x1(r):
+            s, d0 = r // ROUNDS_PER_TILE, (r % ROUNDS_PER_TILE) * D_ROUND
+            x1_by_d[r] = two.tile([P, ROWS], BF16, name="x1_by_d")
+            nc.scalar.copy(
+                out=x1_by_d[r].rearrange("p (d j) -> p d j", d=D_ROUND),
+                in_=x1_sb[s].rearrange("p (j d) -> p d j", d=D)[:, d0 : d0 + D_ROUND, :],
+            )
+
+        def turn_x1(r):
+            x1_t[r] = bank.tile([P, ROWS], BF16, name="x1_t")
             for dl in range(D_ROUND):
                 nc.tensor.transpose(
-                    x1_t[:, dl * P : (dl + 1) * P], x1_by_d[:, dl * P : (dl + 1) * P], ident_b[:]
+                    x1_t[r][:, dl * P : (dl + 1) * P], x1_by_d[r][:, dl * P : (dl + 1) * P], ident_b[:]
                 )
+
+        def double_x1(r):
             x1_twice[r] = three.tile([P, ROWS * 2], BF16, name="x1_twice")
             nc.scalar.copy(
                 out=x1_twice[r].rearrange("p (w e) -> p w e", e=2),
-                in_=x1_t[:].unsqueeze(2).to_broadcast([P, ROWS, 2]),
+                in_=x1_t[r][:].unsqueeze(2).to_broadcast([P, ROWS, 2]),
             )
 
-        def x_of_pass(r, c):
-            return x_all[r][:].bitcast(BF16)[:, c * ROWS * PACK : (c + 1) * ROWS * PACK]
-
-        def z_of_pass(layer, r, c):
-            return z_in[layer, r][:, c * ROWS * PACK : (c + 1) * ROWS * PACK]
+        def x_of_pass(r, c, row0, rows):
+            first = (c * ROWS + row0) * PACK
+            return x_all[r][:].bitcast(BF16)[:, first : first + rows * PACK].rearrange("p (w t) -> p w t", t=PACK)
 
         def new_z(layer, r):
             z_in[layer, r] = two.tile(
@@ -177,48 +193,65 @@ def tile_cin_pa_t_kernel(tc, x, x1, w1, b1, w2, b2, out):
                 [P, PASSES * ROWS], U8, name="z%d_scales" % layer, align_bytes=64
             )
 
+        def word_col(layer, c, dl):
+            if layer == 1:
+                return (c * D_ROUND + dl) * P
+            if dl * P < DVE_ROWS:
+                return c * DVE_ROWS + dl * P
+            return (dl * PASSES + c) * P
+
+        def z2_of(r, c, dl, rows):
+            first = word_col(2, c, dl) * PACK
+            return z_in[2, r][:, first : first + rows * PACK]
+
         def multiply1(r, c):
             nc.vector.tensor_tensor(
-                out=z_of_pass(1, r, c).rearrange("p (w u e) -> p w u e", u=2, e=2),
+                out=z_in[1, r][:, c * ROWS * PACK : (c + 1) * ROWS * PACK].rearrange(
+                    "p (w u e) -> p w u e", u=2, e=2
+                ),
                 in0=x1_twice[r]
                 .rearrange("p (w e) -> p w e", e=2)
                 .unsqueeze(2)
                 .to_broadcast([P, ROWS, 2, 2]),
-                in1=x_of_pass(r, c).rearrange("p (w u e) -> p w u e", u=2, e=2),
+                in1=x_of_pass(r, c, 0, ROWS).rearrange("p w (u e) -> p w u e", e=2),
                 op=MULT,
             )
 
-        def multiply2(r, c):
-            cut = DVE_ROWS * PACK
+        def multiply2_vector(r, c, dl, rows):
             nc.vector.scalar_tensor_tensor(
-                out=z_of_pass(2, r, c)[:, 0:cut].rearrange("p (w t) -> p w t", t=PACK),
-                in0=o1[r][:, 0:DVE_ROWS].unsqueeze(2).to_broadcast([P, DVE_ROWS, PACK]),
+                out=z2_of(r, c, dl, rows).rearrange("p (w t) -> p w t", t=PACK),
+                in0=o1[r][:, dl * P : dl * P + rows].unsqueeze(2).to_broadcast([P, rows, PACK]),
                 scalar=b1_col[:, 0:1],
-                in1=x_of_pass(r, c)[:, 0:cut].rearrange("p (w t) -> p w t", t=PACK),
+                in1=x_of_pass(r, c, dl * P, rows),
                 op0=ADD,
                 op1=MULT,
             )
+
+        def multiply2(r, c):
+            multiply2_vector(r, c, 0, DVE_ROWS)
+            if r >= ROUTED_ROUNDS:
+                multiply2_vector(r, c, ACT_D, P)
             nc.gpsimd.tensor_tensor(
-                out=z_of_pass(2, r, c)[:, cut:].rearrange("p (w t) -> p w t", t=PACK),
-                in0=o1_gp[r][:].unsqueeze(2).to_broadcast([P, GP_ROWS, PACK]),
-                in1=x_of_pass(r, c)[:, cut:].rearrange("p (w t) -> p w t", t=PACK),
+                out=z2_of(r, c, GP_D, P).rearrange("p (w t) -> p w t", t=PACK),
+                in0=o1_gp[r][:].unsqueeze(2).to_broadcast([P, P, PACK]),
+                in1=x_of_pass(r, c, GP_D * P, P),
                 op=MULT,
             )
 
-        def quantise(layer, r, first_pass, passes):
-            cols = slice(first_pass * ROWS, (first_pass + passes) * ROWS)
+        def quantise(layer, r, word0, words):
             nc.vector.quantize_mx(
-                out=z_codes[layer, r][:, cols].bitcast(FP8X4),
-                scales=z_scales[layer, r][:, cols],
-                in_=z_in[layer, r][:, first_pass * ROWS * PACK : (first_pass + passes) * ROWS * PACK],
+                out=z_codes[layer, r][:, word0 : word0 + words].bitcast(FP8X4),
+                scales=z_scales[layer, r][:, word0 : word0 + words],
+                in_=z_in[layer, r][:, word0 * PACK : (word0 + words) * PACK],
             )
 
         def layer1(r):
             o1[r] = bank.tile([P, ROWS], F32, name="o1")
             o1_apart = spread.tile([P, PACK * P], F32, name="o1_apart", tag="x_bank")
-            groups = [(o1[r], 0, 2 * P), (o1[r], 2 * P, P), (o1_apart, DVE_ROWS, GP_ROWS)]
-            for target, row0, rows in groups:
-                col0 = row0 % DVE_ROWS
+            groups = [(o1_apart, 0, GP_D * P, P), (o1[r], 0, 0, DVE_ROWS)]
+            if r >= ROUTED_ROUNDS:
+                groups.append((o1[r], ACT_D * P, ACT_D * P, P))
+            for target, col0, row0, rows in groups:
                 for c in range(PASSES):
                     nc.tensor.matmul_mx(
                         out=target[:, col0 : col0 + rows],
@@ -229,36 +262,86 @@ def tile_cin_pa_t_kernel(tc, x, x1, w1, b1, w2, b2, out):
                         start=(c == 0),
                         stop=(c == PASSES - 1),
                     )
-            o1_gp[r] = two.tile([P, GP_ROWS], F32, name="o1_gp")
-            nc.scalar.activation(
-                out=o1_gp[r][:], in_=o1_apart[:, 0:GP_ROWS], func=IDENTITY, bias=b1_col[:, 0:1]
+            if r < ROUTED_ROUNDS:
+                o1_turned_ps[r] = spread.tile([P, PACK * P], F32, name="o1_turned_ps", tag="x_bank")
+                for c in range(PASSES):
+                    block = slice(word_col(1, c, ACT_D), word_col(1, c, ACT_D) + P)
+                    nc.tensor.matmul_mx(
+                        out=o1_turned_ps[r][:, 0:S1],
+                        lhsT=z_codes[1, r][:, block].bitcast(FP8X4),
+                        lhsT_scale=z_scales[1, r][:, block],
+                        rhs=w1_codes[:, c * S1 : (c + 1) * S1].bitcast(FP8X4),
+                        rhs_scale=w1_scales[:, c * S1 : (c + 1) * S1],
+                        start=(c == 0),
+                        stop=(c == PASSES - 1),
+                    )
+            o1_gp[r] = two.tile([P, P], F32, name="o1_gp")
+            nc.scalar.activation(out=o1_gp[r][:], in_=o1_apart[:, 0:P], func=IDENTITY, bias=b1_col[:, 0:1])
+
+        def add_b1_turned(r):
+            o1_turned[r] = two.tile([P, S1], F32, name="o1_turned")
+            nc.vector.tensor_tensor(out=o1_turned[r][:], in0=o1_turned_ps[r][:, 0:S1], in1=b1_rows[:], op=ADD)
+
+        def multiply2_scalar(r):
+            s, d = r // ROUNDS_PER_TILE, (r % ROUNDS_PER_TILE) * D_ROUND + ACT_D
+            z2_turned[r] = two.tile([P, F0 * S1], BF16, name="z2_turned")
+            for i in range(F0):
+                col = (s * F0 + i) * D + d
+                nc.scalar.activation(
+                    out=z2_turned[r].rearrange("p (g j e) -> p g e j", g=F0 // 2, e=2)[:, i // 2, i % 2],
+                    in_=o1_turned[r][:],
+                    func=COPY,
+                    scale=x_f32[:, col : col + 1],
+                )
+
+        def turn_z2(r):
+            z2_back[r] = spread.tile([P, PACK * P], F32, name="z2_back", tag="x_bank")
+            for g in range(F0 // 2):
+                nc.tensor.transpose(
+                    z2_back[r][:, g * P : (g + 1) * P],
+                    z2_turned[r][:].bitcast(F32)[:, g * P : (g + 1) * P],
+                    ident_f[:],
+                )
+
+        def collect_z2(r):
+            nc.scalar.copy(
+                out=z2_of(r, 0, ACT_D, PASSES * P).bitcast(F32).rearrange("p (c b u) -> p c b u", c=PASSES, u=2),
+                in_=z2_back[r].rearrange("p (c u b) -> p c b u", c=PASSES, u=2),
             )
 
-        def pooled(r, c):
-            s = r // ROUNDS_PER_TILE
-            if r % ROUNDS_PER_TILE == 0 and c == 0:
+        def pooled(r, positions):
+            s, q = r // ROUNDS_PER_TILE, r % ROUNDS_PER_TILE
+            if q == 0 and positions[0] == 0:
                 sums[s] = [bank.tile([P, N2], F32, name="sum_o2_%d" % h) for h in range(HALVES)]
                 sums[s].append(bank.tile([P, S1], F32, name="sum_o1"))
-            first = r % ROUNDS_PER_TILE == 0 and c == 0
-            last = r % ROUNDS_PER_TILE == ROUNDS_PER_TILE - 1 and c == PASSES - 1
-            for h in range(HALVES + 1):
-                layer = 2 if h < HALVES else 1
-                for dl in range(D_ROUND):
-                    block = slice(c * ROWS + dl * P, c * ROWS + (dl + 1) * P)
-                    if layer == 2:
+            for c in range(PASSES):
+                for h in range(HALVES):
+                    for dl in positions:
+                        block = slice(word_col(2, c, dl), word_col(2, c, dl) + P)
                         w_cols = slice(c * S2 + h * N2, c * S2 + (h + 1) * N2)
-                        w_codes, w_scales = w2_codes, w2_scales
-                    else:
-                        w_cols = slice(c * S1, (c + 1) * S1)
-                        w_codes, w_scales = w1_codes, w1_scales
+                        nc.tensor.matmul_mx(
+                            out=sums[s][h][:],
+                            lhsT=z_codes[2, r][:, block].bitcast(FP8X4),
+                            lhsT_scale=z_scales[2, r][:, block],
+                            rhs=w2_codes[:, w_cols].bitcast(FP8X4),
+                            rhs_scale=w2_scales[:, w_cols],
+                            start=(q == 0 and c == 0 and dl == 0),
+                            stop=(q == ROUNDS_PER_TILE - 1 and c == PASSES - 1 and dl == D_ROUND - 1),
+                        )
+
+        def pooled_o1(r):
+            s, q = r // ROUNDS_PER_TILE, r % ROUNDS_PER_TILE
+            for c in range(PASSES):
+                for dl in range(D_ROUND):
+                    block = slice(word_col(1, c, dl), word_col(1, c, dl) + P)
                     nc.tensor.matmul_mx(
-                        out=sums[s][h][:],
-                        lhsT=z_codes[layer, r][:, block].bitcast(FP8X4),
-                        lhsT_scale=z_scales[layer, r][:, block],
-                        rhs=w_codes[:, w_cols].bitcast(FP8X4),
-                        rhs_scale=w_scales[:, w_cols],
-                        start=(first and dl == 0),
-                        stop=(last and dl == D_ROUND - 1),
+                        out=sums[s][HALVES][:],
+                        lhsT=z_codes[1, r][:, block].bitcast(FP8X4),
+                        lhsT_scale=z_scales[1, r][:, block],
+                        rhs=w1_codes[:, c * S1 : (c + 1) * S1].bitcast(FP8X4),
+                        rhs_scale=w1_scales[:, c * S1 : (c + 1) * S1],
+                        start=(q == 0 and c == 0 and dl == 0),
+                        stop=(q == ROUNDS_PER_TILE - 1 and c == PASSES - 1 and dl == D_ROUND - 1),
                     )
 
         def finish(s):
@@ -287,12 +370,19 @@ def tile_cin_pa_t_kernel(tc, x, x1, w1, b1, w2, b2, out):
         def quantise_weights(codes, scales, grouped):
             nc.vector.quantize_mx(out=codes.bitcast(FP8X4), scales=scales, in_=grouped)
 
-        def quantise_w2(c):
-            for h in range(HALVES):
-                quantise_weights(*w2_jobs[c, h])
+        w2_jobs = {}
 
-        spread_inputs(0)
-        spread_inputs(1)
+        def regroup_w2(copy, c, h):
+            w2_grouped = raw_pool.tile([P, N2 * PACK], BF16, name="w2_grouped", align_bytes=64)
+            regroup(copy, w2_grouped[:], w2_raw[c, h][:])
+            cols = slice(c * S2 + h * N2, c * S2 + (h + 1) * N2)
+            w2_jobs[c, h] = (w2_codes[:, cols], w2_scales[:, cols], w2_grouped[:])
+
+        for r in range(PE_SPREAD_ROUNDS):
+            sort_x1(r)
+            spread_x(r)
+            turn_x1(r)
+            double_x1(r)
 
         b1_t = bank.tile([P, ROWS], BF16, name="b1_t", tag="x1_t")
         nc.tensor.transpose(b1_t[:, 0:P], b1_rows[:], ident_b[:])
@@ -307,40 +397,64 @@ def tile_cin_pa_t_kernel(tc, x, x1, w1, b1, w2, b2, out):
         for c in range(PASSES):
             part = slice(c * S1 * PACK, (c + 1) * S1 * PACK)
             regroup(nc.vector.tensor_copy, w1_grouped[:, part], w1_raw[:, part])
-        w2_jobs = {}
-        for c in range(PASSES):
-            for h in range(HALVES):
-                w2_grouped = raw_pool.tile([P, N2 * PACK], BF16, name="w2_grouped", align_bytes=64)
-                regroup(nc.vector.tensor_copy if c == 0 else nc.scalar.copy, w2_grouped[:], w2_raw[c, h][:])
-                cols = slice(c * S2 + h * N2, c * S2 + (h + 1) * N2)
-                w2_jobs[c, h] = (w2_codes[:, cols], w2_scales[:, cols], w2_grouped[:])
-        quantise_weights(w1_codes[:], w1_scales[:], w1_grouped[:])
-
         new_z(1, 0)
-        for c in range(PASSES):
-            multiply1(0, c)
-        quantise(1, 0, 0, PASSES)
+        multiply1(0, 0)
+        quantise_weights(w1_codes[:], w1_scales[:], w1_grouped[:])
+        multiply1(0, 1)
+        regroup_w2(nc.vector.tensor_copy, 0, 0)
+        quantise(1, 0, 0, PASSES * ROWS)
         layer1(0)
+        regroup_w2(nc.vector.tensor_copy, 0, 1)
+        new_z(2, 0)
+        add_b1_turned(0)
+        multiply2_scalar(0)
+        sort_x1(2)
+        turn_z2(0)
+        turn_x1(2)
+        collect_z2(0)
+        double_x1(2)
+        for h in range(HALVES):
+            regroup_w2(nc.scalar.copy, 1, h)
 
         for r in range(ROUNDS):
             ahead = r + 1 < ROUNDS
-            if r + 2 < ROUNDS:
-                spread_inputs(r + 2)
-            new_z(2, r)
+            routed_ahead = r + 1 < ROUTED_ROUNDS
+            if r + 3 < ROUNDS:
+                sort_x1(r + 3)
             if ahead:
                 new_z(1, r + 1)
                 for c in range(PASSES):
                     multiply1(r + 1, c)
             for c in range(PASSES):
                 multiply2(r, c)
+            if ahead:
+                quantise(1, r + 1, 0, PASSES * ROWS)
+                layer1(r + 1)
             if r > 0 and r % ROUNDS_PER_TILE == 0:
                 finish(r // ROUNDS_PER_TILE - 1)
+            if r == 0:
+                for h in range(HALVES):
+                    quantise_weights(*w2_jobs[0, h])
+            quantise(2, r, 0, PASSES * DVE_ROWS)
             if ahead:
-                quantise(1, r + 1, 0, PASSES)
-                layer1(r + 1)
-            for c in range(PASSES):
-                if r == 0:
-                    quantise_w2(c)
-                quantise(2, r, c, 1)
-                pooled(r, c)
+                new_z(2, r + 1)
+            if routed_ahead:
+                add_b1_turned(r + 1)
+                multiply2_scalar(r + 1)
+            if r == 0:
+                for h in range(HALVES):
+                    quantise_weights(*w2_jobs[1, h])
+            pooled(r, (0, 1))
+            quantise(2, r, PASSES * DVE_ROWS, PASSES * (ROWS - DVE_ROWS))
+            pooled(r, (ACT_D,))
+            if routed_ahead:
+                turn_z2(r + 1)
+            if r + 3 < ROUNDS:
+                turn_x1(r + 3)
+            if routed_ahead:
+                collect_z2(r + 1)
+            if r + 3 < ROUNDS:
+                double_x1(r + 3)
+            pooled(r, (GP_D,))
+            pooled_o1(r)
         finish(SAMPLE_TILES - 1)

@@ -20,10 +20,13 @@ D_ROUND = 4
 ROUNDS_PER_TILE = D // D_ROUND
 ROUNDS = SAMPLE_TILES * ROUNDS_PER_TILE
 ROWS = D_ROUND * P
-DVE_ROWS = 2 * P
-ACT_D = 2
-GP_D = 3
-ROUTED_ROUNDS = ROUNDS - 1
+DVE_DS = (0, 1)
+ACT_DS = (2,)
+GP_DS = (3,)
+DVE_ROWS, GP_ROWS = len(DVE_DS) * P, len(GP_DS) * P
+DVE_WORDS = PASSES * DVE_ROWS
+ACT_WORDS = PASSES * P
+GP_WORDS = PASSES * GP_ROWS
 N2 = 512
 HALVES = S2 // N2
 HALF_P = P // 2
@@ -85,27 +88,9 @@ def tile_cin_pa_t_kernel(tc, x, x1, w1, b1, w2, b2, out):
         x_words = x_fields[:].bitcast(F32)
 
         x_all = [keep.tile([P, PASSES * ROWS * 2], F32, name="x_all%d" % r) for r in range(ROUNDS)]
-        x_blocks = keep.tile([P, 3 * HALF_P], F32, name="x_blocks")
-        for block, u in enumerate((0, 1, 0)):
-            nc.vector.tensor_copy(
-                out=x_blocks[:, block * HALF_P : (block + 1) * HALF_P].rearrange(
-                    "p (a c dl) -> p a c dl", c=PASSES, dl=D_ROUND
-                ),
-                in_=x_words.rearrange("p (a dl c u) -> p u a c dl", dl=D_ROUND, c=PASSES, u=2)[:, u],
-            )
-        x_turned_ps = spread.tile([P, PACK * P], F32, name="x_turned_ps", tag="x_bank")
-        for u in range(2):
-            nc.tensor.transpose(
-                x_turned_ps[:, u * P : (u + 1) * P], x_blocks[:, u * HALF_P : u * HALF_P + P], ident_f[:]
-            )
-        x_turned = keep.tile([P, 2 * P], F32, name="x_turned")
-        nc.vector.tensor_copy(
-            out=x_turned.rearrange("p (b u) -> p b u", u=2),
-            in_=x_turned_ps[:, 0 : 2 * P].rearrange("p (u b) -> p b u", u=2),
-        )
         round_words = PASSES * ROWS * 2
         parked = out.rearrange("a n -> (a n)")[0 : ROUNDS * round_words]
-        nc.sync.dma_start(out=parked.rearrange("(p w) -> p w", w=2 * P), in_=x_turned[0:HALF_P, :])
+        b2_rows = keep.tile([P, S2], BF16, name="b2_rows")
 
         def load_x_all(r):
             nc.sync.dma_start(
@@ -113,14 +98,33 @@ def tile_cin_pa_t_kernel(tc, x, x1, w1, b1, w2, b2, out):
                 in_=parked[r * round_words : (r + 1) * round_words].partition_broadcast(P),
             )
 
-        load_w2(1)
-        load_x_all(2)
-        nc.sync.dma_start(out=x1_sb[1][:], in_=x1[P : 2 * P].rearrange("b j d -> b (j d)"))
-        load_x_all(3)
-        b2_rows = keep.tile([P, S2], BF16, name="b2_rows")
-        nc.sync.dma_start(out=b2_rows[:], in_=b2.partition_broadcast(P))
-        for r in range(4, ROUNDS):
-            load_x_all(r)
+        def park_x():
+            x_blocks = keep.tile([P, 3 * HALF_P], F32, name="x_blocks")
+            for block, u in enumerate((0, 1, 0)):
+                nc.vector.tensor_copy(
+                    out=x_blocks[:, block * HALF_P : (block + 1) * HALF_P].rearrange(
+                        "p (a c dl) -> p a c dl", c=PASSES, dl=D_ROUND
+                    ),
+                    in_=x_words.rearrange("p (a dl c u) -> p u a c dl", dl=D_ROUND, c=PASSES, u=2)[:, u],
+                )
+            x_turned_ps = spread.tile([P, PACK * P], F32, name="x_turned_ps", tag="x_bank")
+            for u in range(2):
+                nc.tensor.transpose(
+                    x_turned_ps[:, u * P : (u + 1) * P], x_blocks[:, u * HALF_P : u * HALF_P + P], ident_f[:]
+                )
+            x_turned = keep.tile([P, 2 * P], F32, name="x_turned")
+            nc.vector.tensor_copy(
+                out=x_turned.rearrange("p (b u) -> p b u", u=2),
+                in_=x_turned_ps[:, 0 : 2 * P].rearrange("p (u b) -> p b u", u=2),
+            )
+            nc.sync.dma_start(out=parked.rearrange("(p w) -> p w", w=2 * P), in_=x_turned[0:HALF_P, :])
+            load_w2(1)
+            load_x_all(2)
+            nc.sync.dma_start(out=x1_sb[1][:], in_=x1[P : 2 * P].rearrange("b j d -> b (j d)"))
+            load_x_all(3)
+            nc.sync.dma_start(out=b2_rows[:], in_=b2.partition_broadcast(P))
+            for r in range(4, ROUNDS):
+                load_x_all(r)
 
         x_f32 = keep.tile([P, SAMPLE_TILES * F0 * D], F32, name="x_f32")
         nc.gpsimd.tensor_copy(out=x_f32[:], in_=x_sb[:])
@@ -138,8 +142,10 @@ def tile_cin_pa_t_kernel(tc, x, x1, w1, b1, w2, b2, out):
         z2_turned = {}
         z2_back = {}
         sums = {}
+        sum_o1 = {}
+        result = {}
 
-        def spread_x(r):
+        def spread_x(r, copies):
             for dl in range(D_ROUND):
                 x_bank = spread.tile([P, PACK * P], F32, name="x_bank")
                 for cu in range(PACK):
@@ -149,7 +155,7 @@ def tile_cin_pa_t_kernel(tc, x, x1, w1, b1, w2, b2, out):
                         x_words[:, word : word + 1].to_broadcast([P, P]),
                         ident_f[:],
                     )
-                nc.scalar.copy(
+                copies[dl](
                     out=x_all[r].rearrange("p (c w u) -> p c w u", c=PASSES, u=2)[
                         :, :, dl * P : (dl + 1) * P, :
                     ],
@@ -165,7 +171,7 @@ def tile_cin_pa_t_kernel(tc, x, x1, w1, b1, w2, b2, out):
             )
 
         def turn_x1(r):
-            x1_t[r] = bank.tile([P, ROWS], BF16, name="x1_t")
+            x1_t[r] = bank.tile([P, 2 * ROWS], BF16, name="x1_t")
             for dl in range(D_ROUND):
                 nc.tensor.transpose(
                     x1_t[r][:, dl * P : (dl + 1) * P], x1_by_d[r][:, dl * P : (dl + 1) * P], ident_b[:]
@@ -175,7 +181,7 @@ def tile_cin_pa_t_kernel(tc, x, x1, w1, b1, w2, b2, out):
             x1_twice[r] = three.tile([P, ROWS * 2], BF16, name="x1_twice")
             nc.scalar.copy(
                 out=x1_twice[r].rearrange("p (w e) -> p w e", e=2),
-                in_=x1_t[r][:].unsqueeze(2).to_broadcast([P, ROWS, 2]),
+                in_=x1_t[r][:, 0:ROWS].unsqueeze(2).to_broadcast([P, ROWS, 2]),
             )
 
         def x_of_pass(r, c, row0, rows):
@@ -196,9 +202,11 @@ def tile_cin_pa_t_kernel(tc, x, x1, w1, b1, w2, b2, out):
         def word_col(layer, c, dl):
             if layer == 1:
                 return (c * D_ROUND + dl) * P
-            if dl * P < DVE_ROWS:
-                return c * DVE_ROWS + dl * P
-            return (dl * PASSES + c) * P
+            if dl in DVE_DS:
+                return c * DVE_ROWS + DVE_DS.index(dl) * P
+            if dl in ACT_DS:
+                return DVE_WORDS + ACT_DS.index(dl) * ACT_WORDS + c * P
+            return DVE_WORDS + len(ACT_DS) * ACT_WORDS + c * GP_ROWS + GP_DS.index(dl) * P
 
         def z2_of(r, c, dl, rows):
             first = word_col(2, c, dl) * PACK
@@ -217,24 +225,19 @@ def tile_cin_pa_t_kernel(tc, x, x1, w1, b1, w2, b2, out):
                 op=MULT,
             )
 
-        def multiply2_vector(r, c, dl, rows):
+        def multiply2(r, c):
             nc.vector.scalar_tensor_tensor(
-                out=z2_of(r, c, dl, rows).rearrange("p (w t) -> p w t", t=PACK),
-                in0=o1[r][:, dl * P : dl * P + rows].unsqueeze(2).to_broadcast([P, rows, PACK]),
+                out=z2_of(r, c, DVE_DS[0], DVE_ROWS).rearrange("p (w t) -> p w t", t=PACK),
+                in0=o1[r][:, 0:DVE_ROWS].unsqueeze(2).to_broadcast([P, DVE_ROWS, PACK]),
                 scalar=b1_col[:, 0:1],
-                in1=x_of_pass(r, c, dl * P, rows),
+                in1=x_of_pass(r, c, DVE_DS[0] * P, DVE_ROWS),
                 op0=ADD,
                 op1=MULT,
             )
-
-        def multiply2(r, c):
-            multiply2_vector(r, c, 0, DVE_ROWS)
-            if r >= ROUTED_ROUNDS:
-                multiply2_vector(r, c, ACT_D, P)
             nc.gpsimd.tensor_tensor(
-                out=z2_of(r, c, GP_D, P).rearrange("p (w t) -> p w t", t=PACK),
-                in0=o1_gp[r][:].unsqueeze(2).to_broadcast([P, P, PACK]),
-                in1=x_of_pass(r, c, GP_D * P, P),
+                out=z2_of(r, c, GP_DS[0], GP_ROWS).rearrange("p (w t) -> p w t", t=PACK),
+                in0=o1_gp[r][:].unsqueeze(2).to_broadcast([P, GP_ROWS, PACK]),
+                in1=x_of_pass(r, c, GP_DS[0] * P, GP_ROWS),
                 op=MULT,
             )
 
@@ -246,28 +249,12 @@ def tile_cin_pa_t_kernel(tc, x, x1, w1, b1, w2, b2, out):
             )
 
         def layer1(r):
-            o1[r] = bank.tile([P, ROWS], F32, name="o1")
-            o1_apart = spread.tile([P, PACK * P], F32, name="o1_apart", tag="x_bank")
-            groups = [(o1_apart, 0, GP_D * P, P), (o1[r], 0, 0, DVE_ROWS)]
-            if r >= ROUTED_ROUNDS:
-                groups.append((o1[r], ACT_D * P, ACT_D * P, P))
-            for target, col0, row0, rows in groups:
+            o1_turned_ps[r] = spread.tile([P, PACK * P], F32, name="o1_turned_ps", tag="x_bank")
+            for n, dl in enumerate(ACT_DS):
                 for c in range(PASSES):
+                    block = slice(word_col(1, c, dl), word_col(1, c, dl) + P)
                     nc.tensor.matmul_mx(
-                        out=target[:, col0 : col0 + rows],
-                        lhsT=w1_codes[:, c * S1 : (c + 1) * S1].bitcast(FP8X4),
-                        lhsT_scale=w1_scales[:, c * S1 : (c + 1) * S1],
-                        rhs=z_codes[1, r][:, c * ROWS + row0 : c * ROWS + row0 + rows].bitcast(FP8X4),
-                        rhs_scale=z_scales[1, r][:, c * ROWS + row0 : c * ROWS + row0 + rows],
-                        start=(c == 0),
-                        stop=(c == PASSES - 1),
-                    )
-            if r < ROUTED_ROUNDS:
-                o1_turned_ps[r] = spread.tile([P, PACK * P], F32, name="o1_turned_ps", tag="x_bank")
-                for c in range(PASSES):
-                    block = slice(word_col(1, c, ACT_D), word_col(1, c, ACT_D) + P)
-                    nc.tensor.matmul_mx(
-                        out=o1_turned_ps[r][:, 0:S1],
+                        out=o1_turned_ps[r][:, n * S1 : (n + 1) * S1],
                         lhsT=z_codes[1, r][:, block].bitcast(FP8X4),
                         lhsT_scale=z_scales[1, r][:, block],
                         rhs=w1_codes[:, c * S1 : (c + 1) * S1].bitcast(FP8X4),
@@ -275,67 +262,94 @@ def tile_cin_pa_t_kernel(tc, x, x1, w1, b1, w2, b2, out):
                         start=(c == 0),
                         stop=(c == PASSES - 1),
                     )
-            o1_gp[r] = two.tile([P, P], F32, name="o1_gp")
-            nc.scalar.activation(out=o1_gp[r][:], in_=o1_apart[:, 0:P], func=IDENTITY, bias=b1_col[:, 0:1])
+            o1[r] = bank.tile([P, ROWS], F32, name="o1")
+            o1_apart = spread.tile([P, PACK * P], F32, name="o1_apart", tag="x_bank")
+            for target, row0, rows in [(o1[r], DVE_DS[0] * P, DVE_ROWS), (o1_apart, GP_DS[0] * P, GP_ROWS)]:
+                for c in range(PASSES):
+                    nc.tensor.matmul_mx(
+                        out=target[:, 0:rows],
+                        lhsT=w1_codes[:, c * S1 : (c + 1) * S1].bitcast(FP8X4),
+                        lhsT_scale=w1_scales[:, c * S1 : (c + 1) * S1],
+                        rhs=z_codes[1, r][:, c * ROWS + row0 : c * ROWS + row0 + rows].bitcast(FP8X4),
+                        rhs_scale=z_scales[1, r][:, c * ROWS + row0 : c * ROWS + row0 + rows],
+                        start=(c == 0),
+                        stop=(c == PASSES - 1),
+                    )
+            o1_gp[r] = two.tile([P, GP_ROWS], F32, name="o1_gp")
+            nc.scalar.activation(
+                out=o1_gp[r][:], in_=o1_apart[:, 0:GP_ROWS], func=IDENTITY, bias=b1_col[:, 0:1]
+            )
 
         def add_b1_turned(r):
-            o1_turned[r] = two.tile([P, S1], F32, name="o1_turned")
-            nc.vector.tensor_tensor(out=o1_turned[r][:], in0=o1_turned_ps[r][:, 0:S1], in1=b1_rows[:], op=ADD)
+            width = len(ACT_DS) * S1
+            o1_turned[r] = two.tile([P, width], F32, name="o1_turned")
+            nc.vector.tensor_tensor(
+                out=o1_turned[r].rearrange("p (n j) -> p n j", j=S1),
+                in0=o1_turned_ps[r][:, 0:width].rearrange("p (n j) -> p n j", j=S1),
+                in1=b1_rows[:].unsqueeze(1).to_broadcast([P, len(ACT_DS), S1]),
+                op=ADD,
+            )
 
         def multiply2_scalar(r):
-            s, d = r // ROUNDS_PER_TILE, (r % ROUNDS_PER_TILE) * D_ROUND + ACT_D
-            z2_turned[r] = two.tile([P, F0 * S1], BF16, name="z2_turned")
-            for i in range(F0):
-                col = (s * F0 + i) * D + d
-                nc.scalar.activation(
-                    out=z2_turned[r].rearrange("p (g j e) -> p g e j", g=F0 // 2, e=2)[:, i // 2, i % 2],
-                    in_=o1_turned[r][:],
-                    func=COPY,
-                    scale=x_f32[:, col : col + 1],
-                )
+            s = r // ROUNDS_PER_TILE
+            z2_turned[r] = two.tile([P, len(ACT_DS) * F0 * S1], BF16, name="z2_turned")
+            for n, dl in enumerate(ACT_DS):
+                for i in range(F0):
+                    col = (s * F0 + i) * D + (r % ROUNDS_PER_TILE) * D_ROUND + dl
+                    nc.scalar.activation(
+                        out=z2_turned[r].rearrange("p (n g j e) -> p n g e j", n=len(ACT_DS), g=F0 // 2, e=2)[
+                            :, n, i // 2, i % 2
+                        ],
+                        in_=o1_turned[r][:, n * S1 : (n + 1) * S1],
+                        func=COPY,
+                        scale=x_f32[:, col : col + 1],
+                    )
 
-        def turn_z2(r):
-            z2_back[r] = spread.tile([P, PACK * P], F32, name="z2_back", tag="x_bank")
+        def turn_z2(r, n):
+            z2_back[r, n] = spread.tile([P, PACK * P], F32, name="z2_back", tag="x_bank")
             for g in range(F0 // 2):
+                word0 = (n * (F0 // 2) + g) * P
                 nc.tensor.transpose(
-                    z2_back[r][:, g * P : (g + 1) * P],
-                    z2_turned[r][:].bitcast(F32)[:, g * P : (g + 1) * P],
+                    z2_back[r, n][:, g * P : (g + 1) * P],
+                    z2_turned[r][:].bitcast(F32)[:, word0 : word0 + P],
                     ident_f[:],
                 )
 
-        def collect_z2(r):
+        def collect_z2(r, n):
             nc.scalar.copy(
-                out=z2_of(r, 0, ACT_D, PASSES * P).bitcast(F32).rearrange("p (c b u) -> p c b u", c=PASSES, u=2),
-                in_=z2_back[r].rearrange("p (c u b) -> p c b u", c=PASSES, u=2),
+                out=z2_of(r, 0, ACT_DS[n], PASSES * P)
+                .bitcast(F32)
+                .rearrange("p (c b u) -> p c b u", c=PASSES, u=2),
+                in_=z2_back[r, n].rearrange("p (c u b) -> p c b u", c=PASSES, u=2),
             )
 
-        def pooled(r, positions):
-            s, q = r // ROUNDS_PER_TILE, r % ROUNDS_PER_TILE
-            if q == 0 and positions[0] == 0:
+        def pooled(r, blocks, first=False, last=False):
+            s = r // ROUNDS_PER_TILE
+            if first:
                 sums[s] = [bank.tile([P, N2], F32, name="sum_o2_%d" % h) for h in range(HALVES)]
-                sums[s].append(bank.tile([P, S1], F32, name="sum_o1"))
-            for c in range(PASSES):
-                for h in range(HALVES):
-                    for dl in positions:
-                        block = slice(word_col(2, c, dl), word_col(2, c, dl) + P)
-                        w_cols = slice(c * S2 + h * N2, c * S2 + (h + 1) * N2)
-                        nc.tensor.matmul_mx(
-                            out=sums[s][h][:],
-                            lhsT=z_codes[2, r][:, block].bitcast(FP8X4),
-                            lhsT_scale=z_scales[2, r][:, block],
-                            rhs=w2_codes[:, w_cols].bitcast(FP8X4),
-                            rhs_scale=w2_scales[:, w_cols],
-                            start=(q == 0 and c == 0 and dl == 0),
-                            stop=(q == ROUNDS_PER_TILE - 1 and c == PASSES - 1 and dl == D_ROUND - 1),
-                        )
+            for h in range(HALVES):
+                for n, (c, dl) in enumerate(blocks):
+                    block = slice(word_col(2, c, dl), word_col(2, c, dl) + P)
+                    w_cols = slice(c * S2 + h * N2, c * S2 + (h + 1) * N2)
+                    nc.tensor.matmul_mx(
+                        out=sums[s][h][:],
+                        lhsT=z_codes[2, r][:, block].bitcast(FP8X4),
+                        lhsT_scale=z_scales[2, r][:, block],
+                        rhs=w2_codes[:, w_cols].bitcast(FP8X4),
+                        rhs_scale=w2_scales[:, w_cols],
+                        start=(first and n == 0),
+                        stop=(last and n == len(blocks) - 1),
+                    )
 
         def pooled_o1(r):
             s, q = r // ROUNDS_PER_TILE, r % ROUNDS_PER_TILE
+            if q == 0:
+                sum_o1[s] = bank.tile([P, N2], F32, name="sum_o1")
             for c in range(PASSES):
                 for dl in range(D_ROUND):
                     block = slice(word_col(1, c, dl), word_col(1, c, dl) + P)
                     nc.tensor.matmul_mx(
-                        out=sums[s][HALVES][:],
+                        out=sum_o1[s][:, 0:S1],
                         lhsT=z_codes[1, r][:, block].bitcast(FP8X4),
                         lhsT_scale=z_scales[1, r][:, block],
                         rhs=w1_codes[:, c * S1 : (c + 1) * S1].bitcast(FP8X4),
@@ -344,22 +358,24 @@ def tile_cin_pa_t_kernel(tc, x, x1, w1, b1, w2, b2, out):
                         stop=(q == ROUNDS_PER_TILE - 1 and c == PASSES - 1 and dl == D_ROUND - 1),
                     )
 
-        def finish(s):
-            result = two.tile([P, S1 + S2], F32, name="result")
-            pieces = [(S1 + h * N2, N2, b2_rows[:, h * N2 : (h + 1) * N2]) for h in range(HALVES)]
-            pieces.append((0, S1, b1_rows[:]))
-            for h, (col, width, bias) in enumerate(pieces):
-                nc.vector.scalar_tensor_tensor(
-                    out=result[:, col : col + width],
-                    in0=bias,
-                    scalar=float(D),
-                    in1=sums[s][h][:],
-                    op0=MULT,
-                    op1=ADD,
-                )
-                nc.sync.dma_start(
-                    out=out[s * P : (s + 1) * P, col : col + width], in_=result[:, col : col + width]
-                )
+        def finish(s, col, width, bias, total):
+            if s not in result:
+                result[s] = two.tile([P, S1 + S2], F32, name="result")
+            nc.vector.scalar_tensor_tensor(
+                out=result[s][:, col : col + width],
+                in0=bias,
+                scalar=float(D),
+                in1=total,
+                op0=MULT,
+                op1=ADD,
+            )
+            nc.sync.dma_start(out=out[s * P : (s + 1) * P, col : col + width], in_=result[s][:, col : col + width])
+
+        def finish_o1(s):
+            finish(s, 0, S1, b1_rows[:], sum_o1[s][:, 0:S1])
+
+        def finish_o2(s, h):
+            finish(s, S1 + h * N2, N2, b2_rows[:, h * N2 : (h + 1) * N2], sums[s][h][:])
 
         def regroup(copy, dst, src):
             copy(
@@ -378,13 +394,18 @@ def tile_cin_pa_t_kernel(tc, x, x1, w1, b1, w2, b2, out):
             cols = slice(c * S2 + h * N2, c * S2 + (h + 1) * N2)
             w2_jobs[c, h] = (w2_codes[:, cols], w2_scales[:, cols], w2_grouped[:])
 
-        for r in range(PE_SPREAD_ROUNDS):
-            sort_x1(r)
-            spread_x(r)
-            turn_x1(r)
-            double_x1(r)
+        v_copy, s_copy = nc.vector.tensor_copy, nc.scalar.copy
+        spread_x(0, [s_copy, v_copy, s_copy, v_copy])
+        sort_x1(0)
+        turn_x1(0)
+        double_x1(0)
+        park_x()
+        sort_x1(1)
+        spread_x(1, [s_copy] * D_ROUND)
+        turn_x1(1)
+        double_x1(1)
 
-        b1_t = bank.tile([P, ROWS], BF16, name="b1_t", tag="x1_t")
+        b1_t = bank.tile([P, 2 * ROWS], BF16, name="b1_t", tag="x1_t")
         nc.tensor.transpose(b1_t[:, 0:P], b1_rows[:], ident_b[:])
         b1_col = keep.tile([P, 1], F32, name="b1_col")
         nc.scalar.copy(out=b1_col[:], in_=b1_t[:, 0:1])
@@ -397,64 +418,84 @@ def tile_cin_pa_t_kernel(tc, x, x1, w1, b1, w2, b2, out):
         for c in range(PASSES):
             part = slice(c * S1 * PACK, (c + 1) * S1 * PACK)
             regroup(nc.vector.tensor_copy, w1_grouped[:, part], w1_raw[:, part])
+        dve_blocks = [(c, dl) for c in range(PASSES) for dl in DVE_DS]
+        act_blocks = [(c, dl) for dl in ACT_DS for c in range(PASSES)]
+        gp_blocks = [(c, dl) for c in range(PASSES) for dl in GP_DS]
+        per_pass = len(DVE_DS)
+
+        def quantise1(r):
+            for c in range(PASSES):
+                quantise(1, r, c * ROWS, ROWS)
+
+        def after_layer1(r):
+            new_z(2, r)
+            add_b1_turned(r)
+            multiply2_scalar(r)
+            pooled_o1(r)
+            for n in range(len(ACT_DS)):
+                turn_z2(r, n)
+            if r + 2 < ROUNDS:
+                turn_x1(r + 2)
+            for n in range(len(ACT_DS)):
+                collect_z2(r, n)
+            if r + 2 < ROUNDS:
+                double_x1(r + 2)
+
         new_z(1, 0)
         multiply1(0, 0)
         quantise_weights(w1_codes[:], w1_scales[:], w1_grouped[:])
         multiply1(0, 1)
         regroup_w2(nc.vector.tensor_copy, 0, 0)
-        quantise(1, 0, 0, PASSES * ROWS)
+        quantise1(0)
         layer1(0)
         regroup_w2(nc.vector.tensor_copy, 0, 1)
-        new_z(2, 0)
-        add_b1_turned(0)
-        multiply2_scalar(0)
         sort_x1(2)
-        turn_z2(0)
-        turn_x1(2)
-        collect_z2(0)
-        double_x1(2)
+        after_layer1(0)
         for h in range(HALVES):
             regroup_w2(nc.scalar.copy, 1, h)
 
         for r in range(ROUNDS):
+            s, q = r // ROUNDS_PER_TILE, r % ROUNDS_PER_TILE
             ahead = r + 1 < ROUNDS
-            routed_ahead = r + 1 < ROUTED_ROUNDS
             if r + 3 < ROUNDS:
                 sort_x1(r + 3)
-            if ahead:
-                new_z(1, r + 1)
-                for c in range(PASSES):
-                    multiply1(r + 1, c)
             for c in range(PASSES):
                 multiply2(r, c)
             if ahead:
-                quantise(1, r + 1, 0, PASSES * ROWS)
-                layer1(r + 1)
-            if r > 0 and r % ROUNDS_PER_TILE == 0:
-                finish(r // ROUNDS_PER_TILE - 1)
+                new_z(1, r + 1)
+                multiply1(r + 1, 0)
+            if r > 0 and q == 0:
+                for h in range(HALVES):
+                    finish_o2(s - 1, h)
+            if q == ROUNDS_PER_TILE - 1:
+                finish_o1(s)
             if r == 0:
                 for h in range(HALVES):
                     quantise_weights(*w2_jobs[0, h])
-            quantise(2, r, 0, PASSES * DVE_ROWS)
             if ahead:
-                new_z(2, r + 1)
-            if routed_ahead:
-                add_b1_turned(r + 1)
-                multiply2_scalar(r + 1)
-            if r == 0:
+                quantise(2, r, 0, DVE_WORDS)
+                pooled(r, dve_blocks[0:per_pass], first=(q == 0))
+                if r > 0:
+                    pooled(r, dve_blocks[per_pass:])
+                multiply1(r + 1, 1)
+                quantise1(r + 1)
+                layer1(r + 1)
+                if r == 0:
+                    for h in range(HALVES):
+                        quantise_weights(*w2_jobs[1, h])
+                    pooled(r, dve_blocks[per_pass:])
+                quantise(2, r, DVE_WORDS, len(ACT_DS) * ACT_WORDS)
+                pooled(r, act_blocks)
+                quantise(2, r, DVE_WORDS + len(ACT_DS) * ACT_WORDS, GP_WORDS)
+                pooled(r, gp_blocks, last=(q == ROUNDS_PER_TILE - 1))
+                after_layer1(r + 1)
+            else:
+                for c in range(PASSES):
+                    quantise(2, r, c * DVE_ROWS, DVE_ROWS)
+                    pooled(r, dve_blocks[c * per_pass : (c + 1) * per_pass])
+                quantise(2, r, DVE_WORDS, len(ACT_DS) * ACT_WORDS)
+                pooled(r, act_blocks)
+                quantise(2, r, DVE_WORDS + len(ACT_DS) * ACT_WORDS, GP_WORDS)
+                pooled(r, gp_blocks, last=True)
                 for h in range(HALVES):
-                    quantise_weights(*w2_jobs[1, h])
-            pooled(r, (0, 1))
-            quantise(2, r, PASSES * DVE_ROWS, PASSES * (ROWS - DVE_ROWS))
-            pooled(r, (ACT_D,))
-            if routed_ahead:
-                turn_z2(r + 1)
-            if r + 3 < ROUNDS:
-                turn_x1(r + 3)
-            if routed_ahead:
-                collect_z2(r + 1)
-            if r + 3 < ROUNDS:
-                double_x1(r + 3)
-            pooled(r, (GP_D,))
-            pooled_o1(r)
-        finish(SAMPLE_TILES - 1)
+                    finish_o2(s, h)

@@ -27,6 +27,7 @@ DVE_ROWS, GP_ROWS = len(DVE_DS) * P, len(GP_DS) * P
 DVE_WORDS = PASSES * DVE_ROWS
 ACT_WORDS = PASSES * P
 GP_WORDS = PASSES * GP_ROWS
+ROUTED_ROUNDS = ROUNDS - 1
 N2 = 512
 HALVES = S2 // N2
 HALF_P = P // 2
@@ -73,6 +74,10 @@ def tile_cin_pa_t_kernel(tc, x, x1, w1, b1, w2, b2, out):
                 )
 
         load_w2(0)
+        load_w2(1)
+        nc.sync.dma_start(out=x1_sb[1][:], in_=x1[P : 2 * P].rearrange("b j d -> b (j d)"))
+        b2_rows = keep.tile([P, S2], BF16, name="b2_rows")
+        nc.sync.dma_start(out=b2_rows[:], in_=b2.partition_broadcast(P))
 
         ident_f = keep.tile([P, P], F32, name="ident_f")
         make_identity(nc, ident_f[:])
@@ -90,7 +95,6 @@ def tile_cin_pa_t_kernel(tc, x, x1, w1, b1, w2, b2, out):
         x_all = [keep.tile([P, PASSES * ROWS * 2], F32, name="x_all%d" % r) for r in range(ROUNDS)]
         round_words = PASSES * ROWS * 2
         parked = out.rearrange("a n -> (a n)")[0 : ROUNDS * round_words]
-        b2_rows = keep.tile([P, S2], BF16, name="b2_rows")
 
         def load_x_all(r):
             nc.sync.dma_start(
@@ -118,12 +122,7 @@ def tile_cin_pa_t_kernel(tc, x, x1, w1, b1, w2, b2, out):
                 in_=x_turned_ps[:, 0 : 2 * P].rearrange("p (u b) -> p b u", u=2),
             )
             nc.sync.dma_start(out=parked.rearrange("(p w) -> p w", w=2 * P), in_=x_turned[0:HALF_P, :])
-            load_w2(1)
-            load_x_all(2)
-            nc.sync.dma_start(out=x1_sb[1][:], in_=x1[P : 2 * P].rearrange("b j d -> b (j d)"))
-            load_x_all(3)
-            nc.sync.dma_start(out=b2_rows[:], in_=b2.partition_broadcast(P))
-            for r in range(4, ROUNDS):
+            for r in range(PE_SPREAD_ROUNDS, ROUNDS):
                 load_x_all(r)
 
         x_f32 = keep.tile([P, SAMPLE_TILES * F0 * D], F32, name="x_f32")
@@ -225,15 +224,18 @@ def tile_cin_pa_t_kernel(tc, x, x1, w1, b1, w2, b2, out):
                 op=MULT,
             )
 
-        def multiply2(r, c):
+        def multiply2_vector(r, c, dl, col0, rows):
             nc.vector.scalar_tensor_tensor(
-                out=z2_of(r, c, DVE_DS[0], DVE_ROWS).rearrange("p (w t) -> p w t", t=PACK),
-                in0=o1[r][:, 0:DVE_ROWS].unsqueeze(2).to_broadcast([P, DVE_ROWS, PACK]),
+                out=z2_of(r, c, dl, rows).rearrange("p (w t) -> p w t", t=PACK),
+                in0=o1[r][:, col0 : col0 + rows].unsqueeze(2).to_broadcast([P, rows, PACK]),
                 scalar=b1_col[:, 0:1],
-                in1=x_of_pass(r, c, DVE_DS[0] * P, DVE_ROWS),
+                in1=x_of_pass(r, c, dl * P, rows),
                 op0=ADD,
                 op1=MULT,
             )
+
+        def multiply2(r, c):
+            multiply2_vector(r, c, DVE_DS[0], 0, DVE_ROWS)
             nc.gpsimd.tensor_tensor(
                 out=z2_of(r, c, GP_DS[0], GP_ROWS).rearrange("p (w t) -> p w t", t=PACK),
                 in0=o1_gp[r][:].unsqueeze(2).to_broadcast([P, GP_ROWS, PACK]),
@@ -249,8 +251,9 @@ def tile_cin_pa_t_kernel(tc, x, x1, w1, b1, w2, b2, out):
             )
 
         def layer1(r):
-            o1_turned_ps[r] = spread.tile([P, PACK * P], F32, name="o1_turned_ps", tag="x_bank")
-            for n, dl in enumerate(ACT_DS):
+            if r < ROUTED_ROUNDS:
+                o1_turned_ps[r] = spread.tile([P, PACK * P], F32, name="o1_turned_ps", tag="x_bank")
+            for n, dl in enumerate(ACT_DS if r < ROUTED_ROUNDS else ()):
                 for c in range(PASSES):
                     block = slice(word_col(1, c, dl), word_col(1, c, dl) + P)
                     nc.tensor.matmul_mx(
@@ -264,10 +267,13 @@ def tile_cin_pa_t_kernel(tc, x, x1, w1, b1, w2, b2, out):
                     )
             o1[r] = bank.tile([P, ROWS], F32, name="o1")
             o1_apart = spread.tile([P, PACK * P], F32, name="o1_apart", tag="x_bank")
-            for target, row0, rows in [(o1[r], DVE_DS[0] * P, DVE_ROWS), (o1_apart, GP_DS[0] * P, GP_ROWS)]:
+            groups = [(o1[r], 0, DVE_DS[0] * P, DVE_ROWS), (o1_apart, 0, GP_DS[0] * P, GP_ROWS)]
+            if r >= ROUTED_ROUNDS:
+                groups.extend((o1[r], DVE_ROWS + n * P, dl * P, P) for n, dl in enumerate(ACT_DS))
+            for target, col0, row0, rows in groups:
                 for c in range(PASSES):
                     nc.tensor.matmul_mx(
-                        out=target[:, 0:rows],
+                        out=target[:, col0 : col0 + rows],
                         lhsT=w1_codes[:, c * S1 : (c + 1) * S1].bitcast(FP8X4),
                         lhsT_scale=w1_scales[:, c * S1 : (c + 1) * S1],
                         rhs=z_codes[1, r][:, c * ROWS + row0 : c * ROWS + row0 + rows].bitcast(FP8X4),
@@ -395,11 +401,29 @@ def tile_cin_pa_t_kernel(tc, x, x1, w1, b1, w2, b2, out):
             w2_jobs[c, h] = (w2_codes[:, cols], w2_scales[:, cols], w2_grouped[:])
 
         v_copy, s_copy = nc.vector.tensor_copy, nc.scalar.copy
-        spread_x(0, [s_copy, v_copy, s_copy, v_copy])
+        w1_grouped = keep.tile([P, PASSES * S1 * PACK], BF16, name="w1_grouped", align_bytes=64)
+        w1_codes = keep.tile([P, PASSES * S1], U32, name="w1_codes", align_bytes=64)
+        w1_scales = keep.tile([P, PASSES * S1], U8, name="w1_scales", align_bytes=64)
+        w2_codes = keep.tile([P, PASSES * S2], U32, name="w2_codes", align_bytes=64)
+        w2_scales = keep.tile([P, PASSES * S2], U8, name="w2_scales", align_bytes=64)
+        dve_blocks = [(c, dl) for c in range(PASSES) for dl in DVE_DS]
+        act_blocks = [(c, dl) for dl in ACT_DS for c in range(PASSES)]
+        gp_blocks = [(c, dl) for c in range(PASSES) for dl in GP_DS]
+        per_pass = len(DVE_DS)
+        act_words0 = DVE_WORDS
+        gp_words0 = DVE_WORDS + len(ACT_DS) * ACT_WORDS
+
+        def regroup_w1(c):
+            part = slice(c * S1 * PACK, (c + 1) * S1 * PACK)
+            regroup(nc.vector.tensor_copy, w1_grouped[:, part], w1_raw[:, part])
+
         sort_x1(0)
+        spread_x(0, [s_copy, v_copy, s_copy, v_copy])
         turn_x1(0)
         double_x1(0)
         park_x()
+        regroup_w1(0)
+        regroup_w1(1)
         sort_x1(1)
         spread_x(1, [s_copy] * D_ROUND)
         turn_x1(1)
@@ -410,92 +434,79 @@ def tile_cin_pa_t_kernel(tc, x, x1, w1, b1, w2, b2, out):
         b1_col = keep.tile([P, 1], F32, name="b1_col")
         nc.scalar.copy(out=b1_col[:], in_=b1_t[:, 0:1])
 
-        w1_grouped = keep.tile([P, PASSES * S1 * PACK], BF16, name="w1_grouped", align_bytes=64)
-        w1_codes = keep.tile([P, PASSES * S1], U32, name="w1_codes", align_bytes=64)
-        w1_scales = keep.tile([P, PASSES * S1], U8, name="w1_scales", align_bytes=64)
-        w2_codes = keep.tile([P, PASSES * S2], U32, name="w2_codes", align_bytes=64)
-        w2_scales = keep.tile([P, PASSES * S2], U8, name="w2_scales", align_bytes=64)
-        for c in range(PASSES):
-            part = slice(c * S1 * PACK, (c + 1) * S1 * PACK)
-            regroup(nc.vector.tensor_copy, w1_grouped[:, part], w1_raw[:, part])
-        dve_blocks = [(c, dl) for c in range(PASSES) for dl in DVE_DS]
-        act_blocks = [(c, dl) for dl in ACT_DS for c in range(PASSES)]
-        gp_blocks = [(c, dl) for c in range(PASSES) for dl in GP_DS]
-        per_pass = len(DVE_DS)
-
-        def quantise1(r):
-            for c in range(PASSES):
-                quantise(1, r, c * ROWS, ROWS)
-
-        def after_layer1(r):
-            new_z(2, r)
-            add_b1_turned(r)
-            multiply2_scalar(r)
-            pooled_o1(r)
-            for n in range(len(ACT_DS)):
-                turn_z2(r, n)
-            if r + 2 < ROUNDS:
-                turn_x1(r + 2)
-            for n in range(len(ACT_DS)):
-                collect_z2(r, n)
-            if r + 2 < ROUNDS:
-                double_x1(r + 2)
-
         new_z(1, 0)
         multiply1(0, 0)
         quantise_weights(w1_codes[:], w1_scales[:], w1_grouped[:])
         multiply1(0, 1)
-        regroup_w2(nc.vector.tensor_copy, 0, 0)
-        quantise1(0)
-        layer1(0)
-        regroup_w2(nc.vector.tensor_copy, 0, 1)
         sort_x1(2)
-        after_layer1(0)
+        turn_x1(2)
+        double_x1(2)
         for h in range(HALVES):
             regroup_w2(nc.scalar.copy, 1, h)
+        quantise(1, 0, 0, PASSES * ROWS)
+        layer1(0)
+        pooled_o1(0)
+        for h in range(HALVES):
+            regroup_w2(nc.vector.tensor_copy, 0, h)
+
+        def transposes(r):
+            routed = range(len(ACT_DS) if r < ROUTED_ROUNDS else 0)
+            for n in routed:
+                turn_z2(r, n)
+            if r + 3 < ROUNDS:
+                turn_x1(r + 3)
+            for n in routed:
+                collect_z2(r, n)
+            if r + 3 < ROUNDS:
+                double_x1(r + 3)
+
+        def quantise_scalars(r, last=False):
+            quantise(2, r, act_words0, len(ACT_DS) * ACT_WORDS)
+            pooled(r, act_blocks, last=last)
 
         for r in range(ROUNDS):
             s, q = r // ROUNDS_PER_TILE, r % ROUNDS_PER_TILE
             ahead = r + 1 < ROUNDS
-            if r + 3 < ROUNDS:
-                sort_x1(r + 3)
-            for c in range(PASSES):
-                multiply2(r, c)
+            new_z(2, r)
             if ahead:
                 new_z(1, r + 1)
                 multiply1(r + 1, 0)
+            if r > 0:
+                quantise_scalars(r - 1, last=(q == 0))
+            if r < ROUTED_ROUNDS:
+                add_b1_turned(r)
+                multiply2_scalar(r)
+            if r + 3 < ROUNDS:
+                sort_x1(r + 3)
+            if ahead:
+                multiply1(r + 1, 1)
+            for c in range(PASSES):
+                multiply2(r, c)
+            if r >= ROUTED_ROUNDS:
+                for n, dl in enumerate(ACT_DS):
+                    for c in range(PASSES):
+                        multiply2_vector(r, c, dl, DVE_ROWS + n * P, P)
+            transposes(r)
+            if q == ROUNDS_PER_TILE - 1:
+                finish_o1(s)
+            if ahead:
+                quantise(1, r + 1, 0, PASSES * ROWS)
+                layer1(r + 1)
+                pooled_o1(r + 1)
             if r > 0 and q == 0:
                 for h in range(HALVES):
                     finish_o2(s - 1, h)
-            if q == ROUNDS_PER_TILE - 1:
-                finish_o1(s)
             if r == 0:
                 for h in range(HALVES):
                     quantise_weights(*w2_jobs[0, h])
-            if ahead:
-                quantise(2, r, 0, DVE_WORDS)
-                pooled(r, dve_blocks[0:per_pass], first=(q == 0))
-                if r > 0:
-                    pooled(r, dve_blocks[per_pass:])
-                multiply1(r + 1, 1)
-                quantise1(r + 1)
-                layer1(r + 1)
-                if r == 0:
-                    for h in range(HALVES):
-                        quantise_weights(*w2_jobs[1, h])
-                    pooled(r, dve_blocks[per_pass:])
-                quantise(2, r, DVE_WORDS, len(ACT_DS) * ACT_WORDS)
-                pooled(r, act_blocks)
-                quantise(2, r, DVE_WORDS + len(ACT_DS) * ACT_WORDS, GP_WORDS)
-                pooled(r, gp_blocks, last=(q == ROUNDS_PER_TILE - 1))
-                after_layer1(r + 1)
-            else:
-                for c in range(PASSES):
-                    quantise(2, r, c * DVE_ROWS, DVE_ROWS)
-                    pooled(r, dve_blocks[c * per_pass : (c + 1) * per_pass])
-                quantise(2, r, DVE_WORDS, len(ACT_DS) * ACT_WORDS)
-                pooled(r, act_blocks)
-                quantise(2, r, DVE_WORDS + len(ACT_DS) * ACT_WORDS, GP_WORDS)
-                pooled(r, gp_blocks, last=True)
+            quantise(2, r, 0, DVE_WORDS)
+            pooled(r, dve_blocks[0:per_pass], first=(q == 0))
+            if r == 0:
                 for h in range(HALVES):
-                    finish_o2(s, h)
+                    quantise_weights(*w2_jobs[1, h])
+            pooled(r, dve_blocks[per_pass:])
+            quantise(2, r, gp_words0, GP_WORDS)
+            pooled(r, gp_blocks)
+        quantise_scalars(ROUNDS - 1, last=True)
+        for h in range(HALVES):
+            finish_o2(SAMPLE_TILES - 1, h)

@@ -441,11 +441,11 @@ def tile_cin_pa_t_kernel(tc, x, x1, w1, b1, w2, b2, out):
         sort_x1(2)
         turn_x1(2)
         double_x1(2)
-        for h in range(HALVES):
-            regroup_w2(nc.scalar.copy, 1, h)
         quantise(1, 0, 0, PASSES * ROWS)
         layer1(0)
         pooled_o1(0)
+        for h in range(HALVES):
+            regroup_w2(nc.scalar.copy, 1, h)
         for h in range(HALVES):
             regroup_w2(nc.vector.tensor_copy, 0, h)
 
@@ -473,13 +473,13 @@ def tile_cin_pa_t_kernel(tc, x, x1, w1, b1, w2, b2, out):
                 multiply1(r + 1, 0)
             if r > 0:
                 quantise_scalars(r - 1, last=(q == 0))
-            if r < ROUTED_ROUNDS:
-                add_b1_turned(r)
-                multiply2_scalar(r)
             if r + 3 < ROUNDS:
                 sort_x1(r + 3)
             if ahead:
                 multiply1(r + 1, 1)
+            if r < ROUTED_ROUNDS:
+                add_b1_turned(r)
+                multiply2_scalar(r)
             for c in range(PASSES):
                 multiply2(r, c)
             if r >= ROUTED_ROUNDS:

@@ -27,6 +27,7 @@ DVE_ROWS, GP_ROWS = len(DVE_DS) * P, len(GP_DS) * P
 DVE_WORDS = PASSES * DVE_ROWS
 ACT_WORDS = PASSES * P
 GP_WORDS = PASSES * GP_ROWS
+GP_EXTRA = 64
 ROUTED_ROUNDS = ROUNDS - 1
 N2 = 512
 HALVES = S2 // N2
@@ -102,7 +103,9 @@ def tile_cin_pa_t_kernel(tc, x, x1, w1, b1, w2, b2, out):
                 in_=parked[r * round_words : (r + 1) * round_words].partition_broadcast(P),
             )
 
-        def park_x():
+        x_turned_ps = {}
+
+        def turn_x():
             x_blocks = keep.tile([P, 3 * HALF_P], F32, name="x_blocks")
             for block, u in enumerate((0, 1, 0)):
                 nc.vector.tensor_copy(
@@ -111,15 +114,17 @@ def tile_cin_pa_t_kernel(tc, x, x1, w1, b1, w2, b2, out):
                     ),
                     in_=x_words.rearrange("p (a dl c u) -> p u a c dl", dl=D_ROUND, c=PASSES, u=2)[:, u],
                 )
-            x_turned_ps = spread.tile([P, PACK * P], F32, name="x_turned_ps", tag="x_bank")
+            x_turned_ps[0] = spread.tile([P, PACK * P], F32, name="x_turned_ps", tag="x_bank")
             for u in range(2):
                 nc.tensor.transpose(
-                    x_turned_ps[:, u * P : (u + 1) * P], x_blocks[:, u * HALF_P : u * HALF_P + P], ident_f[:]
+                    x_turned_ps[0][:, u * P : (u + 1) * P], x_blocks[:, u * HALF_P : u * HALF_P + P], ident_f[:]
                 )
+
+        def park_x():
             x_turned = keep.tile([P, 2 * P], F32, name="x_turned")
             nc.vector.tensor_copy(
                 out=x_turned.rearrange("p (b u) -> p b u", u=2),
-                in_=x_turned_ps[:, 0 : 2 * P].rearrange("p (u b) -> p b u", u=2),
+                in_=x_turned_ps[0][:, 0 : 2 * P].rearrange("p (u b) -> p b u", u=2),
             )
             nc.sync.dma_start(out=parked.rearrange("(p w) -> p w", w=2 * P), in_=x_turned[0:HALF_P, :])
             for r in range(PE_SPREAD_ROUNDS, ROUNDS):
@@ -144,8 +149,8 @@ def tile_cin_pa_t_kernel(tc, x, x1, w1, b1, w2, b2, out):
         sum_o1 = {}
         result = {}
 
-        def spread_x(r, copies):
-            for dl in range(D_ROUND):
+        def spread_x(r, copies, positions=range(D_ROUND)):
+            for dl in positions:
                 x_bank = spread.tile([P, PACK * P], F32, name="x_bank")
                 for cu in range(PACK):
                     word = (r * D_ROUND + dl) * PACK + cu
@@ -163,25 +168,23 @@ def tile_cin_pa_t_kernel(tc, x, x1, w1, b1, w2, b2, out):
 
         def sort_x1(r):
             s, d0 = r // ROUNDS_PER_TILE, (r % ROUNDS_PER_TILE) * D_ROUND
-            x1_by_d[r] = two.tile([P, ROWS], BF16, name="x1_by_d")
+            x1_by_d[r] = two.tile([P, ROWS * 2], BF16, name="x1_by_d")
             nc.scalar.copy(
-                out=x1_by_d[r].rearrange("p (d j) -> p d j", d=D_ROUND),
-                in_=x1_sb[s].rearrange("p (j d) -> p d j", d=D)[:, d0 : d0 + D_ROUND, :],
+                out=x1_by_d[r].rearrange("p (d j e) -> p d j e", d=D_ROUND, e=2),
+                in_=x1_sb[s]
+                .rearrange("p (j d) -> p d j", d=D)[:, d0 : d0 + D_ROUND, :]
+                .unsqueeze(3)
+                .to_broadcast([P, D_ROUND, FK, 2]),
             )
 
         def turn_x1(r):
-            x1_t[r] = bank.tile([P, 2 * ROWS], BF16, name="x1_t")
+            x1_t[r] = bank.tile([P, ROWS], F32, name="x1_t")
             for dl in range(D_ROUND):
                 nc.tensor.transpose(
-                    x1_t[r][:, dl * P : (dl + 1) * P], x1_by_d[r][:, dl * P : (dl + 1) * P], ident_b[:]
+                    x1_t[r][:, dl * P : (dl + 1) * P],
+                    x1_by_d[r][:].bitcast(F32)[:, dl * P : (dl + 1) * P],
+                    ident_f[:],
                 )
-
-        def double_x1(r):
-            x1_twice[r] = three.tile([P, ROWS * 2], BF16, name="x1_twice")
-            nc.scalar.copy(
-                out=x1_twice[r].rearrange("p (w e) -> p w e", e=2),
-                in_=x1_t[r][:, 0:ROWS].unsqueeze(2).to_broadcast([P, ROWS, 2]),
-            )
 
         def x_of_pass(r, c, row0, rows):
             first = (c * ROWS + row0) * PACK
@@ -216,7 +219,8 @@ def tile_cin_pa_t_kernel(tc, x, x1, w1, b1, w2, b2, out):
                 out=z_in[1, r][:, c * ROWS * PACK : (c + 1) * ROWS * PACK].rearrange(
                     "p (w u e) -> p w u e", u=2, e=2
                 ),
-                in0=x1_twice[r]
+                in0=x1_t[r][:]
+                .bitcast(BF16)
                 .rearrange("p (w e) -> p w e", e=2)
                 .unsqueeze(2)
                 .to_broadcast([P, ROWS, 2, 2]),
@@ -235,10 +239,19 @@ def tile_cin_pa_t_kernel(tc, x, x1, w1, b1, w2, b2, out):
             )
 
         def multiply2(r, c):
-            multiply2_vector(r, c, DVE_DS[0], 0, DVE_ROWS)
+            multiply2_vector(r, c, DVE_DS[0], 0, DVE_ROWS - GP_EXTRA)
+            first = (word_col(2, c, DVE_DS[0]) + DVE_ROWS - GP_EXTRA) * PACK
+            nc.gpsimd.tensor_tensor(
+                out=z_in[2, r][:, first : first + GP_EXTRA * PACK].rearrange("p (w t) -> p w t", t=PACK),
+                in0=o1_gp[r][:, GP_ROWS + P - GP_EXTRA : GP_ROWS + P].unsqueeze(2).to_broadcast([P, GP_EXTRA, PACK]),
+                in1=x_of_pass(r, c, DVE_DS[0] * P + DVE_ROWS - GP_EXTRA, GP_EXTRA),
+                op=MULT,
+            )
+
+        def multiply2_gpsimd(r, c):
             nc.gpsimd.tensor_tensor(
                 out=z2_of(r, c, GP_DS[0], GP_ROWS).rearrange("p (w t) -> p w t", t=PACK),
-                in0=o1_gp[r][:].unsqueeze(2).to_broadcast([P, GP_ROWS, PACK]),
+                in0=o1_gp[r][:, 0:GP_ROWS].unsqueeze(2).to_broadcast([P, GP_ROWS, PACK]),
                 in1=x_of_pass(r, c, GP_DS[0] * P, GP_ROWS),
                 op=MULT,
             )
@@ -251,9 +264,33 @@ def tile_cin_pa_t_kernel(tc, x, x1, w1, b1, w2, b2, out):
             )
 
         def layer1(r):
-            if r < ROUTED_ROUNDS:
-                o1_turned_ps[r] = spread.tile([P, PACK * P], F32, name="o1_turned_ps", tag="x_bank")
-            for n, dl in enumerate(ACT_DS if r < ROUTED_ROUNDS else ()):
+            def with_w1_stationary(target, col0, row0, rows):
+                for c in range(PASSES):
+                    nc.tensor.matmul_mx(
+                        out=target[:, col0 : col0 + rows],
+                        lhsT=w1_codes[:, c * S1 : (c + 1) * S1].bitcast(FP8X4),
+                        lhsT_scale=w1_scales[:, c * S1 : (c + 1) * S1],
+                        rhs=z_codes[1, r][:, c * ROWS + row0 : c * ROWS + row0 + rows].bitcast(FP8X4),
+                        rhs_scale=z_scales[1, r][:, c * ROWS + row0 : c * ROWS + row0 + rows],
+                        start=(c == 0),
+                        stop=(c == PASSES - 1),
+                    )
+
+            o1_apart = spread.tile([P, PACK * P], F32, name="o1_apart", tag="x_bank")
+            with_w1_stationary(o1_apart, 0, GP_DS[0] * P, GP_ROWS)
+            with_w1_stationary(o1_apart, GP_ROWS, DVE_DS[-1] * P, P)
+            o1_gp[r] = two.tile([P, GP_ROWS + P], F32, name="o1_gp")
+            nc.scalar.activation(
+                out=o1_gp[r][:], in_=o1_apart[:, 0 : GP_ROWS + P], func=IDENTITY, bias=b1_col[:, 0:1]
+            )
+            o1[r] = bank.tile([P, ROWS], F32, name="o1")
+            with_w1_stationary(o1[r], 0, DVE_DS[0] * P, DVE_ROWS)
+            if r >= ROUTED_ROUNDS:
+                for n, dl in enumerate(ACT_DS):
+                    with_w1_stationary(o1[r], DVE_ROWS + n * P, dl * P, P)
+                return
+            o1_turned_ps[r] = spread.tile([P, PACK * P], F32, name="o1_turned_ps", tag="x_bank")
+            for n, dl in enumerate(ACT_DS):
                 for c in range(PASSES):
                     block = slice(word_col(1, c, dl), word_col(1, c, dl) + P)
                     nc.tensor.matmul_mx(
@@ -265,26 +302,6 @@ def tile_cin_pa_t_kernel(tc, x, x1, w1, b1, w2, b2, out):
                         start=(c == 0),
                         stop=(c == PASSES - 1),
                     )
-            o1[r] = bank.tile([P, ROWS], F32, name="o1")
-            o1_apart = spread.tile([P, PACK * P], F32, name="o1_apart", tag="x_bank")
-            groups = [(o1[r], 0, DVE_DS[0] * P, DVE_ROWS), (o1_apart, 0, GP_DS[0] * P, GP_ROWS)]
-            if r >= ROUTED_ROUNDS:
-                groups.extend((o1[r], DVE_ROWS + n * P, dl * P, P) for n, dl in enumerate(ACT_DS))
-            for target, col0, row0, rows in groups:
-                for c in range(PASSES):
-                    nc.tensor.matmul_mx(
-                        out=target[:, col0 : col0 + rows],
-                        lhsT=w1_codes[:, c * S1 : (c + 1) * S1].bitcast(FP8X4),
-                        lhsT_scale=w1_scales[:, c * S1 : (c + 1) * S1],
-                        rhs=z_codes[1, r][:, c * ROWS + row0 : c * ROWS + row0 + rows].bitcast(FP8X4),
-                        rhs_scale=z_scales[1, r][:, c * ROWS + row0 : c * ROWS + row0 + rows],
-                        start=(c == 0),
-                        stop=(c == PASSES - 1),
-                    )
-            o1_gp[r] = two.tile([P, GP_ROWS], F32, name="o1_gp")
-            nc.scalar.activation(
-                out=o1_gp[r][:], in_=o1_apart[:, 0:GP_ROWS], func=IDENTITY, bias=b1_col[:, 0:1]
-            )
 
         def add_b1_turned(r):
             width = len(ACT_DS) * S1
@@ -418,18 +435,18 @@ def tile_cin_pa_t_kernel(tc, x, x1, w1, b1, w2, b2, out):
             regroup(nc.vector.tensor_copy, w1_grouped[:, part], w1_raw[:, part])
 
         sort_x1(0)
-        spread_x(0, [s_copy, v_copy, s_copy, v_copy])
-        turn_x1(0)
-        double_x1(0)
-        park_x()
         regroup_w1(0)
+        copies0 = [s_copy, v_copy, s_copy, v_copy]
+        spread_x(0, copies0, (0, 1))
         regroup_w1(1)
+        spread_x(0, copies0, (2,))
+        turn_x1(0)
+        spread_x(0, copies0, (3,))
+        turn_x()
         sort_x1(1)
         spread_x(1, [s_copy] * D_ROUND)
-        turn_x1(1)
-        double_x1(1)
 
-        b1_t = bank.tile([P, 2 * ROWS], BF16, name="b1_t", tag="x1_t")
+        b1_t = spread.tile([P, 2 * PACK * P], BF16, name="b1_t", tag="x_bank")
         nc.tensor.transpose(b1_t[:, 0:P], b1_rows[:], ident_b[:])
         b1_col = keep.tile([P, 1], F32, name="b1_col")
         nc.scalar.copy(out=b1_col[:], in_=b1_t[:, 0:1])
@@ -438,9 +455,8 @@ def tile_cin_pa_t_kernel(tc, x, x1, w1, b1, w2, b2, out):
         multiply1(0, 0)
         quantise_weights(w1_codes[:], w1_scales[:], w1_grouped[:])
         multiply1(0, 1)
-        sort_x1(2)
-        turn_x1(2)
-        double_x1(2)
+        turn_x1(1)
+        park_x()
         quantise(1, 0, 0, PASSES * ROWS)
         layer1(0)
         pooled_o1(0)
@@ -453,12 +469,10 @@ def tile_cin_pa_t_kernel(tc, x, x1, w1, b1, w2, b2, out):
             routed = range(len(ACT_DS) if r < ROUTED_ROUNDS else 0)
             for n in routed:
                 turn_z2(r, n)
-            if r + 3 < ROUNDS:
-                turn_x1(r + 3)
+            if r + 2 < ROUNDS:
+                turn_x1(r + 2)
             for n in routed:
                 collect_z2(r, n)
-            if r + 3 < ROUNDS:
-                double_x1(r + 3)
 
         def quantise_scalars(r, last=False):
             quantise(2, r, act_words0, len(ACT_DS) * ACT_WORDS)
@@ -468,20 +482,22 @@ def tile_cin_pa_t_kernel(tc, x, x1, w1, b1, w2, b2, out):
             s, q = r // ROUNDS_PER_TILE, r % ROUNDS_PER_TILE
             ahead = r + 1 < ROUNDS
             new_z(2, r)
+            if r > 0:
+                quantise_scalars(r - 1, last=(q == 0))
             if ahead:
                 new_z(1, r + 1)
                 multiply1(r + 1, 0)
-            if r > 0:
-                quantise_scalars(r - 1, last=(q == 0))
-            if r + 3 < ROUNDS:
-                sort_x1(r + 3)
-            if ahead:
-                multiply1(r + 1, 1)
             if r < ROUTED_ROUNDS:
                 add_b1_turned(r)
                 multiply2_scalar(r)
+            if r + 2 < ROUNDS:
+                sort_x1(r + 2)
+            if ahead:
+                multiply1(r + 1, 1)
             for c in range(PASSES):
                 multiply2(r, c)
+            for c in range(PASSES):
+                multiply2_gpsimd(r, c)
             if r >= ROUTED_ROUNDS:
                 for n, dl in enumerate(ACT_DS):
                     for c in range(PASSES):

@@ -27,6 +27,7 @@ DVE_ROWS, GP_ROWS = len(DVE_DS) * P, len(GP_DS) * P
 DVE_WORDS = PASSES * DVE_ROWS
 ACT_WORDS = PASSES * P
 GP_WORDS = PASSES * GP_ROWS
+WARM_UP = 3
 GP_EXTRA = 64
 ROUTED_ROUNDS = ROUNDS - 1
 N2 = 512
@@ -48,6 +49,12 @@ def tile_cin_pa_t_kernel(tc, x, x1, w1, b1, w2, b2, out):
         tc.psum_pool(name="bank", bufs=1) as bank,
         tc.psum_pool(name="spread", bufs=3) as spread,
     ):
+        warm = keep.tile([P, N2], BF16, name="warm")
+        nc.vector.memset(warm[:], 0.0)
+        warm_ps = spread.tile([P, PACK * P], F32, name="warm_ps", tag="x_bank")
+        for n in range(WARM_UP):
+            nc.tensor.matmul(out=warm_ps[:], lhsT=warm[:, 0:P], rhs=warm[:], start=True, stop=True)
+
         x_sb = keep.tile([P, SAMPLE_TILES * F0 * D], BF16, name="x_sb")
         nc.sync.dma_start(
             out=x_sb.rearrange("p (s f) -> p s f", s=SAMPLE_TILES),

@@ -247,19 +247,39 @@ def tile_cin_pa_t_kernel(tc, x, x1, w1, b1, w2, b2, out):
 
         def multiply2(r, c):
             multiply2_vector(r, c, DVE_DS[0], 0, DVE_ROWS - GP_EXTRA)
-            first = (word_col(2, c, DVE_DS[0]) + DVE_ROWS - GP_EXTRA) * PACK
+
+        def multiply2_gpsimd(r, z_word0, z_step, o1_col0, x_row0, rows):
             nc.gpsimd.tensor_tensor(
-                out=z_in[2, r][:, first : first + GP_EXTRA * PACK].rearrange("p (w t) -> p w t", t=PACK),
-                in0=o1_gp[r][:, GP_ROWS + P - GP_EXTRA : GP_ROWS + P].unsqueeze(2).to_broadcast([P, GP_EXTRA, PACK]),
-                in1=x_of_pass(r, c, DVE_DS[0] * P + DVE_ROWS - GP_EXTRA, GP_EXTRA),
+                out=z_in[2, r][:, z_word0 * PACK : (z_word0 + PASSES * z_step) * PACK].rearrange(
+                    "p (c w t) -> p c w t", c=PASSES, t=PACK
+                )[:, :, 0:rows, :],
+                in0=o1_gp[r][:, o1_col0 : o1_col0 + rows]
+                .unsqueeze(1)
+                .unsqueeze(3)
+                .to_broadcast([P, PASSES, rows, PACK]),
+                in1=x_all[r][:].bitcast(BF16).rearrange("p (c w t) -> p c w t", c=PASSES, t=PACK)[
+                    :, :, x_row0 : x_row0 + rows, :
+                ],
                 op=MULT,
             )
 
-        def multiply2_gpsimd(r, c):
+        def multiply2_gpsimd_all(r):
+            extra0 = DVE_ROWS - GP_EXTRA
+            multiply2_gpsimd_extra(r, extra0)
+            multiply2_gpsimd(r, word_col(2, 0, GP_DS[0]), GP_ROWS, 0, GP_DS[0] * P, GP_ROWS)
+
+        def multiply2_gpsimd_extra(r, extra0):
             nc.gpsimd.tensor_tensor(
-                out=z2_of(r, c, GP_DS[0], GP_ROWS).rearrange("p (w t) -> p w t", t=PACK),
-                in0=o1_gp[r][:, 0:GP_ROWS].unsqueeze(2).to_broadcast([P, GP_ROWS, PACK]),
-                in1=x_of_pass(r, c, GP_DS[0] * P, GP_ROWS),
+                out=z_in[2, r][:, 0 : DVE_WORDS * PACK].rearrange("p (c w t) -> p c w t", c=PASSES, t=PACK)[
+                    :, :, extra0:DVE_ROWS, :
+                ],
+                in0=o1_gp[r][:, GP_ROWS + P - GP_EXTRA : GP_ROWS + P]
+                .unsqueeze(1)
+                .unsqueeze(3)
+                .to_broadcast([P, PASSES, GP_EXTRA, PACK]),
+                in1=x_all[r][:].bitcast(BF16).rearrange("p (c w t) -> p c w t", c=PASSES, t=PACK)[
+                    :, :, DVE_DS[0] * P + extra0 : DVE_DS[0] * P + DVE_ROWS, :
+                ],
                 op=MULT,
             )
 
@@ -503,8 +523,7 @@ def tile_cin_pa_t_kernel(tc, x, x1, w1, b1, w2, b2, out):
                 multiply1(r + 1, 1)
             for c in range(PASSES):
                 multiply2(r, c)
-            for c in range(PASSES):
-                multiply2_gpsimd(r, c)
+            multiply2_gpsimd_all(r)
             if r >= ROUTED_ROUNDS:
                 for n, dl in enumerate(ACT_DS):
                     for c in range(PASSES):

@@ -21,15 +21,17 @@ ROUNDS_PER_TILE = D // D_ROUND
 ROUNDS = SAMPLE_TILES * ROUNDS_PER_TILE
 ROWS = D_ROUND * P
 DVE_DS = (0, 1)
-ACT_DS = (2,)
-GP_DS = (3,)
+GP_DS = (2,)
+ACT_DS = (3,)
 DVE_ROWS, GP_ROWS = len(DVE_DS) * P, len(GP_DS) * P
 DVE_WORDS = PASSES * DVE_ROWS
 ACT_WORDS = PASSES * P
 GP_WORDS = PASSES * GP_ROWS
 WARM_UP = 3
-GP_EXTRA = 64
-ROUTED_ROUNDS = ROUNDS - 1
+GP_EXTRA = [64] * ROUNDS
+GP_EXTRA[1] = 128
+GP_EXTRA[ROUNDS - 1] = 0
+ROUTED = range(1, ROUNDS - 1)
 N2 = 512
 HALVES = S2 // N2
 HALF_P = P // 2
@@ -46,12 +48,12 @@ def tile_cin_pa_t_kernel(tc, x, x1, w1, b1, w2, b2, out):
         tc.tile_pool(name="raw", bufs=4) as raw_pool,
         tc.tile_pool(name="two", bufs=2) as two,
         tc.tile_pool(name="three", bufs=3) as three,
+        tc.tile_pool(name="keep_gp", bufs=1) as keep_gp,
         tc.psum_pool(name="bank", bufs=1) as bank,
-        tc.psum_pool(name="spread", bufs=3) as spread,
     ):
         warm = keep.tile([P, N2], BF16, name="warm")
         nc.vector.memset(warm[:], 0.0)
-        warm_ps = spread.tile([P, PACK * P], F32, name="warm_ps", tag="x_bank")
+        warm_ps = bank.tile([P, N2], F32, name="warm_ps", tag="o1")
         for n in range(WARM_UP):
             nc.tensor.matmul(out=warm_ps[:], lhsT=warm[:, 0:P], rhs=warm[:], start=True, stop=True)
 
@@ -83,9 +85,7 @@ def tile_cin_pa_t_kernel(tc, x, x1, w1, b1, w2, b2, out):
 
         load_w2(0)
         load_w2(1)
-        nc.sync.dma_start(out=x1_sb[1][:], in_=x1[P : 2 * P].rearrange("b j d -> b (j d)"))
         b2_rows = keep.tile([P, S2], BF16, name="b2_rows")
-        nc.sync.dma_start(out=b2_rows[:], in_=b2.partition_broadcast(P))
 
         ident_f = keep.tile([P, P], F32, name="ident_f")
         make_identity(nc, ident_f[:])
@@ -112,8 +112,9 @@ def tile_cin_pa_t_kernel(tc, x, x1, w1, b1, w2, b2, out):
 
         x_turned_ps = {}
 
-        def turn_x():
-            x_blocks = keep.tile([P, 3 * HALF_P], F32, name="x_blocks")
+        x_blocks = keep.tile([P, 3 * HALF_P], F32, name="x_blocks")
+
+        def sort_x():
             for block, u in enumerate((0, 1, 0)):
                 nc.vector.tensor_copy(
                     out=x_blocks[:, block * HALF_P : (block + 1) * HALF_P].rearrange(
@@ -121,7 +122,9 @@ def tile_cin_pa_t_kernel(tc, x, x1, w1, b1, w2, b2, out):
                     ),
                     in_=x_words.rearrange("p (a dl c u) -> p u a c dl", dl=D_ROUND, c=PASSES, u=2)[:, u],
                 )
-            x_turned_ps[0] = spread.tile([P, PACK * P], F32, name="x_turned_ps", tag="x_bank")
+
+        def turn_x():
+            x_turned_ps[0] = bank.tile([P, N2], F32, name="x_turned_ps", tag="o1_turned")
             for u in range(2):
                 nc.tensor.transpose(
                     x_turned_ps[0][:, u * P : (u + 1) * P], x_blocks[:, u * HALF_P : u * HALF_P + P], ident_f[:]
@@ -129,16 +132,19 @@ def tile_cin_pa_t_kernel(tc, x, x1, w1, b1, w2, b2, out):
 
         def park_x():
             x_turned = keep.tile([P, 2 * P], F32, name="x_turned")
-            nc.vector.tensor_copy(
+            nc.scalar.copy(
                 out=x_turned.rearrange("p (b u) -> p b u", u=2),
                 in_=x_turned_ps[0][:, 0 : 2 * P].rearrange("p (u b) -> p b u", u=2),
             )
-            nc.sync.dma_start(out=parked.rearrange("(p w) -> p w", w=2 * P), in_=x_turned[0:HALF_P, :])
-            for r in range(PE_SPREAD_ROUNDS, ROUNDS):
+            nc.scalar.dma_start(out=parked.rearrange("(p w) -> p w", w=2 * P), in_=x_turned[0:HALF_P, :])
+            load_x_all(1)
+            nc.sync.dma_start(out=x1_sb[1][:], in_=x1[P : 2 * P].rearrange("b j d -> b (j d)"))
+            load_x_all(2)
+            nc.sync.dma_start(out=b2_rows[:], in_=b2.partition_broadcast(P))
+            for r in range(3, ROUNDS):
                 load_x_all(r)
 
         x_f32 = keep.tile([P, SAMPLE_TILES * F0 * D], F32, name="x_f32")
-        nc.gpsimd.tensor_copy(out=x_f32[:], in_=x_sb[:])
 
         x1_by_d = {}
         x1_t = {}
@@ -156,9 +162,11 @@ def tile_cin_pa_t_kernel(tc, x, x1, w1, b1, w2, b2, out):
         sum_o1 = {}
         result = {}
 
+        x_banks = ("z2_back", "sum_2", "sum_0", "sum_1")
+
         def spread_x(r, copies, positions=range(D_ROUND)):
             for dl in positions:
-                x_bank = spread.tile([P, PACK * P], F32, name="x_bank")
+                x_bank = bank.tile([P, N2], F32, name="x_bank%d" % dl, tag=x_banks[dl])
                 for cu in range(PACK):
                     word = (r * D_ROUND + dl) * PACK + cu
                     nc.tensor.transpose(
@@ -198,40 +206,44 @@ def tile_cin_pa_t_kernel(tc, x, x1, w1, b1, w2, b2, out):
             return x_all[r][:].bitcast(BF16)[:, first : first + rows * PACK].rearrange("p (w t) -> p w t", t=PACK)
 
         def new_z(layer, r):
-            z_in[layer, r] = two.tile(
-                [P, PASSES * ROWS * PACK], BF16, name="z%d_in" % layer, align_bytes=64
-            )
-            z_codes[layer, r] = three.tile(
-                [P, PASSES * ROWS], U32, name="z%d_codes" % layer, align_bytes=64
-            )
-            z_scales[layer, r] = three.tile(
-                [P, PASSES * ROWS], U8, name="z%d_scales" % layer, align_bytes=64
-            )
+            words = PASSES * ROWS if layer == 1 else DVE_WORDS + ACT_WORDS
+            z_in[layer, r] = two.tile([P, words * PACK], BF16, name="z%d_in" % layer, align_bytes=64)
+            z_codes[layer, r] = three.tile([P, words], U32, name="z%d_codes" % layer, align_bytes=64)
+            z_scales[layer, r] = three.tile([P, words], U8, name="z%d_scales" % layer, align_bytes=64)
 
-        def word_col(layer, c, dl):
+        def new_z_gp(r):
+            z_in["gp", r] = keep_gp.tile([P, GP_WORDS * PACK], BF16, name="zg_in", align_bytes=64)
+            z_codes["gp", r] = three.tile([P, GP_WORDS], U32, name="zg_codes", align_bytes=64)
+            z_scales["gp", r] = three.tile([P, GP_WORDS], U8, name="zg_scales", align_bytes=64)
+
+        def word_col(layer, c, dl, r=-1):
+            if layer == 1 and r == 0:
+                return ((dl // 2 * PASSES + c) * 2 + dl % 2) * P
             if layer == 1:
                 return (c * D_ROUND + dl) * P
             if dl in DVE_DS:
                 return c * DVE_ROWS + DVE_DS.index(dl) * P
             if dl in ACT_DS:
                 return DVE_WORDS + ACT_DS.index(dl) * ACT_WORDS + c * P
-            return DVE_WORDS + len(ACT_DS) * ACT_WORDS + c * GP_ROWS + GP_DS.index(dl) * P
+            return c * GP_ROWS + GP_DS.index(dl) * P
+
+        def z2_key(r, dl):
+            return ("gp" if dl in GP_DS else 2, r)
 
         def z2_of(r, c, dl, rows):
             first = word_col(2, c, dl) * PACK
-            return z_in[2, r][:, first : first + rows * PACK]
+            return z_in[z2_key(r, dl)][:, first : first + rows * PACK]
 
-        def multiply1(r, c):
+        def multiply1(r, c, dl0=0, dls=D_ROUND):
+            first, rows = word_col(1, c, dl0, r) * PACK, dls * P
             nc.vector.tensor_tensor(
-                out=z_in[1, r][:, c * ROWS * PACK : (c + 1) * ROWS * PACK].rearrange(
-                    "p (w u e) -> p w u e", u=2, e=2
-                ),
-                in0=x1_t[r][:]
+                out=z_in[1, r][:, first : first + rows * PACK].rearrange("p (w u e) -> p w u e", u=2, e=2),
+                in0=x1_t[r][:, dl0 * P : dl0 * P + rows]
                 .bitcast(BF16)
                 .rearrange("p (w e) -> p w e", e=2)
                 .unsqueeze(2)
-                .to_broadcast([P, ROWS, 2, 2]),
-                in1=x_of_pass(r, c, 0, ROWS).rearrange("p w (u e) -> p w u e", e=2),
+                .to_broadcast([P, rows, 2, 2]),
+                in1=x_of_pass(r, c, dl0 * P, rows).rearrange("p w (u e) -> p w u e", e=2),
                 op=MULT,
             )
 
@@ -246,13 +258,11 @@ def tile_cin_pa_t_kernel(tc, x, x1, w1, b1, w2, b2, out):
             )
 
         def multiply2(r, c):
-            multiply2_vector(r, c, DVE_DS[0], 0, DVE_ROWS - GP_EXTRA)
+            multiply2_vector(r, c, DVE_DS[0], 0, DVE_ROWS - GP_EXTRA[r])
 
-        def multiply2_gpsimd(r, z_word0, z_step, o1_col0, x_row0, rows):
+        def multiply2_gpsimd(r, out_words, o1_col0, x_row0, rows):
             nc.gpsimd.tensor_tensor(
-                out=z_in[2, r][:, z_word0 * PACK : (z_word0 + PASSES * z_step) * PACK].rearrange(
-                    "p (c w t) -> p c w t", c=PASSES, t=PACK
-                )[:, :, 0:rows, :],
+                out=out_words,
                 in0=o1_gp[r][:, o1_col0 : o1_col0 + rows]
                 .unsqueeze(1)
                 .unsqueeze(3)
@@ -263,25 +273,15 @@ def tile_cin_pa_t_kernel(tc, x, x1, w1, b1, w2, b2, out):
                 op=MULT,
             )
 
-        def multiply2_gpsimd_all(r):
-            extra0 = DVE_ROWS - GP_EXTRA
-            multiply2_gpsimd_extra(r, extra0)
-            multiply2_gpsimd(r, word_col(2, 0, GP_DS[0]), GP_ROWS, 0, GP_DS[0] * P, GP_ROWS)
+        def multiply2_gpsimd_extra(r):
+            row0 = DVE_ROWS - GP_EXTRA[r]
+            words = z_in[2, r][:, 0 : DVE_WORDS * PACK].rearrange("p (c w t) -> p c w t", c=PASSES, t=PACK)
+            multiply2_gpsimd(r, words[:, :, row0:DVE_ROWS, :], 0, row0, GP_EXTRA[r])
 
-        def multiply2_gpsimd_extra(r, extra0):
-            nc.gpsimd.tensor_tensor(
-                out=z_in[2, r][:, 0 : DVE_WORDS * PACK].rearrange("p (c w t) -> p c w t", c=PASSES, t=PACK)[
-                    :, :, extra0:DVE_ROWS, :
-                ],
-                in0=o1_gp[r][:, GP_ROWS + P - GP_EXTRA : GP_ROWS + P]
-                .unsqueeze(1)
-                .unsqueeze(3)
-                .to_broadcast([P, PASSES, GP_EXTRA, PACK]),
-                in1=x_all[r][:].bitcast(BF16).rearrange("p (c w t) -> p c w t", c=PASSES, t=PACK)[
-                    :, :, DVE_DS[0] * P + extra0 : DVE_DS[0] * P + DVE_ROWS, :
-                ],
-                op=MULT,
-            )
+        def multiply2_gpsimd_own(r):
+            new_z_gp(r)
+            words = z_in["gp", r].rearrange("p (c w t) -> p c w t", c=PASSES, t=PACK)
+            multiply2_gpsimd(r, words, GP_EXTRA[r], GP_DS[0] * P, GP_ROWS)
 
         def quantise(layer, r, word0, words):
             nc.vector.quantize_mx(
@@ -290,45 +290,60 @@ def tile_cin_pa_t_kernel(tc, x, x1, w1, b1, w2, b2, out):
                 in_=z_in[layer, r][:, word0 * PACK : (word0 + words) * PACK],
             )
 
-        def layer1(r):
-            def with_w1_stationary(target, col0, row0, rows):
+        def layer1(r, half=None):
+            def with_w1_stationary(dl0, dls):
                 for c in range(PASSES):
+                    first = word_col(1, c, dl0, r)
                     nc.tensor.matmul_mx(
-                        out=target[:, col0 : col0 + rows],
+                        out=o1[r][:, dl0 * P : (dl0 + dls) * P],
                         lhsT=w1_codes[:, c * S1 : (c + 1) * S1].bitcast(FP8X4),
                         lhsT_scale=w1_scales[:, c * S1 : (c + 1) * S1],
-                        rhs=z_codes[1, r][:, c * ROWS + row0 : c * ROWS + row0 + rows].bitcast(FP8X4),
-                        rhs_scale=z_scales[1, r][:, c * ROWS + row0 : c * ROWS + row0 + rows],
+                        rhs=z_codes[1, r][:, first : first + dls * P].bitcast(FP8X4),
+                        rhs_scale=z_scales[1, r][:, first : first + dls * P],
                         start=(c == 0),
                         stop=(c == PASSES - 1),
                     )
 
-            o1_apart = spread.tile([P, PACK * P], F32, name="o1_apart", tag="x_bank")
-            with_w1_stationary(o1_apart, 0, GP_DS[0] * P, GP_ROWS)
-            with_w1_stationary(o1_apart, GP_ROWS, DVE_DS[-1] * P, P)
-            o1_gp[r] = two.tile([P, GP_ROWS + P], F32, name="o1_gp")
-            nc.scalar.activation(
-                out=o1_gp[r][:], in_=o1_apart[:, 0 : GP_ROWS + P], func=IDENTITY, bias=b1_col[:, 0:1]
-            )
-            o1[r] = bank.tile([P, ROWS], F32, name="o1")
-            with_w1_stationary(o1[r], 0, DVE_DS[0] * P, DVE_ROWS)
-            if r >= ROUTED_ROUNDS:
+            def turned_rows():
+                o1_turned_ps[r] = bank.tile([P, N2], F32, name="o1_turned")
                 for n, dl in enumerate(ACT_DS):
-                    with_w1_stationary(o1[r], DVE_ROWS + n * P, dl * P, P)
+                    for c in range(PASSES):
+                        block = slice(word_col(1, c, dl, r), word_col(1, c, dl, r) + P)
+                        nc.tensor.matmul_mx(
+                            out=o1_turned_ps[r][:, n * S1 : (n + 1) * S1],
+                            lhsT=z_codes[1, r][:, block].bitcast(FP8X4),
+                            lhsT_scale=z_scales[1, r][:, block],
+                            rhs=w1_codes[:, c * S1 : (c + 1) * S1].bitcast(FP8X4),
+                            rhs_scale=w1_scales[:, c * S1 : (c + 1) * S1],
+                            start=(c == 0),
+                            stop=(c == PASSES - 1),
+                        )
+
+            def copy_for_gpsimd(col0, cols):
+                to = col0 - (DVE_ROWS - GP_EXTRA[r])
+                nc.scalar.activation(
+                    out=o1_gp[r][:, to : to + cols],
+                    in_=o1[r][:, col0 : col0 + cols],
+                    func=IDENTITY,
+                    bias=b1_col[:, 0:1],
+                )
+
+            if r in ROUTED:
+                turned_rows()
+            if half in (None, 0):
+                o1[r] = bank.tile([P, ROWS], F32, name="o1")
+                o1_gp[r] = two.tile([P, P + GP_ROWS], F32, name="o1_gp")
+                with_w1_stationary(DVE_DS[0], len(DVE_DS))
+            if half == 0:
+                copy_for_gpsimd(DVE_ROWS - GP_EXTRA[r], GP_EXTRA[r])
                 return
-            o1_turned_ps[r] = spread.tile([P, PACK * P], F32, name="o1_turned_ps", tag="x_bank")
-            for n, dl in enumerate(ACT_DS):
-                for c in range(PASSES):
-                    block = slice(word_col(1, c, dl), word_col(1, c, dl) + P)
-                    nc.tensor.matmul_mx(
-                        out=o1_turned_ps[r][:, n * S1 : (n + 1) * S1],
-                        lhsT=z_codes[1, r][:, block].bitcast(FP8X4),
-                        lhsT_scale=z_scales[1, r][:, block],
-                        rhs=w1_codes[:, c * S1 : (c + 1) * S1].bitcast(FP8X4),
-                        rhs_scale=w1_scales[:, c * S1 : (c + 1) * S1],
-                        start=(c == 0),
-                        stop=(c == PASSES - 1),
-                    )
+            with_w1_stationary(GP_DS[0], 1)
+            if not (r in ROUTED):
+                with_w1_stationary(ACT_DS[0], 1)
+            if half == 1:
+                copy_for_gpsimd(DVE_ROWS, GP_ROWS)
+            else:
+                copy_for_gpsimd(DVE_ROWS - GP_EXTRA[r], GP_EXTRA[r] + GP_ROWS)
 
         def add_b1_turned(r):
             width = len(ACT_DS) * S1
@@ -356,7 +371,7 @@ def tile_cin_pa_t_kernel(tc, x, x1, w1, b1, w2, b2, out):
                     )
 
         def turn_z2(r, n):
-            z2_back[r, n] = spread.tile([P, PACK * P], F32, name="z2_back", tag="x_bank")
+            z2_back[r, n] = bank.tile([P, N2], F32, name="z2_back")
             for g in range(F0 // 2):
                 word0 = (n * (F0 // 2) + g) * P
                 nc.tensor.transpose(
@@ -373,18 +388,19 @@ def tile_cin_pa_t_kernel(tc, x, x1, w1, b1, w2, b2, out):
                 in_=z2_back[r, n].rearrange("p (c u b) -> p c b u", c=PASSES, u=2),
             )
 
-        def pooled(r, blocks, first=False, last=False):
+        def pooled(r, blocks, first=False, last=False, halves=range(HALVES)):
             s = r // ROUNDS_PER_TILE
-            if first:
-                sums[s] = [bank.tile([P, N2], F32, name="sum_o2_%d" % h) for h in range(HALVES)]
-            for h in range(HALVES):
+            for h in halves:
+                if first:
+                    sums[s, h] = bank.tile([P, N2], F32, name="sum_o2_%d" % h, tag="sum_%d" % ((2 * s + h) % 3))
                 for n, (c, dl) in enumerate(blocks):
+                    key = z2_key(r, dl)
                     block = slice(word_col(2, c, dl), word_col(2, c, dl) + P)
                     w_cols = slice(c * S2 + h * N2, c * S2 + (h + 1) * N2)
                     nc.tensor.matmul_mx(
-                        out=sums[s][h][:],
-                        lhsT=z_codes[2, r][:, block].bitcast(FP8X4),
-                        lhsT_scale=z_scales[2, r][:, block],
+                        out=sums[s, h][:],
+                        lhsT=z_codes[key][:, block].bitcast(FP8X4),
+                        lhsT_scale=z_scales[key][:, block],
                         rhs=w2_codes[:, w_cols].bitcast(FP8X4),
                         rhs_scale=w2_scales[:, w_cols],
                         start=(first and n == 0),
@@ -397,7 +413,7 @@ def tile_cin_pa_t_kernel(tc, x, x1, w1, b1, w2, b2, out):
                 sum_o1[s] = bank.tile([P, N2], F32, name="sum_o1")
             for c in range(PASSES):
                 for dl in range(D_ROUND):
-                    block = slice(word_col(1, c, dl), word_col(1, c, dl) + P)
+                    block = slice(word_col(1, c, dl, r), word_col(1, c, dl, r) + P)
                     nc.tensor.matmul_mx(
                         out=sum_o1[s][:, 0:S1],
                         lhsT=z_codes[1, r][:, block].bitcast(FP8X4),
@@ -425,7 +441,7 @@ def tile_cin_pa_t_kernel(tc, x, x1, w1, b1, w2, b2, out):
             finish(s, 0, S1, b1_rows[:], sum_o1[s][:, 0:S1])
 
         def finish_o2(s, h):
-            finish(s, S1 + h * N2, N2, b2_rows[:, h * N2 : (h + 1) * N2], sums[s][h][:])
+            finish(s, S1 + h * N2, N2, b2_rows[:, h * N2 : (h + 1) * N2], sums[s, h][:])
 
         def regroup(copy, dst, src):
             copy(
@@ -439,7 +455,10 @@ def tile_cin_pa_t_kernel(tc, x, x1, w1, b1, w2, b2, out):
         w2_jobs = {}
 
         def regroup_w2(copy, c, h):
-            w2_grouped = raw_pool.tile([P, N2 * PACK], BF16, name="w2_grouped", align_bytes=64)
+            if (c, h) == (1, 0):
+                w2_grouped = keep_gp.tile([P, N2 * PACK], BF16, name="w2_last", tag="zg_in", align_bytes=64)
+            else:
+                w2_grouped = raw_pool.tile([P, N2 * PACK], BF16, name="w2_grouped", align_bytes=64)
             regroup(copy, w2_grouped[:], w2_raw[c, h][:])
             cols = slice(c * S2 + h * N2, c * S2 + (h + 1) * N2)
             w2_jobs[c, h] = (w2_codes[:, cols], w2_scales[:, cols], w2_grouped[:])
@@ -455,100 +474,147 @@ def tile_cin_pa_t_kernel(tc, x, x1, w1, b1, w2, b2, out):
         gp_blocks = [(c, dl) for c in range(PASSES) for dl in GP_DS]
         per_pass = len(DVE_DS)
         act_words0 = DVE_WORDS
-        gp_words0 = DVE_WORDS + len(ACT_DS) * ACT_WORDS
 
         def regroup_w1(c):
             part = slice(c * S1 * PACK, (c + 1) * S1 * PACK)
             regroup(nc.vector.tensor_copy, w1_grouped[:, part], w1_raw[:, part])
 
-        sort_x1(0)
-        regroup_w1(0)
-        copies0 = [s_copy, v_copy, s_copy, v_copy]
-        spread_x(0, copies0, (0, 1))
-        regroup_w1(1)
-        spread_x(0, copies0, (2,))
-        turn_x1(0)
-        spread_x(0, copies0, (3,))
-        turn_x()
-        sort_x1(1)
-        spread_x(1, [s_copy] * D_ROUND)
-
-        b1_t = spread.tile([P, 2 * PACK * P], BF16, name="b1_t", tag="x_bank")
-        nc.tensor.transpose(b1_t[:, 0:P], b1_rows[:], ident_b[:])
-        b1_col = keep.tile([P, 1], F32, name="b1_col")
-        nc.scalar.copy(out=b1_col[:], in_=b1_t[:, 0:1])
-
-        new_z(1, 0)
-        multiply1(0, 0)
-        quantise_weights(w1_codes[:], w1_scales[:], w1_grouped[:])
-        multiply1(0, 1)
-        turn_x1(1)
-        park_x()
-        quantise(1, 0, 0, PASSES * ROWS)
-        layer1(0)
-        pooled_o1(0)
-        for h in range(HALVES):
-            regroup_w2(nc.scalar.copy, 1, h)
-        for h in range(HALVES):
-            regroup_w2(nc.vector.tensor_copy, 0, h)
-
         def transposes(r):
-            routed = range(len(ACT_DS) if r < ROUTED_ROUNDS else 0)
-            for n in routed:
+            for n in range(len(ACT_DS) if (r in ROUTED) else 0):
                 turn_z2(r, n)
             if r + 2 < ROUNDS:
                 turn_x1(r + 2)
-            for n in routed:
+            for n in range(len(ACT_DS) if (r in ROUTED) else 0):
                 collect_z2(r, n)
 
-        def quantise_scalars(r, last=False):
-            quantise(2, r, act_words0, len(ACT_DS) * ACT_WORDS)
-            pooled(r, act_blocks, last=last)
+        def multiply2_act_d(r):
+            if (r in ROUTED):
+                add_b1_turned(r)
+                multiply2_scalar(r)
 
-        for r in range(ROUNDS):
+        def multiply2_act_d_vector(r):
+            if not (r in ROUTED):
+                for n, dl in enumerate(ACT_DS):
+                    for c in range(PASSES):
+                        multiply2_vector(r, c, dl, dl * P, P)
+
+        def quantise_act_d(r):
+            quantise(2, r, act_words0, len(ACT_DS) * ACT_WORDS)
+
+        sort_x()
+        sort_x1(0)
+        copies0 = [s_copy, v_copy, s_copy, s_copy]
+        regroup_w1(0)
+        spread_x(0, copies0, (0, 1, 2))
+        turn_x1(0)
+        spread_x(0, copies0, (3,))
+        turn_x()
+        new_z(1, 0)
+        new_z(2, 0)
+        for c in range(PASSES):
+            multiply1(0, c, 0, 2)
+        regroup_w1(1)
+        quantise_weights(w1_codes[:], w1_scales[:], w1_grouped[:])
+        park_x()
+        regroup_w2(s_copy, 0, 0)
+        b1_t = bank.tile([P, 2 * N2], BF16, name="b1_t", tag="z2_back")
+        nc.tensor.transpose(b1_t[:, 0:P], b1_rows[:], ident_b[:])
+        b1_col = keep.tile([P, 1], F32, name="b1_col")
+        nc.scalar.copy(out=b1_col[:], in_=b1_t[:, 0:1])
+        regroup_w2(s_copy, 0, 1)
+        quantise(1, 0, 0, ROWS)
+        layer1(0, 0)
+        for c in range(PASSES):
+            multiply1(0, c, 2, 2)
+        quantise_weights(*w2_jobs[0, 0])
+        quantise(1, 0, ROWS, ROWS)
+        layer1(0, 1)
+        pooled_o1(0)
+        sort_x1(1)
+        turn_x1(1)
+        for c in range(PASSES):
+            multiply2(0, c)
+        multiply2_gpsimd_extra(0)
+        for h in range(HALVES):
+            regroup_w2(s_copy, 1, h)
+        quantise_weights(*w2_jobs[0, 1])
+        quantise(2, 0, 0, DVE_WORDS)
+        pooled(0, dve_blocks[0:per_pass], first=True)
+        new_z(1, 1)
+        multiply1(1, 0)
+        for h in range(HALVES):
+            quantise_weights(*w2_jobs[1, h])
+        pooled(0, dve_blocks[per_pass:])
+        multiply2_gpsimd_own(0)
+        multiply1(1, 1)
+        multiply2_act_d_vector(0)
+        nc.scalar.copy(out=x_f32[:], in_=x_sb[:])
+        sort_x1(2)
+        transposes(0)
+        quantise(1, 1, 0, PASSES * ROWS)
+        layer1(1)
+        pooled_o1(1)
+        quantise_act_d(0)
+        pooled(0, act_blocks)
+
+        late = []
+        for r in range(1, ROUNDS):
             s, q = r // ROUNDS_PER_TILE, r % ROUNDS_PER_TILE
             ahead = r + 1 < ROUNDS
             new_z(2, r)
-            if r > 0:
-                quantise_scalars(r - 1, last=(q == 0))
             if ahead:
                 new_z(1, r + 1)
                 multiply1(r + 1, 0)
-            if r < ROUTED_ROUNDS:
-                add_b1_turned(r)
-                multiply2_scalar(r)
+            multiply2_act_d(r)
             if r + 2 < ROUNDS:
                 sort_x1(r + 2)
             if ahead:
                 multiply1(r + 1, 1)
+            if q == 1 and s > 0:
+                finish_o2(s - 1, 0)
+                pooled(r - 1, dve_blocks + act_blocks, first=True, halves=(1,))
+                finish_o2(s - 1, 1)
+            if r > 1:
+                multiply2_gpsimd_own(r - 1)
+            if ahead:
+                multiply2_gpsimd_extra(r)
             for c in range(PASSES):
                 multiply2(r, c)
-            multiply2_gpsimd_all(r)
-            if r >= ROUTED_ROUNDS:
-                for n, dl in enumerate(ACT_DS):
-                    for c in range(PASSES):
-                        multiply2_vector(r, c, dl, DVE_ROWS + n * P, P)
             transposes(r)
+            for g in late:
+                pooled(g, gp_blocks)
+            late = []
             if q == ROUNDS_PER_TILE - 1:
                 finish_o1(s)
             if ahead:
                 quantise(1, r + 1, 0, PASSES * ROWS)
                 layer1(r + 1)
                 pooled_o1(r + 1)
-            if r > 0 and q == 0:
-                for h in range(HALVES):
-                    finish_o2(s - 1, h)
-            if r == 0:
-                for h in range(HALVES):
-                    quantise_weights(*w2_jobs[0, h])
-            quantise(2, r, 0, DVE_WORDS)
-            pooled(r, dve_blocks[0:per_pass], first=(q == 0))
-            if r == 0:
-                for h in range(HALVES):
-                    quantise_weights(*w2_jobs[1, h])
-            pooled(r, dve_blocks[per_pass:])
-            quantise(2, r, gp_words0, GP_WORDS)
-            pooled(r, gp_blocks)
-        quantise_scalars(ROUNDS - 1, last=True)
+            if q == 0:
+                quantise("gp", r - 1, 0, GP_WORDS)
+                pooled(r - 1, gp_blocks, last=True)
+                quantise(2, r, 0, DVE_WORDS)
+                quantise_act_d(r)
+                pooled(r, dve_blocks + act_blocks, first=True, halves=(0,))
+            elif ahead:
+                quantise(2, r, 0, DVE_WORDS)
+                pooled(r, dve_blocks)
+                quantise_act_d(r)
+                pooled(r, act_blocks)
+                quantise("gp", r - 1, 0, GP_WORDS)
+                late.append(r - 1)
+            else:
+                quantise(2, r, 0, DVE_WORDS)
+                quantise("gp", r - 1, 0, GP_WORDS)
+                multiply2_act_d_vector(r)
+                new_z_gp(r)
+                for c in range(PASSES):
+                    multiply2_vector(r, c, GP_DS[0], DVE_ROWS, P)
+                pooled(r - 1, gp_blocks)
+                pooled(r, dve_blocks)
+                quantise_act_d(r)
+                pooled(r, act_blocks)
+                quantise("gp", r, 0, GP_WORDS)
+                pooled(r, gp_blocks, last=True)
         for h in range(HALVES):
             finish_o2(SAMPLE_TILES - 1, h)

@@ -29,9 +29,9 @@ ACT_WORDS = PASSES * P
 GP_WORDS = PASSES * GP_ROWS
 WARM_UP = 3
 GP_EXTRA = [64] * ROUNDS
-GP_EXTRA[1] = 128
+GP_EXTRA[1] = 96
 GP_EXTRA[ROUNDS - 1] = 0
-ROUTED = range(1, ROUNDS - 1)
+ROUTED = range(ROUNDS - 1)
 N2 = 512
 HALVES = S2 // N2
 HALF_P = P // 2
@@ -104,13 +104,17 @@ def tile_cin_pa_t_kernel(tc, x, x1, w1, b1, w2, b2, out):
         round_words = PASSES * ROWS * 2
         parked = out.rearrange("a n -> (a n)")[0 : ROUNDS * round_words]
 
-        def load_x_all(r):
-            nc.sync.dma_start(
-                out=x_all[r][:],
-                in_=parked[r * round_words : (r + 1) * round_words].partition_broadcast(P),
-            )
+        def load_x_all(r, parts=1):
+            words = round_words // parts
+            for n in range(parts):
+                first = r * round_words + n * words
+                nc.sync.dma_start(
+                    out=x_all[r][:, n * words : (n + 1) * words],
+                    in_=parked[first : first + words].partition_broadcast(P),
+                )
 
         x_turned_ps = {}
+        park = []
 
         x_blocks = keep.tile([P, 3 * HALF_P], F32, name="x_blocks")
 
@@ -132,12 +136,15 @@ def tile_cin_pa_t_kernel(tc, x, x1, w1, b1, w2, b2, out):
 
         def park_x():
             x_turned = keep.tile([P, 2 * P], F32, name="x_turned")
-            nc.scalar.copy(
+            nc.vector.tensor_copy(
                 out=x_turned.rearrange("p (b u) -> p b u", u=2),
                 in_=x_turned_ps[0][:, 0 : 2 * P].rearrange("p (u b) -> p b u", u=2),
             )
-            nc.scalar.dma_start(out=parked.rearrange("(p w) -> p w", w=2 * P), in_=x_turned[0:HALF_P, :])
-            load_x_all(1)
+            park.append(x_turned)
+
+        def load_x():
+            nc.scalar.dma_start(out=parked.rearrange("(p w) -> p w", w=2 * P), in_=park[0][0:HALF_P, :])
+            load_x_all(1, PASSES)
             nc.sync.dma_start(out=x1_sb[1][:], in_=x1[P : 2 * P].rearrange("b j d -> b (j d)"))
             load_x_all(2)
             nc.sync.dma_start(out=b2_rows[:], in_=b2.partition_broadcast(P))
@@ -162,7 +169,7 @@ def tile_cin_pa_t_kernel(tc, x, x1, w1, b1, w2, b2, out):
         sum_o1 = {}
         result = {}
 
-        x_banks = ("z2_back", "sum_2", "sum_0", "sum_1")
+        x_banks = ("scal", "sum_2", "sum_0", "sum_1")
 
         def spread_x(r, copies, positions=range(D_ROUND)):
             for dl in positions:
@@ -291,11 +298,11 @@ def tile_cin_pa_t_kernel(tc, x, x1, w1, b1, w2, b2, out):
             )
 
         def layer1(r, half=None):
-            def with_w1_stationary(dl0, dls):
+            def with_w1_stationary(target, dl0, dls):
                 for c in range(PASSES):
                     first = word_col(1, c, dl0, r)
                     nc.tensor.matmul_mx(
-                        out=o1[r][:, dl0 * P : (dl0 + dls) * P],
+                        out=target,
                         lhsT=w1_codes[:, c * S1 : (c + 1) * S1].bitcast(FP8X4),
                         lhsT_scale=w1_scales[:, c * S1 : (c + 1) * S1],
                         rhs=z_codes[1, r][:, first : first + dls * P].bitcast(FP8X4),
@@ -319,31 +326,26 @@ def tile_cin_pa_t_kernel(tc, x, x1, w1, b1, w2, b2, out):
                             stop=(c == PASSES - 1),
                         )
 
-            def copy_for_gpsimd(col0, cols):
-                to = col0 - (DVE_ROWS - GP_EXTRA[r])
+            def copy_for_gpsimd(col, source):
                 nc.scalar.activation(
-                    out=o1_gp[r][:, to : to + cols],
-                    in_=o1[r][:, col0 : col0 + cols],
-                    func=IDENTITY,
-                    bias=b1_col[:, 0:1],
+                    out=o1_gp[r][:, col : col + source.shape[1]], in_=source, func=IDENTITY, bias=b1_col[:, 0:1]
                 )
 
-            if r in ROUTED:
-                turned_rows()
-            if half in (None, 0):
+            if half != 1:
                 o1[r] = bank.tile([P, ROWS], F32, name="o1")
                 o1_gp[r] = two.tile([P, P + GP_ROWS], F32, name="o1_gp")
-                with_w1_stationary(DVE_DS[0], len(DVE_DS))
-            if half == 0:
-                copy_for_gpsimd(DVE_ROWS - GP_EXTRA[r], GP_EXTRA[r])
+            if r == ROUNDS - 1:
+                with_w1_stationary(o1[r][:], 0, D_ROUND)
                 return
-            with_w1_stationary(GP_DS[0], 1)
-            if not (r in ROUTED):
-                with_w1_stationary(ACT_DS[0], 1)
-            if half == 1:
-                copy_for_gpsimd(DVE_ROWS, GP_ROWS)
-            else:
-                copy_for_gpsimd(DVE_ROWS - GP_EXTRA[r], GP_EXTRA[r] + GP_ROWS)
+            if r in ROUTED and half != 0:
+                turned_rows()
+            if half != 1:
+                with_w1_stationary(o1[r][:, 0:DVE_ROWS], DVE_DS[0], len(DVE_DS))
+                copy_for_gpsimd(0, o1[r][:, DVE_ROWS - GP_EXTRA[r] : DVE_ROWS])
+            if half != 0:
+                o1_apart = bank.tile([P, N2], F32, name="o1_apart", tag="scal")
+                with_w1_stationary(o1_apart[:, 0:GP_ROWS], GP_DS[0], 1)
+                copy_for_gpsimd(GP_EXTRA[r], o1_apart[:, 0:GP_ROWS])
 
         def add_b1_turned(r):
             width = len(ACT_DS) * S1
@@ -354,6 +356,18 @@ def tile_cin_pa_t_kernel(tc, x, x1, w1, b1, w2, b2, out):
                 in1=b1_rows[:].unsqueeze(1).to_broadcast([P, len(ACT_DS), S1]),
                 op=ADD,
             )
+
+        def sum_turned(r):
+            s, q = r // ROUNDS_PER_TILE, r % ROUNDS_PER_TILE
+            if q == 0:
+                result[s] = two.tile([P, S1 + S2], F32, name="result")
+                nc.vector.scalar_tensor_tensor(
+                    out=result[s][:, 0:S1], in0=b1_rows[:], scalar=float(D), in1=o1_turned_ps[r][:, 0:S1], op0=MULT, op1=ADD
+                )
+            else:
+                nc.vector.tensor_tensor(
+                    out=result[s][:, 0:S1], in0=o1_turned_ps[r][:, 0:S1], in1=result[s][:, 0:S1], op=ADD
+                )
 
         def multiply2_scalar(r):
             s = r // ROUNDS_PER_TILE
@@ -371,7 +385,7 @@ def tile_cin_pa_t_kernel(tc, x, x1, w1, b1, w2, b2, out):
                     )
 
         def turn_z2(r, n):
-            z2_back[r, n] = bank.tile([P, N2], F32, name="z2_back")
+            z2_back[r, n] = bank.tile([P, N2], F32, name="z2_back", tag="scal")
             for g in range(F0 // 2):
                 word0 = (n * (F0 // 2) + g) * P
                 nc.tensor.transpose(
@@ -411,8 +425,9 @@ def tile_cin_pa_t_kernel(tc, x, x1, w1, b1, w2, b2, out):
             s, q = r // ROUNDS_PER_TILE, r % ROUNDS_PER_TILE
             if q == 0:
                 sum_o1[s] = bank.tile([P, N2], F32, name="sum_o1")
+            ds = [dl for dl in range(D_ROUND) if dl not in ACT_DS or not (r in ROUTED)]
             for c in range(PASSES):
-                for dl in range(D_ROUND):
+                for dl in ds:
                     block = slice(word_col(1, c, dl, r), word_col(1, c, dl, r) + P)
                     nc.tensor.matmul_mx(
                         out=sum_o1[s][:, 0:S1],
@@ -420,13 +435,11 @@ def tile_cin_pa_t_kernel(tc, x, x1, w1, b1, w2, b2, out):
                         lhsT_scale=z_scales[1, r][:, block],
                         rhs=w1_codes[:, c * S1 : (c + 1) * S1].bitcast(FP8X4),
                         rhs_scale=w1_scales[:, c * S1 : (c + 1) * S1],
-                        start=(q == 0 and c == 0 and dl == 0),
-                        stop=(q == ROUNDS_PER_TILE - 1 and c == PASSES - 1 and dl == D_ROUND - 1),
+                        start=(q == 0 and c == 0 and dl == ds[0]),
+                        stop=(q == ROUNDS_PER_TILE - 1 and c == PASSES - 1 and dl == ds[-1]),
                     )
 
         def finish(s, col, width, bias, total):
-            if s not in result:
-                result[s] = two.tile([P, S1 + S2], F32, name="result")
             nc.vector.scalar_tensor_tensor(
                 out=result[s][:, col : col + width],
                 in0=bias,
@@ -438,10 +451,17 @@ def tile_cin_pa_t_kernel(tc, x, x1, w1, b1, w2, b2, out):
             nc.sync.dma_start(out=out[s * P : (s + 1) * P, col : col + width], in_=result[s][:, col : col + width])
 
         def finish_o1(s):
-            finish(s, 0, S1, b1_rows[:], sum_o1[s][:, 0:S1])
+            nc.vector.tensor_tensor(
+                out=result[s][:, 0:S1], in0=sum_o1[s][:, 0:S1], in1=result[s][:, 0:S1], op=ADD
+            )
+            nc.sync.dma_start(out=out[s * P : (s + 1) * P, 0:S1], in_=result[s][:, 0:S1])
 
-        def finish_o2(s, h):
-            finish(s, S1 + h * N2, N2, b2_rows[:, h * N2 : (h + 1) * N2], sums[s, h][:])
+        def finish_o2(s, h, pieces=1):
+            width = N2 // pieces
+            for col in range(0, N2, width):
+                finish(
+                    s, S1 + h * N2 + col, width, b2_rows[:, h * N2 + col : h * N2 + col + width], sums[s, h][:, col : col + width]
+                )
 
         def regroup(copy, dst, src):
             copy(
@@ -455,7 +475,7 @@ def tile_cin_pa_t_kernel(tc, x, x1, w1, b1, w2, b2, out):
         w2_jobs = {}
 
         def regroup_w2(copy, c, h):
-            if (c, h) == (1, 0):
+            if (c, h) == (0, 1):
                 w2_grouped = keep_gp.tile([P, N2 * PACK], BF16, name="w2_last", tag="zg_in", align_bytes=64)
             else:
                 w2_grouped = raw_pool.tile([P, N2 * PACK], BF16, name="w2_grouped", align_bytes=64)
@@ -464,6 +484,10 @@ def tile_cin_pa_t_kernel(tc, x, x1, w1, b1, w2, b2, out):
             w2_jobs[c, h] = (w2_codes[:, cols], w2_scales[:, cols], w2_grouped[:])
 
         v_copy, s_copy = nc.vector.tensor_copy, nc.scalar.copy
+
+        def g_copy(out, in_):
+            nc.gpsimd.tensor_scalar(out=out, in0=in_, scalar1=1.0, scalar2=0.0, op0=MULT, op1=ADD)
+
         w1_grouped = keep.tile([P, PASSES * S1 * PACK], BF16, name="w1_grouped", align_bytes=64)
         w1_codes = keep.tile([P, PASSES * S1], U32, name="w1_codes", align_bytes=64)
         w1_scales = keep.tile([P, PASSES * S1], U8, name="w1_scales", align_bytes=64)
@@ -477,7 +501,7 @@ def tile_cin_pa_t_kernel(tc, x, x1, w1, b1, w2, b2, out):
 
         def regroup_w1(c):
             part = slice(c * S1 * PACK, (c + 1) * S1 * PACK)
-            regroup(nc.vector.tensor_copy, w1_grouped[:, part], w1_raw[:, part])
+            regroup(g_copy, w1_grouped[:, part], w1_raw[:, part])
 
         def transposes(r):
             for n in range(len(ACT_DS) if (r in ROUTED) else 0):
@@ -505,57 +529,58 @@ def tile_cin_pa_t_kernel(tc, x, x1, w1, b1, w2, b2, out):
         sort_x1(0)
         copies0 = [s_copy, v_copy, s_copy, s_copy]
         regroup_w1(0)
-        spread_x(0, copies0, (0, 1, 2))
+        regroup_w1(1)
+        spread_x(0, copies0, (0,))
+        turn_x()
+        park_x()
+        load_x()
+        spread_x(0, copies0, (1, 2))
         turn_x1(0)
         spread_x(0, copies0, (3,))
-        turn_x()
         new_z(1, 0)
         new_z(2, 0)
         for c in range(PASSES):
             multiply1(0, c, 0, 2)
-        regroup_w1(1)
         quantise_weights(w1_codes[:], w1_scales[:], w1_grouped[:])
-        park_x()
         regroup_w2(s_copy, 0, 0)
-        b1_t = bank.tile([P, 2 * N2], BF16, name="b1_t", tag="z2_back")
+        b1_t = bank.tile([P, 2 * N2], BF16, name="b1_t", tag="scal")
         nc.tensor.transpose(b1_t[:, 0:P], b1_rows[:], ident_b[:])
         b1_col = keep.tile([P, 1], F32, name="b1_col")
         nc.scalar.copy(out=b1_col[:], in_=b1_t[:, 0:1])
-        regroup_w2(s_copy, 0, 1)
         quantise(1, 0, 0, ROWS)
         layer1(0, 0)
+        regroup_w2(s_copy, 0, 1)
+        sort_x1(1)
         for c in range(PASSES):
             multiply1(0, c, 2, 2)
         quantise_weights(*w2_jobs[0, 0])
         quantise(1, 0, ROWS, ROWS)
         layer1(0, 1)
+        regroup_w2(s_copy, 1, 0)
         pooled_o1(0)
-        sort_x1(1)
         turn_x1(1)
         for c in range(PASSES):
             multiply2(0, c)
         multiply2_gpsimd_extra(0)
-        for h in range(HALVES):
-            regroup_w2(s_copy, 1, h)
         quantise_weights(*w2_jobs[0, 1])
         quantise(2, 0, 0, DVE_WORDS)
         pooled(0, dve_blocks[0:per_pass], first=True)
+        regroup_w2(v_copy, 1, 1)
+        multiply2_gpsimd_own(0)
         new_z(1, 1)
         multiply1(1, 0)
+        nc.scalar.copy(out=x_f32[:], in_=x_sb[:])
+        multiply2_act_d(0)
+        multiply1(1, 1)
+        sum_turned(0)
         for h in range(HALVES):
             quantise_weights(*w2_jobs[1, h])
-        pooled(0, dve_blocks[per_pass:])
-        multiply2_gpsimd_own(0)
-        multiply1(1, 1)
-        multiply2_act_d_vector(0)
-        nc.scalar.copy(out=x_f32[:], in_=x_sb[:])
         sort_x1(2)
         transposes(0)
+        pooled(0, dve_blocks[per_pass:])
         quantise(1, 1, 0, PASSES * ROWS)
         layer1(1)
         pooled_o1(1)
-        quantise_act_d(0)
-        pooled(0, act_blocks)
 
         late = []
         for r in range(1, ROUNDS):
@@ -565,14 +590,18 @@ def tile_cin_pa_t_kernel(tc, x, x1, w1, b1, w2, b2, out):
             if ahead:
                 new_z(1, r + 1)
                 multiply1(r + 1, 0)
+            if r == 1:
+                quantise_act_d(0)
+                pooled(0, act_blocks)
             multiply2_act_d(r)
             if r + 2 < ROUNDS:
                 sort_x1(r + 2)
             if ahead:
                 multiply1(r + 1, 1)
+                sum_turned(r)
             if q == 1 and s > 0:
                 finish_o2(s - 1, 0)
-                pooled(r - 1, dve_blocks + act_blocks, first=True, halves=(1,))
+            if q == 2 and s > 0:
                 finish_o2(s - 1, 1)
             if r > 1:
                 multiply2_gpsimd_own(r - 1)
@@ -581,6 +610,8 @@ def tile_cin_pa_t_kernel(tc, x, x1, w1, b1, w2, b2, out):
             for c in range(PASSES):
                 multiply2(r, c)
             transposes(r)
+            if q == 1 and s > 0:
+                pooled(r - 1, dve_blocks + act_blocks, first=True, halves=(1,))
             for g in late:
                 pooled(g, gp_blocks)
             late = []
@@ -591,10 +622,10 @@ def tile_cin_pa_t_kernel(tc, x, x1, w1, b1, w2, b2, out):
                 layer1(r + 1)
                 pooled_o1(r + 1)
             if q == 0:
-                quantise("gp", r - 1, 0, GP_WORDS)
-                pooled(r - 1, gp_blocks, last=True)
                 quantise(2, r, 0, DVE_WORDS)
                 quantise_act_d(r)
+                quantise("gp", r - 1, 0, GP_WORDS)
+                pooled(r - 1, gp_blocks, last=True)
                 pooled(r, dve_blocks + act_blocks, first=True, halves=(0,))
             elif ahead:
                 quantise(2, r, 0, DVE_WORDS)
@@ -613,8 +644,7 @@ def tile_cin_pa_t_kernel(tc, x, x1, w1, b1, w2, b2, out):
                 pooled(r - 1, gp_blocks)
                 pooled(r, dve_blocks)
                 quantise_act_d(r)
-                pooled(r, act_blocks)
                 quantise("gp", r, 0, GP_WORDS)
-                pooled(r, gp_blocks, last=True)
-        for h in range(HALVES):
-            finish_o2(SAMPLE_TILES - 1, h)
+                for h in range(HALVES):
+                    pooled(r, act_blocks + gp_blocks, last=True, halves=(h,))
+                    finish_o2(s, h, 2)

@@ -29,6 +29,7 @@ ACT_WORDS = PASSES * P
 GP_WORDS = PASSES * GP_ROWS
 WARM_UP = 3
 GP_EXTRA = [64] * ROUNDS
+GP_EXTRA[0] = 0
 GP_EXTRA[1] = 96
 GP_EXTRA[ROUNDS - 1] = 0
 ROUTED = range(ROUNDS - 1)
@@ -144,11 +145,11 @@ def tile_cin_pa_t_kernel(tc, x, x1, w1, b1, w2, b2, out):
 
         def load_x():
             nc.scalar.dma_start(out=parked.rearrange("(p w) -> p w", w=2 * P), in_=park[0][0:HALF_P, :])
-            load_x_all(1, PASSES)
-            nc.sync.dma_start(out=x1_sb[1][:], in_=x1[P : 2 * P].rearrange("b j d -> b (j d)"))
             load_x_all(2)
+            nc.sync.dma_start(out=x1_sb[1][:], in_=x1[P : 2 * P].rearrange("b j d -> b (j d)"))
+            load_x_all(3)
             nc.sync.dma_start(out=b2_rows[:], in_=b2.partition_broadcast(P))
-            for r in range(3, ROUNDS):
+            for r in range(4, ROUNDS):
                 load_x_all(r)
 
         x_f32 = keep.tile([P, SAMPLE_TILES * F0 * D], F32, name="x_f32")
@@ -169,11 +170,14 @@ def tile_cin_pa_t_kernel(tc, x, x1, w1, b1, w2, b2, out):
         sum_o1 = {}
         result = {}
 
-        x_banks = ("scal", "sum_2", "sum_0", "sum_1")
+        x_banks = ("sum_0", "sum_1", "sum_2", "scal")
 
-        def spread_x(r, copies, positions=range(D_ROUND)):
+        x_bank_of = {}
+
+        def spread_x(r, positions=range(D_ROUND)):
             for dl in positions:
                 x_bank = bank.tile([P, N2], F32, name="x_bank%d" % dl, tag=x_banks[dl])
+                x_bank_of[r, dl] = x_bank
                 for cu in range(PACK):
                     word = (r * D_ROUND + dl) * PACK + cu
                     nc.tensor.transpose(
@@ -181,12 +185,12 @@ def tile_cin_pa_t_kernel(tc, x, x1, w1, b1, w2, b2, out):
                         x_words[:, word : word + 1].to_broadcast([P, P]),
                         ident_f[:],
                     )
-                copies[dl](
-                    out=x_all[r].rearrange("p (c w u) -> p c w u", c=PASSES, u=2)[
-                        :, :, dl * P : (dl + 1) * P, :
-                    ],
-                    in_=x_bank.rearrange("p (c u b) -> p c b u", c=PASSES, u=2),
-                )
+
+        def collect_x(copy, r, dl):
+            copy(
+                out=x_all[r].rearrange("p (c w u) -> p c w u", c=PASSES, u=2)[:, :, dl * P : (dl + 1) * P, :],
+                in_=x_bank_of[r, dl].rearrange("p (c u b) -> p c b u", c=PASSES, u=2),
+            )
 
         def sort_x1(r):
             s, d0 = r // ROUNDS_PER_TILE, (r % ROUNDS_PER_TILE) * D_ROUND
@@ -341,7 +345,8 @@ def tile_cin_pa_t_kernel(tc, x, x1, w1, b1, w2, b2, out):
                 turned_rows()
             if half != 1:
                 with_w1_stationary(o1[r][:, 0:DVE_ROWS], DVE_DS[0], len(DVE_DS))
-                copy_for_gpsimd(0, o1[r][:, DVE_ROWS - GP_EXTRA[r] : DVE_ROWS])
+                if GP_EXTRA[r]:
+                    copy_for_gpsimd(0, o1[r][:, DVE_ROWS - GP_EXTRA[r] : DVE_ROWS])
             if half != 0:
                 o1_apart = bank.tile([P, N2], F32, name="o1_apart", tag="scal")
                 with_w1_stationary(o1_apart[:, 0:GP_ROWS], GP_DS[0], 1)
@@ -466,7 +471,7 @@ def tile_cin_pa_t_kernel(tc, x, x1, w1, b1, w2, b2, out):
         def regroup(copy, dst, src):
             copy(
                 out=dst.rearrange("p (g i t) -> p g t i", i=4, t=PACK),
-                in_=src.rearrange("p (t g i) -> p g t i", i=4, t=PACK),
+                in_=src.rearrange("p t (g i) -> p g t i", i=4),
             )
 
         def quantise_weights(codes, scales, grouped):
@@ -474,14 +479,24 @@ def tile_cin_pa_t_kernel(tc, x, x1, w1, b1, w2, b2, out):
 
         w2_jobs = {}
 
-        def regroup_w2(copy, c, h):
+        def regroup_w2(copies, c, h):
             if (c, h) == (0, 1):
                 w2_grouped = keep_gp.tile([P, N2 * PACK], BF16, name="w2_last", tag="zg_in", align_bytes=64)
+            elif c == h:
+                w2_grouped = keep_gp.tile([P, N2 * PACK], BF16, name="w2_turn", align_bytes=64)
             else:
                 w2_grouped = raw_pool.tile([P, N2 * PACK], BF16, name="w2_grouped", align_bytes=64)
-            regroup(copy, w2_grouped[:], w2_raw[c, h][:])
             cols = slice(c * S2 + h * N2, c * S2 + (h + 1) * N2)
             w2_jobs[c, h] = (w2_codes[:, cols], w2_scales[:, cols], w2_grouped[:])
+            for n, copy in enumerate(copies):
+                regroup_part(copy, c, h, n, N2 // len(copies))
+
+        def regroup_part(copy, c, h, n, width):
+            regroup(
+                copy,
+                w2_jobs[c, h][2][:, n * width * PACK : (n + 1) * width * PACK],
+                w2_raw[c, h].rearrange("p (t n) -> p t n", t=PACK)[:, :, n * width : (n + 1) * width],
+            )
 
         v_copy, s_copy = nc.vector.tensor_copy, nc.scalar.copy
 
@@ -501,7 +516,7 @@ def tile_cin_pa_t_kernel(tc, x, x1, w1, b1, w2, b2, out):
 
         def regroup_w1(c):
             part = slice(c * S1 * PACK, (c + 1) * S1 * PACK)
-            regroup(g_copy, w1_grouped[:, part], w1_raw[:, part])
+            regroup(g_copy, w1_grouped[:, part], w1_raw[:, part].rearrange("p (t n) -> p t n", t=PACK))
 
         def transposes(r):
             for n in range(len(ACT_DS) if (r in ROUTED) else 0):
@@ -527,45 +542,53 @@ def tile_cin_pa_t_kernel(tc, x, x1, w1, b1, w2, b2, out):
 
         sort_x()
         sort_x1(0)
-        copies0 = [s_copy, v_copy, s_copy, s_copy]
         regroup_w1(0)
         regroup_w1(1)
-        spread_x(0, copies0, (0,))
+        spread_x(0, (0,))
+        collect_x(s_copy, 0, 0)
         turn_x()
         park_x()
         load_x()
-        spread_x(0, copies0, (1, 2))
+        spread_x(0, (1, 2))
+        collect_x(v_copy, 0, 1)
+        collect_x(s_copy, 0, 2)
         turn_x1(0)
-        spread_x(0, copies0, (3,))
+        spread_x(0, (3,))
+        collect_x(s_copy, 0, 3)
+        spread_x(1)
         new_z(1, 0)
         new_z(2, 0)
         for c in range(PASSES):
             multiply1(0, c, 0, 2)
         quantise_weights(w1_codes[:], w1_scales[:], w1_grouped[:])
-        regroup_w2(s_copy, 0, 0)
-        b1_t = bank.tile([P, 2 * N2], BF16, name="b1_t", tag="scal")
+        regroup_w2([s_copy], 0, 0)
+        b1_t = bank.tile([P, 2 * N2], BF16, name="b1_t", tag="o1")
         nc.tensor.transpose(b1_t[:, 0:P], b1_rows[:], ident_b[:])
         b1_col = keep.tile([P, 1], F32, name="b1_col")
         nc.scalar.copy(out=b1_col[:], in_=b1_t[:, 0:1])
+        collect_x(s_copy, 1, 3)
         quantise(1, 0, 0, ROWS)
         layer1(0, 0)
-        regroup_w2(s_copy, 0, 1)
+        regroup_w2([s_copy], 0, 1)
         sort_x1(1)
+        collect_x(s_copy, 1, 2)
         for c in range(PASSES):
             multiply1(0, c, 2, 2)
         quantise_weights(*w2_jobs[0, 0])
+        regroup_w2([], 1, 1)
+        regroup_part(g_copy, 1, 1, 0, N2 // 2)
         quantise(1, 0, ROWS, ROWS)
         layer1(0, 1)
-        regroup_w2(s_copy, 1, 0)
+        regroup_w2([s_copy], 1, 0)
         pooled_o1(0)
         turn_x1(1)
         for c in range(PASSES):
             multiply2(0, c)
-        multiply2_gpsimd_extra(0)
         quantise_weights(*w2_jobs[0, 1])
         quantise(2, 0, 0, DVE_WORDS)
+        collect_x(v_copy, 1, 0)
+        collect_x(v_copy, 1, 1)
         pooled(0, dve_blocks[0:per_pass], first=True)
-        regroup_w2(v_copy, 1, 1)
         multiply2_gpsimd_own(0)
         new_z(1, 1)
         multiply1(1, 0)
@@ -573,6 +596,7 @@ def tile_cin_pa_t_kernel(tc, x, x1, w1, b1, w2, b2, out):
         multiply2_act_d(0)
         multiply1(1, 1)
         sum_turned(0)
+        regroup_part(v_copy, 1, 1, 1, N2 // 2)
         for h in range(HALVES):
             quantise_weights(*w2_jobs[1, h])
         sort_x1(2)

@@ -28,8 +28,7 @@ DVE_WORDS = PASSES * DVE_ROWS
 ACT_WORDS = PASSES * P
 GP_WORDS = PASSES * GP_ROWS
 WARM_UP = 3
-GP_EXTRA = [64] * ROUNDS
-GP_EXTRA[0] = 0
+GP_EXTRA = [72] * ROUNDS
 GP_EXTRA[1] = 96
 GP_EXTRA[ROUNDS - 1] = 0
 ROUTED = range(ROUNDS - 1)
@@ -362,18 +361,6 @@ def tile_cin_pa_t_kernel(tc, x, x1, w1, b1, w2, b2, out):
                 op=ADD,
             )
 
-        def sum_turned(r):
-            s, q = r // ROUNDS_PER_TILE, r % ROUNDS_PER_TILE
-            if q == 0:
-                result[s] = two.tile([P, S1 + S2], F32, name="result")
-                nc.vector.scalar_tensor_tensor(
-                    out=result[s][:, 0:S1], in0=b1_rows[:], scalar=float(D), in1=o1_turned_ps[r][:, 0:S1], op0=MULT, op1=ADD
-                )
-            else:
-                nc.vector.tensor_tensor(
-                    out=result[s][:, 0:S1], in0=o1_turned_ps[r][:, 0:S1], in1=result[s][:, 0:S1], op=ADD
-                )
-
         def multiply2_scalar(r):
             s = r // ROUNDS_PER_TILE
             z2_turned[r] = two.tile([P, len(ACT_DS) * F0 * S1], BF16, name="z2_turned")
@@ -430,9 +417,8 @@ def tile_cin_pa_t_kernel(tc, x, x1, w1, b1, w2, b2, out):
             s, q = r // ROUNDS_PER_TILE, r % ROUNDS_PER_TILE
             if q == 0:
                 sum_o1[s] = bank.tile([P, N2], F32, name="sum_o1")
-            ds = [dl for dl in range(D_ROUND) if dl not in ACT_DS or not (r in ROUTED)]
             for c in range(PASSES):
-                for dl in ds:
+                for dl in range(D_ROUND):
                     block = slice(word_col(1, c, dl, r), word_col(1, c, dl, r) + P)
                     nc.tensor.matmul_mx(
                         out=sum_o1[s][:, 0:S1],
@@ -440,11 +426,13 @@ def tile_cin_pa_t_kernel(tc, x, x1, w1, b1, w2, b2, out):
                         lhsT_scale=z_scales[1, r][:, block],
                         rhs=w1_codes[:, c * S1 : (c + 1) * S1].bitcast(FP8X4),
                         rhs_scale=w1_scales[:, c * S1 : (c + 1) * S1],
-                        start=(q == 0 and c == 0 and dl == ds[0]),
-                        stop=(q == ROUNDS_PER_TILE - 1 and c == PASSES - 1 and dl == ds[-1]),
+                        start=(q == 0 and c == 0 and dl == 0),
+                        stop=(q == ROUNDS_PER_TILE - 1 and c == PASSES - 1 and dl == D_ROUND - 1),
                     )
 
         def finish(s, col, width, bias, total):
+            if s not in result:
+                result[s] = two.tile([P, S1 + S2], F32, name="result")
             nc.vector.scalar_tensor_tensor(
                 out=result[s][:, col : col + width],
                 in0=bias,
@@ -456,10 +444,7 @@ def tile_cin_pa_t_kernel(tc, x, x1, w1, b1, w2, b2, out):
             nc.sync.dma_start(out=out[s * P : (s + 1) * P, col : col + width], in_=result[s][:, col : col + width])
 
         def finish_o1(s):
-            nc.vector.tensor_tensor(
-                out=result[s][:, 0:S1], in0=sum_o1[s][:, 0:S1], in1=result[s][:, 0:S1], op=ADD
-            )
-            nc.sync.dma_start(out=out[s * P : (s + 1) * P, 0:S1], in_=result[s][:, 0:S1])
+            finish(s, 0, S1, b1_rows[:], sum_o1[s][:, 0:S1])
 
         def finish_o2(s, h, pieces=1):
             width = N2 // pieces
@@ -482,8 +467,6 @@ def tile_cin_pa_t_kernel(tc, x, x1, w1, b1, w2, b2, out):
         def regroup_w2(copies, c, h):
             if (c, h) == (0, 1):
                 w2_grouped = keep_gp.tile([P, N2 * PACK], BF16, name="w2_last", tag="zg_in", align_bytes=64)
-            elif c == h:
-                w2_grouped = keep_gp.tile([P, N2 * PACK], BF16, name="w2_turn", align_bytes=64)
             else:
                 w2_grouped = raw_pool.tile([P, N2 * PACK], BF16, name="w2_grouped", align_bytes=64)
             cols = slice(c * S2 + h * N2, c * S2 + (h + 1) * N2)
@@ -500,9 +483,6 @@ def tile_cin_pa_t_kernel(tc, x, x1, w1, b1, w2, b2, out):
 
         v_copy, s_copy = nc.vector.tensor_copy, nc.scalar.copy
 
-        def g_copy(out, in_):
-            nc.gpsimd.tensor_scalar(out=out, in0=in_, scalar1=1.0, scalar2=0.0, op0=MULT, op1=ADD)
-
         w1_grouped = keep.tile([P, PASSES * S1 * PACK], BF16, name="w1_grouped", align_bytes=64)
         w1_codes = keep.tile([P, PASSES * S1], U32, name="w1_codes", align_bytes=64)
         w1_scales = keep.tile([P, PASSES * S1], U8, name="w1_scales", align_bytes=64)
@@ -516,7 +496,7 @@ def tile_cin_pa_t_kernel(tc, x, x1, w1, b1, w2, b2, out):
 
         def regroup_w1(c):
             part = slice(c * S1 * PACK, (c + 1) * S1 * PACK)
-            regroup(g_copy, w1_grouped[:, part], w1_raw[:, part].rearrange("p (t n) -> p t n", t=PACK))
+            regroup(v_copy, w1_grouped[:, part], w1_raw[:, part].rearrange("p (t n) -> p t n", t=PACK))
 
         def transposes(r):
             for n in range(len(ACT_DS) if (r in ROUTED) else 0):
@@ -542,18 +522,18 @@ def tile_cin_pa_t_kernel(tc, x, x1, w1, b1, w2, b2, out):
 
         sort_x()
         sort_x1(0)
-        regroup_w1(0)
-        regroup_w1(1)
         spread_x(0, (0,))
         collect_x(s_copy, 0, 0)
         turn_x()
         park_x()
         load_x()
-        spread_x(0, (1, 2))
-        collect_x(v_copy, 0, 1)
-        collect_x(s_copy, 0, 2)
+        for c in range(PASSES):
+            regroup_w1(c)
+        spread_x(0, (1,))
+        collect_x(s_copy, 0, 1)
         turn_x1(0)
-        spread_x(0, (3,))
+        spread_x(0, (2, 3))
+        collect_x(s_copy, 0, 2)
         collect_x(s_copy, 0, 3)
         spread_x(1)
         new_z(1, 0)
@@ -561,46 +541,44 @@ def tile_cin_pa_t_kernel(tc, x, x1, w1, b1, w2, b2, out):
         for c in range(PASSES):
             multiply1(0, c, 0, 2)
         quantise_weights(w1_codes[:], w1_scales[:], w1_grouped[:])
-        regroup_w2([s_copy], 0, 0)
         b1_t = bank.tile([P, 2 * N2], BF16, name="b1_t", tag="o1")
         nc.tensor.transpose(b1_t[:, 0:P], b1_rows[:], ident_b[:])
         b1_col = keep.tile([P, 1], F32, name="b1_col")
         nc.scalar.copy(out=b1_col[:], in_=b1_t[:, 0:1])
-        collect_x(s_copy, 1, 3)
+        for dl in reversed(range(D_ROUND)):
+            collect_x(s_copy, 1, dl)
         quantise(1, 0, 0, ROWS)
         layer1(0, 0)
-        regroup_w2([s_copy], 0, 1)
         sort_x1(1)
-        collect_x(s_copy, 1, 2)
+        sort_x1(2)
         for c in range(PASSES):
             multiply1(0, c, 2, 2)
-        quantise_weights(*w2_jobs[0, 0])
-        regroup_w2([], 1, 1)
-        regroup_part(g_copy, 1, 1, 0, N2 // 2)
+        regroup_w2([v_copy], 0, 0)
         quantise(1, 0, ROWS, ROWS)
-        layer1(0, 1)
         regroup_w2([s_copy], 1, 0)
+        layer1(0, 1)
         pooled_o1(0)
         turn_x1(1)
         for c in range(PASSES):
             multiply2(0, c)
-        quantise_weights(*w2_jobs[0, 1])
+        multiply2_gpsimd_extra(0)
+        regroup_w2([v_copy], 0, 1)
+        for h in range(HALVES):
+            quantise_weights(*w2_jobs[0, h])
         quantise(2, 0, 0, DVE_WORDS)
-        collect_x(v_copy, 1, 0)
-        collect_x(v_copy, 1, 1)
         pooled(0, dve_blocks[0:per_pass], first=True)
         multiply2_gpsimd_own(0)
         new_z(1, 1)
         multiply1(1, 0)
+        regroup_w2([s_copy], 1, 1)
         nc.scalar.copy(out=x_f32[:], in_=x_sb[:])
         multiply2_act_d(0)
         multiply1(1, 1)
-        sum_turned(0)
-        regroup_part(v_copy, 1, 1, 1, N2 // 2)
+        turn_x1(2)
         for h in range(HALVES):
             quantise_weights(*w2_jobs[1, h])
-        sort_x1(2)
-        transposes(0)
+        turn_z2(0, 0)
+        collect_z2(0, 0)
         pooled(0, dve_blocks[per_pass:])
         quantise(1, 1, 0, PASSES * ROWS)
         layer1(1)
@@ -622,7 +600,6 @@ def tile_cin_pa_t_kernel(tc, x, x1, w1, b1, w2, b2, out):
                 sort_x1(r + 2)
             if ahead:
                 multiply1(r + 1, 1)
-                sum_turned(r)
             if q == 1 and s > 0:
                 finish_o2(s - 1, 0)
             if q == 2 and s > 0:

@@ -27,7 +27,7 @@ DVE_ROWS, GP_ROWS = len(DVE_DS) * P, len(GP_DS) * P
 DVE_WORDS = PASSES * DVE_ROWS
 ACT_WORDS = PASSES * P
 GP_WORDS = PASSES * GP_ROWS
-WARM_UP = 3
+WARM_UP = 6
 GP_EXTRA = [72] * ROUNDS
 GP_EXTRA[1] = 96
 GP_EXTRA[ROUNDS - 1] = 0
@@ -498,6 +498,11 @@ def tile_cin_pa_t_kernel(tc, x, x1, w1, b1, w2, b2, out):
             part = slice(c * S1 * PACK, (c + 1) * S1 * PACK)
             regroup(v_copy, w1_grouped[:, part], w1_raw[:, part].rearrange("p (t n) -> p t n", t=PACK))
 
+        def keep_warm(n, idle_bank):
+            idle_ps = bank.tile([P, N2], F32, name="idle_ps", tag=idle_bank)
+            for k in range(n):
+                nc.tensor.matmul(out=idle_ps[:], lhsT=warm[:, 0:P], rhs=warm[:], start=True, stop=True)
+
         def transposes(r):
             for n in range(len(ACT_DS) if (r in ROUTED) else 0):
                 turn_z2(r, n)
@@ -559,6 +564,7 @@ def tile_cin_pa_t_kernel(tc, x, x1, w1, b1, w2, b2, out):
         layer1(0, 1)
         pooled_o1(0)
         turn_x1(1)
+        keep_warm(2, "sum_2")
         for c in range(PASSES):
             multiply2(0, c)
         multiply2_gpsimd_extra(0)
@@ -567,6 +573,7 @@ def tile_cin_pa_t_kernel(tc, x, x1, w1, b1, w2, b2, out):
             quantise_weights(*w2_jobs[0, h])
         quantise(2, 0, 0, DVE_WORDS)
         pooled(0, dve_blocks[0:per_pass], first=True)
+        keep_warm(2, "sum_2")
         multiply2_gpsimd_own(0)
         new_z(1, 1)
         multiply1(1, 0)
@@ -602,8 +609,6 @@ def tile_cin_pa_t_kernel(tc, x, x1, w1, b1, w2, b2, out):
                 multiply1(r + 1, 1)
             if q == 1 and s > 0:
                 finish_o2(s - 1, 0)
-            if q == 2 and s > 0:
-                finish_o2(s - 1, 1)
             if r > 1:
                 multiply2_gpsimd_own(r - 1)
             if ahead:
@@ -611,6 +616,8 @@ def tile_cin_pa_t_kernel(tc, x, x1, w1, b1, w2, b2, out):
             for c in range(PASSES):
                 multiply2(r, c)
             transposes(r)
+            if r == 1:
+                keep_warm(2, "sum_2")
             if q == 1 and s > 0:
                 pooled(r - 1, dve_blocks + act_blocks, first=True, halves=(1,))
             for g in late:
@@ -646,6 +653,7 @@ def tile_cin_pa_t_kernel(tc, x, x1, w1, b1, w2, b2, out):
                 pooled(r, dve_blocks)
                 quantise_act_d(r)
                 quantise("gp", r, 0, GP_WORDS)
+                finish_o2(s - 1, 1)
                 for h in range(HALVES):
                     pooled(r, act_blocks + gp_blocks, last=True, halves=(h,))
                     finish_o2(s, h, 2)

@@ -27,8 +27,8 @@ DVE_ROWS, GP_ROWS = len(DVE_DS) * P, len(GP_DS) * P
 DVE_WORDS = PASSES * DVE_ROWS
 ACT_WORDS = PASSES * P
 GP_WORDS = PASSES * GP_ROWS
-WARM_UP = 6
-GP_EXTRA = [72] * ROUNDS
+WARM_UP = 3
+GP_EXTRA = [56] * ROUNDS
 GP_EXTRA[1] = 96
 GP_EXTRA[ROUNDS - 1] = 0
 ROUTED = range(ROUNDS - 1)
@@ -169,13 +169,13 @@ def tile_cin_pa_t_kernel(tc, x, x1, w1, b1, w2, b2, out):
         sum_o1 = {}
         result = {}
 
-        x_banks = ("sum_0", "sum_1", "sum_2", "scal")
+        x_banks = (("sum_0", "sum_1", "sum_2", "scal"), ("sum_0", "sum_1", "o1_turned", "sum_o1"))
 
         x_bank_of = {}
 
         def spread_x(r, positions=range(D_ROUND)):
             for dl in positions:
-                x_bank = bank.tile([P, N2], F32, name="x_bank%d" % dl, tag=x_banks[dl])
+                x_bank = bank.tile([P, N2], F32, name="x_bank%d_%d" % (r, dl), tag=x_banks[r][dl])
                 x_bank_of[r, dl] = x_bank
                 for cu in range(PACK):
                     word = (r * D_ROUND + dl) * PACK + cu
@@ -191,20 +191,22 @@ def tile_cin_pa_t_kernel(tc, x, x1, w1, b1, w2, b2, out):
                 in_=x_bank_of[r, dl].rearrange("p (c u b) -> p c b u", c=PASSES, u=2),
             )
 
-        def sort_x1(r):
-            s, d0 = r // ROUNDS_PER_TILE, (r % ROUNDS_PER_TILE) * D_ROUND
-            x1_by_d[r] = two.tile([P, ROWS * 2], BF16, name="x1_by_d")
+        def sort_x1(r, dl0=0, dls=D_ROUND):
+            s, d0 = r // ROUNDS_PER_TILE, (r % ROUNDS_PER_TILE) * D_ROUND + dl0
+            if dl0 == 0:
+                x1_by_d[r] = two.tile([P, ROWS * 2], BF16, name="x1_by_d")
             nc.scalar.copy(
-                out=x1_by_d[r].rearrange("p (d j e) -> p d j e", d=D_ROUND, e=2),
+                out=x1_by_d[r].rearrange("p (d j e) -> p d j e", d=D_ROUND, e=2)[:, dl0 : dl0 + dls],
                 in_=x1_sb[s]
-                .rearrange("p (j d) -> p d j", d=D)[:, d0 : d0 + D_ROUND, :]
+                .rearrange("p (j d) -> p d j", d=D)[:, d0 : d0 + dls, :]
                 .unsqueeze(3)
-                .to_broadcast([P, D_ROUND, FK, 2]),
+                .to_broadcast([P, dls, FK, 2]),
             )
 
-        def turn_x1(r):
-            x1_t[r] = bank.tile([P, ROWS], F32, name="x1_t")
-            for dl in range(D_ROUND):
+        def turn_x1(r, dl0=0, dls=D_ROUND):
+            if dl0 == 0:
+                x1_t[r] = bank.tile([P, ROWS], F32, name="x1_t")
+            for dl in range(dl0, dl0 + dls):
                 nc.tensor.transpose(
                     x1_t[r][:, dl * P : (dl + 1) * P],
                     x1_by_d[r][:].bitcast(F32)[:, dl * P : (dl + 1) * P],
@@ -496,12 +498,14 @@ def tile_cin_pa_t_kernel(tc, x, x1, w1, b1, w2, b2, out):
 
         def regroup_w1(c):
             part = slice(c * S1 * PACK, (c + 1) * S1 * PACK)
-            regroup(v_copy, w1_grouped[:, part], w1_raw[:, part].rearrange("p (t n) -> p t n", t=PACK))
-
-        def keep_warm(n, idle_bank):
-            idle_ps = bank.tile([P, N2], F32, name="idle_ps", tag=idle_bank)
-            for k in range(n):
-                nc.tensor.matmul(out=idle_ps[:], lhsT=warm[:, 0:P], rhs=warm[:], start=True, stop=True)
+            nc.gpsimd.tensor_scalar(
+                out=w1_grouped[:, part].rearrange("p (n t) -> p n t", t=PACK),
+                in0=w1_raw[:, part].rearrange("p (t n) -> p n t", t=PACK),
+                scalar1=1.0,
+                scalar2=0.0,
+                op0=MULT,
+                op1=ADD,
+            )
 
         def transposes(r):
             for n in range(len(ACT_DS) if (r in ROUTED) else 0):
@@ -526,30 +530,33 @@ def tile_cin_pa_t_kernel(tc, x, x1, w1, b1, w2, b2, out):
             quantise(2, r, act_words0, len(ACT_DS) * ACT_WORDS)
 
         sort_x()
-        sort_x1(0)
+        sort_x1(0, 0, 2)
         spread_x(0, (0,))
         collect_x(s_copy, 0, 0)
+        sort_x1(0, 2, 2)
         turn_x()
         park_x()
         load_x()
         for c in range(PASSES):
             regroup_w1(c)
         spread_x(0, (1,))
-        collect_x(s_copy, 0, 1)
-        turn_x1(0)
+        collect_x(v_copy, 0, 1)
+        turn_x1(0, 0, 2)
         spread_x(0, (2, 3))
         collect_x(s_copy, 0, 2)
         collect_x(s_copy, 0, 3)
-        spread_x(1)
-        new_z(1, 0)
-        new_z(2, 0)
-        for c in range(PASSES):
-            multiply1(0, c, 0, 2)
-        quantise_weights(w1_codes[:], w1_scales[:], w1_grouped[:])
         b1_t = bank.tile([P, 2 * N2], BF16, name="b1_t", tag="o1")
         nc.tensor.transpose(b1_t[:, 0:P], b1_rows[:], ident_b[:])
         b1_col = keep.tile([P, 1], F32, name="b1_col")
         nc.scalar.copy(out=b1_col[:], in_=b1_t[:, 0:1])
+        spread_x(1, (3, 2))
+        new_z(1, 0)
+        new_z(2, 0)
+        for c in range(PASSES):
+            multiply1(0, c, 0, 2)
+        turn_x1(0, 2, 2)
+        spread_x(1, (1, 0))
+        quantise_weights(w1_codes[:], w1_scales[:], w1_grouped[:])
         for dl in reversed(range(D_ROUND)):
             collect_x(s_copy, 1, dl)
         quantise(1, 0, 0, ROWS)
@@ -564,7 +571,6 @@ def tile_cin_pa_t_kernel(tc, x, x1, w1, b1, w2, b2, out):
         layer1(0, 1)
         pooled_o1(0)
         turn_x1(1)
-        keep_warm(2, "sum_2")
         for c in range(PASSES):
             multiply2(0, c)
         multiply2_gpsimd_extra(0)
@@ -573,7 +579,6 @@ def tile_cin_pa_t_kernel(tc, x, x1, w1, b1, w2, b2, out):
             quantise_weights(*w2_jobs[0, h])
         quantise(2, 0, 0, DVE_WORDS)
         pooled(0, dve_blocks[0:per_pass], first=True)
-        keep_warm(2, "sum_2")
         multiply2_gpsimd_own(0)
         new_z(1, 1)
         multiply1(1, 0)
@@ -616,8 +621,6 @@ def tile_cin_pa_t_kernel(tc, x, x1, w1, b1, w2, b2, out):
             for c in range(PASSES):
                 multiply2(r, c)
             transposes(r)
-            if r == 1:
-                keep_warm(2, "sum_2")
             if q == 1 and s > 0:
                 pooled(r - 1, dve_blocks + act_blocks, first=True, halves=(1,))
             for g in late:

@@ -69,8 +69,14 @@ def tile_cin_pa_t_kernel(tc, x, x1, w1, b1, w2, b2, out):
             out=w1_raw.rearrange("p (g n) -> p g n", n=S1),
             in_=w1.rearrange("(g p) n -> p g n", p=P),
         )
+        b_row = keep.tile([P, S1 + S2], BF16, name="b_row")
+        nc.vector.memset(b_row[:], 0.0)
+        ones = keep.tile([P, P], BF16, name="ones")
+        nc.vector.memset(ones[:], 1.0)
+        nc.sync.dma_start(out=b_row[0:1, 0:S1], in_=b1.unsqueeze(0))
+        nc.sync.dma_start(out=b_row[0:1, S1 : S1 + S2], in_=b2.unsqueeze(0))
         b1_rows = keep.tile([P, S1], BF16, name="b1_rows")
-        nc.sync.dma_start(out=b1_rows[:], in_=b1.partition_broadcast(P))
+        b1_col = keep.tile([P, 1], F32, name="b1_col")
         w2_raw = {}
 
         def load_w2(c):
@@ -89,8 +95,6 @@ def tile_cin_pa_t_kernel(tc, x, x1, w1, b1, w2, b2, out):
 
         ident_f = keep.tile([P, P], F32, name="ident_f")
         make_identity(nc, ident_f[:])
-        ident_b = keep.tile([P, P], BF16, name="ident_b")
-        make_identity(nc, ident_b[:])
 
         x_fields = keep.tile([P, SAMPLE_TILES * F0 * D], BF16, name="x_fields")
         for s in range(SAMPLE_TILES):
@@ -147,7 +151,6 @@ def tile_cin_pa_t_kernel(tc, x, x1, w1, b1, w2, b2, out):
             load_x_all(2)
             nc.sync.dma_start(out=x1_sb[1][:], in_=x1[P : 2 * P].rearrange("b j d -> b (j d)"))
             load_x_all(3)
-            nc.sync.dma_start(out=b2_rows[:], in_=b2.partition_broadcast(P))
             for r in range(4, ROUNDS):
                 load_x_all(r)
 
@@ -464,6 +467,21 @@ def tile_cin_pa_t_kernel(tc, x, x1, w1, b1, w2, b2, out):
         def quantise_weights(codes, scales, grouped):
             nc.vector.quantize_mx(out=codes.bitcast(FP8X4), scales=scales, in_=grouped)
 
+        def spread_b1():
+            b1_ps = bank.tile([P, N2], F32, name="b1_ps", tag="o1")
+            nc.tensor.matmul(out=b1_ps[:, 0:S1], lhsT=ones[:], rhs=b_row[:, 0:S1], start=True, stop=True)
+            nc.tensor.matmul(out=b1_ps[:, S1 : 2 * S1], lhsT=b_row[:, 0:S1], rhs=ones[:], start=True, stop=True)
+            nc.scalar.copy(out=b1_rows[:], in_=b1_ps[:, 0:S1])
+            nc.scalar.copy(out=b1_col[:], in_=b1_ps[:, S1 : S1 + 1])
+
+        def spread_b2(h):
+            cols = slice(h * N2, (h + 1) * N2)
+            b2_ps = bank.tile([P, N2], F32, name="b2_ps", tag="sum_2")
+            nc.tensor.matmul(
+                out=b2_ps[:], lhsT=ones[:], rhs=b_row[:, S1 + h * N2 : S1 + (h + 1) * N2], start=True, stop=True
+            )
+            nc.scalar.copy(out=b2_rows[:, cols], in_=b2_ps[:])
+
         w2_jobs = {}
 
         def regroup_w2(copies, c, h):
@@ -545,10 +563,7 @@ def tile_cin_pa_t_kernel(tc, x, x1, w1, b1, w2, b2, out):
         spread_x(0, (2, 3))
         collect_x(s_copy, 0, 2)
         collect_x(s_copy, 0, 3)
-        b1_t = bank.tile([P, 2 * N2], BF16, name="b1_t", tag="o1")
-        nc.tensor.transpose(b1_t[:, 0:P], b1_rows[:], ident_b[:])
-        b1_col = keep.tile([P, 1], F32, name="b1_col")
-        nc.scalar.copy(out=b1_col[:], in_=b1_t[:, 0:1])
+        spread_b1()
         spread_x(1, (3, 2))
         new_z(1, 0)
         new_z(2, 0)
@@ -621,6 +636,8 @@ def tile_cin_pa_t_kernel(tc, x, x1, w1, b1, w2, b2, out):
             for c in range(PASSES):
                 multiply2(r, c)
             transposes(r)
+            if 0 < r <= HALVES:
+                spread_b2(r - 1)
             if q == 1 and s > 0:
                 pooled(r - 1, dve_blocks + act_blocks, first=True, halves=(1,))
             for g in late:

@@ -28,9 +28,10 @@ DVE_WORDS = PASSES * DVE_ROWS
 ACT_WORDS = PASSES * P
 GP_WORDS = PASSES * GP_ROWS
 WARM_UP = 3
-GP_EXTRA = [56] * ROUNDS
+GP_EXTRA = [72] * ROUNDS
 GP_EXTRA[1] = 96
 GP_EXTRA[ROUNDS - 1] = 0
+SUMMED_BY_VECTOR = range(2, ROUNDS - 1)
 ROUTED = range(ROUNDS - 1)
 N2 = 512
 HALVES = S2 // N2
@@ -366,6 +367,18 @@ def tile_cin_pa_t_kernel(tc, x, x1, w1, b1, w2, b2, out):
                 op=ADD,
             )
 
+        def sum_turned(r):
+            s = r // ROUNDS_PER_TILE
+            if s not in result:
+                result[s] = two.tile([P, S1 + S2], F32, name="result")
+                nc.vector.scalar_tensor_tensor(
+                    out=result[s][:, 0:S1], in0=b1_rows[:], scalar=float(D), in1=o1_turned_ps[r][:, 0:S1], op0=MULT, op1=ADD
+                )
+            else:
+                nc.vector.tensor_tensor(
+                    out=result[s][:, 0:S1], in0=o1_turned_ps[r][:, 0:S1], in1=result[s][:, 0:S1], op=ADD
+                )
+
         def multiply2_scalar(r):
             s = r // ROUNDS_PER_TILE
             z2_turned[r] = two.tile([P, len(ACT_DS) * F0 * S1], BF16, name="z2_turned")
@@ -422,8 +435,9 @@ def tile_cin_pa_t_kernel(tc, x, x1, w1, b1, w2, b2, out):
             s, q = r // ROUNDS_PER_TILE, r % ROUNDS_PER_TILE
             if q == 0:
                 sum_o1[s] = bank.tile([P, N2], F32, name="sum_o1")
+            ds = [dl for dl in range(D_ROUND) if dl not in ACT_DS or r not in SUMMED_BY_VECTOR]
             for c in range(PASSES):
-                for dl in range(D_ROUND):
+                for dl in ds:
                     block = slice(word_col(1, c, dl, r), word_col(1, c, dl, r) + P)
                     nc.tensor.matmul_mx(
                         out=sum_o1[s][:, 0:S1],
@@ -431,8 +445,8 @@ def tile_cin_pa_t_kernel(tc, x, x1, w1, b1, w2, b2, out):
                         lhsT_scale=z_scales[1, r][:, block],
                         rhs=w1_codes[:, c * S1 : (c + 1) * S1].bitcast(FP8X4),
                         rhs_scale=w1_scales[:, c * S1 : (c + 1) * S1],
-                        start=(q == 0 and c == 0 and dl == 0),
-                        stop=(q == ROUNDS_PER_TILE - 1 and c == PASSES - 1 and dl == D_ROUND - 1),
+                        start=(q == 0 and c == 0 and dl == ds[0]),
+                        stop=(q == ROUNDS_PER_TILE - 1 and c == PASSES - 1 and dl == ds[-1]),
                     )
 
         def finish(s, col, width, bias, total):
@@ -449,7 +463,13 @@ def tile_cin_pa_t_kernel(tc, x, x1, w1, b1, w2, b2, out):
             nc.sync.dma_start(out=out[s * P : (s + 1) * P, col : col + width], in_=result[s][:, col : col + width])
 
         def finish_o1(s):
-            finish(s, 0, S1, b1_rows[:], sum_o1[s][:, 0:S1])
+            if s not in result:
+                finish(s, 0, S1, b1_rows[:], sum_o1[s][:, 0:S1])
+                return
+            nc.vector.tensor_tensor(
+                out=result[s][:, 0:S1], in0=sum_o1[s][:, 0:S1], in1=result[s][:, 0:S1], op=ADD
+            )
+            nc.sync.dma_start(out=out[s * P : (s + 1) * P, 0:S1], in_=result[s][:, 0:S1])
 
         def finish_o2(s, h, pieces=1):
             width = N2 // pieces
@@ -627,6 +647,8 @@ def tile_cin_pa_t_kernel(tc, x, x1, w1, b1, w2, b2, out):
                 sort_x1(r + 2)
             if ahead:
                 multiply1(r + 1, 1)
+            if r in SUMMED_BY_VECTOR:
+                sum_turned(r)
             if q == 1 and s > 0:
                 finish_o2(s - 1, 0)
             if r > 1:

from concourse import mybir
from concourse.masks import make_identity

BF16 = mybir.dt.bfloat16
F32 = mybir.dt.float32
U32 = mybir.dt.uint32
U8 = mybir.dt.uint8
FP8X4 = mybir.dt.float8_e4m3fn_x4
IDENTITY = mybir.ActivationFunctionType.Identity
COPY = mybir.ActivationFunctionType.Copy
MULT = mybir.AluOpType.mult
ADD = mybir.AluOpType.add

P = 128
PACK = 4
B, F0, FK, S1, S2, D = 256, 8, 128, 128, 1024, 16
PASSES = F0 // PACK
SAMPLE_TILES = B // P
D_ROUND = 4
ROUNDS_PER_TILE = D // D_ROUND
ROUNDS = SAMPLE_TILES * ROUNDS_PER_TILE
ROWS = D_ROUND * P
DVE_DS = (0, 1)
GP_DS = (2,)
ACT_DS = (3,)
DVE_ROWS, GP_ROWS = len(DVE_DS) * P, len(GP_DS) * P
DVE_WORDS = PASSES * DVE_ROWS
ACT_WORDS = PASSES * P
GP_WORDS = PASSES * GP_ROWS
WARM_UP = 3
GP_EXTRA = [72] * ROUNDS
GP_EXTRA[1] = 96
GP_EXTRA[ROUNDS - 1] = 0
SUMMED_BY_VECTOR = range(2, ROUNDS - 1)
ROUTED = range(ROUNDS - 1)
N2 = 512
HALVES = S2 // N2
HALF_P = P // 2
PE_SPREAD_ROUNDS = 2

FLOPS = 2 * B * D * (F0 * FK * S1 + F0 * S1 * S2)


def tile_cin_pa_t_kernel(tc, x, x1, w1, b1, w2, b2, out):
    nc = tc.nc
    with (
        tc.manual_schedule(),
        tc.tile_pool(name="keep", bufs=1) as keep,
        tc.tile_pool(name="raw", bufs=4) as raw_pool,
        tc.tile_pool(name="two", bufs=2) as two,
        tc.tile_pool(name="three", bufs=3) as three,
        tc.tile_pool(name="keep_gp", bufs=1) as keep_gp,
        tc.psum_pool(name="bank", bufs=1) as bank,
    ):
        warm = keep.tile([P, N2], BF16, name="warm")
        nc.vector.memset(warm[:], 0.0)
        warm_ps = bank.tile([P, N2], F32, name="warm_ps", tag="o1")
        for n in range(WARM_UP):
            nc.tensor.matmul(out=warm_ps[:], lhsT=warm[:, 0:P], rhs=warm[:], start=True, stop=True)

        x_sb = keep.tile([P, SAMPLE_TILES * F0 * D], BF16, name="x_sb")
        nc.sync.dma_start(
            out=x_sb.rearrange("p (s f) -> p s f", s=SAMPLE_TILES),
            in_=x.rearrange("(s b) i d -> b s (i d)", s=SAMPLE_TILES),
        )
        x1_sb = [keep.tile([P, FK * D], BF16, name="x1_sb%d" % s) for s in range(SAMPLE_TILES)]
        nc.sync.dma_start(out=x1_sb[0][:], in_=x1[0:P].rearrange("b j d -> b (j d)"))
        w1_raw = keep.tile([P, PASSES * PACK * S1], BF16, name="w1_raw")
        nc.sync.dma_start(
            out=w1_raw.rearrange("p (g n) -> p g n", n=S1),
            in_=w1.rearrange("(g p) n -> p g n", p=P),
        )
        b_row = keep.tile([P, S1 + S2], BF16, name="b_row")
        nc.vector.memset(b_row[:], 0.0)
        ones = keep.tile([P, P], BF16, name="ones")
        nc.vector.memset(ones[:], 1.0)
        nc.sync.dma_start(out=b_row[0:1, 0:S1], in_=b1.unsqueeze(0))
        nc.sync.dma_start(out=b_row[0:1, S1 : S1 + S2], in_=b2.unsqueeze(0))
        b1_rows = keep.tile([P, S1], BF16, name="b1_rows")
        b1_col = keep.tile([P, 1], F32, name="b1_col")
        w2_raw = {}

        def load_w2(c):
            for h in range(HALVES):
                w2_raw[c, h] = raw_pool.tile([P, PACK * N2], BF16, name="w2_raw")
                nc.sync.dma_start(
                    out=w2_raw[c, h].rearrange("p (t n) -> p t n", t=PACK),
                    in_=w2[c * PACK * P : (c + 1) * PACK * P, h * N2 : (h + 1) * N2].rearrange(
                        "(t p) n -> p t n", p=P
                    ),
                )

        load_w2(0)
        load_w2(1)
        b2_rows = keep.tile([P, S2], BF16, name="b2_rows")

        ident_f = keep.tile([P, P], F32, name="ident_f")
        make_identity(nc, ident_f[:])

        x_fields = keep.tile([P, SAMPLE_TILES * F0 * D], BF16, name="x_fields")
        for s in range(SAMPLE_TILES):
            nc.vector.tensor_copy(
                out=x_fields.rearrange("p (s d c t) -> p s d c t", s=SAMPLE_TILES, d=D, c=PASSES)[:, s],
                in_=x_sb.rearrange("p (s c t d) -> p s d c t", s=SAMPLE_TILES, d=D, c=PASSES)[:, s],
            )
        x_words = x_fields[:].bitcast(F32)

        x_all = [keep.tile([P, PASSES * ROWS * 2], F32, name="x_all%d" % r) for r in range(ROUNDS)]
        round_words = PASSES * ROWS * 2
        parked = out.rearrange("a n -> (a n)")[0 : ROUNDS * round_words]

        def load_x_all(r, parts=1):
            words = round_words // parts
            for n in range(parts):
                first = r * round_words + n * words
                nc.sync.dma_start(
                    out=x_all[r][:, n * words : (n + 1) * words],
                    in_=parked[first : first + words].partition_broadcast(P),
                )

        x_turned_ps = {}
        park = []

        x_blocks = keep.tile([P, 3 * HALF_P], F32, name="x_blocks")

        def sort_x():
            for block, u in enumerate((0, 1, 0)):
                nc.vector.tensor_copy(
                    out=x_blocks[:, block * HALF_P : (block + 1) * HALF_P].rearrange(
                        "p (a c dl) -> p a c dl", c=PASSES, dl=D_ROUND
                    ),
                    in_=x_words.rearrange("p (a dl c u) -> p u a c dl", dl=D_ROUND, c=PASSES, u=2)[:, u],
                )

        def turn_x():
            x_turned_ps[0] = bank.tile([P, N2], F32, name="x_turned_ps", tag="o1_turned")
            for u in range(2):
                nc.tensor.transpose(
                    x_turned_ps[0][:, u * P : (u + 1) * P], x_blocks[:, u * HALF_P : u * HALF_P + P], ident_f[:]
                )

        def park_x():
            x_turned = keep.tile([P, 2 * P], F32, name="x_turned")
            nc.vector.tensor_copy(
                out=x_turned.rearrange("p (b u) -> p b u", u=2),
                in_=x_turned_ps[0][:, 0 : 2 * P].rearrange("p (u b) -> p b u", u=2),
            )
            park.append(x_turned)

        def load_x():
            nc.scalar.dma_start(out=parked.rearrange("(p w) -> p w", w=2 * P), in_=park[0][0:HALF_P, :])
            load_x_all(2)
            nc.sync.dma_start(out=x1_sb[1][:], in_=x1[P : 2 * P].rearrange("b j d -> b (j d)"))
            load_x_all(3)
            for r in range(4, ROUNDS):
                load_x_all(r)

        x_f32 = keep.tile([P, SAMPLE_TILES * F0 * D], F32, name="x_f32")

        x1_by_d = {}
        x1_t = {}
        x1_twice = {}
        z_in = {}
        z_codes = {}
        z_scales = {}
        o1 = {}
        o1_gp = {}
        o1_turned_ps = {}
        o1_turned = {}
        z2_turned = {}
        z2_back = {}
        sums = {}
        sum_o1 = {}
        result = {}

        x_banks = (("sum_0", "sum_1", "sum_2", "scal"), ("sum_0", "sum_1", "o1_turned", "sum_o1"))

        x_bank_of = {}

        def spread_x(r, positions=range(D_ROUND)):
            for dl in positions:
                x_bank = bank.tile([P, N2], F32, name="x_bank%d_%d" % (r, dl), tag=x_banks[r][dl])
                x_bank_of[r, dl] = x_bank
                for cu in range(PACK):
                    word = (r * D_ROUND + dl) * PACK + cu
                    nc.tensor.transpose(
                        x_bank[:, cu * P : (cu + 1) * P],
                        x_words[:, word : word + 1].to_broadcast([P, P]),
                        ident_f[:],
                    )

        def collect_x(copy, r, dl):
            copy(
                out=x_all[r].rearrange("p (c w u) -> p c w u", c=PASSES, u=2)[:, :, dl * P : (dl + 1) * P, :],
                in_=x_bank_of[r, dl].rearrange("p (c u b) -> p c b u", c=PASSES, u=2),
            )

        def sort_x1(r, dl0=0, dls=D_ROUND):
            s, d0 = r // ROUNDS_PER_TILE, (r % ROUNDS_PER_TILE) * D_ROUND + dl0
            if dl0 == 0:
                x1_by_d[r] = two.tile([P, ROWS * 2], BF16, name="x1_by_d")
            nc.scalar.copy(
                out=x1_by_d[r].rearrange("p (d j e) -> p d j e", d=D_ROUND, e=2)[:, dl0 : dl0 + dls],
                in_=x1_sb[s]
                .rearrange("p (j d) -> p d j", d=D)[:, d0 : d0 + dls, :]
                .unsqueeze(3)
                .to_broadcast([P, dls, FK, 2]),
            )

        def turn_x1(r, dl0=0, dls=D_ROUND):
            if dl0 == 0:
                x1_t[r] = bank.tile([P, ROWS], F32, name="x1_t")
            for dl in range(dl0, dl0 + dls):
                nc.tensor.transpose(
                    x1_t[r][:, dl * P : (dl + 1) * P],
                    x1_by_d[r][:].bitcast(F32)[:, dl * P : (dl + 1) * P],
                    ident_f[:],
                )

        def x_of_pass(r, c, row0, rows):
            first = (c * ROWS + row0) * PACK
            return x_all[r][:].bitcast(BF16)[:, first : first + rows * PACK].rearrange("p (w t) -> p w t", t=PACK)

        def new_z(layer, r):
            words = PASSES * ROWS if layer == 1 else DVE_WORDS + ACT_WORDS
            z_in[layer, r] = two.tile([P, words * PACK], BF16, name="z%d_in" % layer, align_bytes=64)
            z_codes[layer, r] = three.tile([P, words], U32, name="z%d_codes" % layer, align_bytes=64)
            z_scales[layer, r] = three.tile([P, words], U8, name="z%d_scales" % layer, align_bytes=64)

        def new_z_gp(r):
            z_in["gp", r] = keep_gp.tile([P, GP_WORDS * PACK], BF16, name="zg_in", align_bytes=64)
            z_codes["gp", r] = three.tile([P, GP_WORDS], U32, name="zg_codes", align_bytes=64)
            z_scales["gp", r] = three.tile([P, GP_WORDS], U8, name="zg_scales", align_bytes=64)

        def word_col(layer, c, dl, r=-1):
            if layer == 1 and r == 0:
                return ((dl // 2 * PASSES + c) * 2 + dl % 2) * P
            if layer == 1:
                return (c * D_ROUND + dl) * P
            if dl in DVE_DS:
                return c * DVE_ROWS + DVE_DS.index(dl) * P
            if dl in ACT_DS:
                return DVE_WORDS + ACT_DS.index(dl) * ACT_WORDS + c * P
            return c * GP_ROWS + GP_DS.index(dl) * P

        def z2_key(r, dl):
            return ("gp" if dl in GP_DS else 2, r)

        def z2_of(r, c, dl, rows):
            first = word_col(2, c, dl) * PACK
            return z_in[z2_key(r, dl)][:, first : first + rows * PACK]

        def multiply1(r, c, dl0=0, dls=D_ROUND):
            first, rows = word_col(1, c, dl0, r) * PACK, dls * P
            nc.vector.tensor_tensor(
                out=z_in[1, r][:, first : first + rows * PACK].rearrange("p (w u e) -> p w u e", u=2, e=2),
                in0=x1_t[r][:, dl0 * P : dl0 * P + rows]
                .bitcast(BF16)
                .rearrange("p (w e) -> p w e", e=2)
                .unsqueeze(2)
                .to_broadcast([P, rows, 2, 2]),
                in1=x_of_pass(r, c, dl0 * P, rows).rearrange("p w (u e) -> p w u e", e=2),
                op=MULT,
            )

        def multiply2_vector(r, c, dl, col0, rows):
            nc.vector.scalar_tensor_tensor(
                out=z2_of(r, c, dl, rows).rearrange("p (w t) -> p w t", t=PACK),
                in0=o1[r][:, col0 : col0 + rows].unsqueeze(2).to_broadcast([P, rows, PACK]),
                scalar=b1_col[:, 0:1],
                in1=x_of_pass(r, c, dl * P, rows),
                op0=ADD,
                op1=MULT,
            )

        def multiply2(r, c):
            multiply2_vector(r, c, DVE_DS[0], 0, DVE_ROWS - GP_EXTRA[r])

        def multiply2_gpsimd(r, out_words, o1_col0, x_row0, rows):
            nc.gpsimd.tensor_tensor(
                out=out_words,
                in0=o1_gp[r][:, o1_col0 : o1_col0 + rows]
                .unsqueeze(1)
                .unsqueeze(3)
                .to_broadcast([P, PASSES, rows, PACK]),
                in1=x_all[r][:].bitcast(BF16).rearrange("p (c w t) -> p c w t", c=PASSES, t=PACK)[
                    :, :, x_row0 : x_row0 + rows, :
                ],
                op=MULT,
            )

        def multiply2_gpsimd_extra(r):
            row0 = DVE_ROWS - GP_EXTRA[r]
            words = z_in[2, r][:, 0 : DVE_WORDS * PACK].rearrange("p (c w t) -> p c w t", c=PASSES, t=PACK)
            multiply2_gpsimd(r, words[:, :, row0:DVE_ROWS, :], 0, row0, GP_EXTRA[r])

        def multiply2_gpsimd_own(r):
            new_z_gp(r)
            words = z_in["gp", r].rearrange("p (c w t) -> p c w t", c=PASSES, t=PACK)
            multiply2_gpsimd(r, words, GP_EXTRA[r], GP_DS[0] * P, GP_ROWS)

        def quantise(layer, r, word0, words):
            nc.vector.quantize_mx(
                out=z_codes[layer, r][:, word0 : word0 + words].bitcast(FP8X4),
                scales=z_scales[layer, r][:, word0 : word0 + words],
                in_=z_in[layer, r][:, word0 * PACK : (word0 + words) * PACK],
            )

        def layer1(r, half=None):
            def with_w1_stationary(target, dl0, dls):
                for c in range(PASSES):
                    first = word_col(1, c, dl0, r)
                    nc.tensor.matmul_mx(
                        out=target,
                        lhsT=w1_codes[:, c * S1 : (c + 1) * S1].bitcast(FP8X4),
                        lhsT_scale=w1_scales[:, c * S1 : (c + 1) * S1],
                        rhs=z_codes[1, r][:, first : first + dls * P].bitcast(FP8X4),
                        rhs_scale=z_scales[1, r][:, first : first + dls * P],
                        start=(c == 0),
                        stop=(c == PASSES - 1),
                    )

            def turned_rows():
                o1_turned_ps[r] = bank.tile([P, N2], F32, name="o1_turned")
                for n, dl in enumerate(ACT_DS):
                    for c in range(PASSES):
                        block = slice(word_col(1, c, dl, r), word_col(1, c, dl, r) + P)
                        nc.tensor.matmul_mx(
                            out=o1_turned_ps[r][:, n * S1 : (n + 1) * S1],
                            lhsT=z_codes[1, r][:, block].bitcast(FP8X4),
                            lhsT_scale=z_scales[1, r][:, block],
                            rhs=w1_codes[:, c * S1 : (c + 1) * S1].bitcast(FP8X4),
                            rhs_scale=w1_scales[:, c * S1 : (c + 1) * S1],
                            start=(c == 0),
                            stop=(c == PASSES - 1),
                        )

            def copy_for_gpsimd(col, source):
                nc.scalar.activation(
                    out=o1_gp[r][:, col : col + source.shape[1]], in_=source, func=IDENTITY, bias=b1_col[:, 0:1]
                )

            if half != 1:
                o1[r] = bank.tile([P, ROWS], F32, name="o1")
                o1_gp[r] = two.tile([P, P + GP_ROWS], F32, name="o1_gp")
            if r == ROUNDS - 1:
                with_w1_stationary(o1[r][:], 0, D_ROUND)
                return
            if r in ROUTED and half != 0:
                turned_rows()
            if half != 1:
                with_w1_stationary(o1[r][:, 0:DVE_ROWS], DVE_DS[0], len(DVE_DS))
                if GP_EXTRA[r]:
                    copy_for_gpsimd(0, o1[r][:, DVE_ROWS - GP_EXTRA[r] : DVE_ROWS])
            if half != 0:
                o1_apart = bank.tile([P, N2], F32, name="o1_apart", tag="scal")
                with_w1_stationary(o1_apart[:, 0:GP_ROWS], GP_DS[0], 1)
                copy_for_gpsimd(GP_EXTRA[r], o1_apart[:, 0:GP_ROWS])

        def add_b1_turned(r):
            width = len(ACT_DS) * S1
            o1_turned[r] = two.tile([P, width], F32, name="o1_turned")
            nc.vector.tensor_tensor(
                out=o1_turned[r].rearrange("p (n j) -> p n j", j=S1),
                in0=o1_turned_ps[r][:, 0:width].rearrange("p (n j) -> p n j", j=S1),
                in1=b1_rows[:].unsqueeze(1).to_broadcast([P, len(ACT_DS), S1]),
                op=ADD,
            )

        def sum_turned(r):
            s = r // ROUNDS_PER_TILE
            if s not in result:
                result[s] = two.tile([P, S1 + S2], F32, name="result")
                nc.vector.scalar_tensor_tensor(
                    out=result[s][:, 0:S1], in0=b1_rows[:], scalar=float(D), in1=o1_turned_ps[r][:, 0:S1], op0=MULT, op1=ADD
                )
            else:
                nc.vector.tensor_tensor(
                    out=result[s][:, 0:S1], in0=o1_turned_ps[r][:, 0:S1], in1=result[s][:, 0:S1], op=ADD
                )

        def multiply2_scalar(r):
            s = r // ROUNDS_PER_TILE
            z2_turned[r] = two.tile([P, len(ACT_DS) * F0 * S1], BF16, name="z2_turned")
            for n, dl in enumerate(ACT_DS):
                for i in range(F0):
                    col = (s * F0 + i) * D + (r % ROUNDS_PER_TILE) * D_ROUND + dl
                    nc.scalar.activation(
                        out=z2_turned[r].rearrange("p (n g j e) -> p n g e j", n=len(ACT_DS), g=F0 // 2, e=2)[
                            :, n, i // 2, i % 2
                        ],
                        in_=o1_turned[r][:, n * S1 : (n + 1) * S1],
                        func=COPY,
                        scale=x_f32[:, col : col + 1],
                    )

        def turn_z2(r, n):
            z2_back[r, n] = bank.tile([P, N2], F32, name="z2_back", tag="scal")
            for g in range(F0 // 2):
                word0 = (n * (F0 // 2) + g) * P
                nc.tensor.transpose(
                    z2_back[r, n][:, g * P : (g + 1) * P],
                    z2_turned[r][:].bitcast(F32)[:, word0 : word0 + P],
                    ident_f[:],
                )

        def collect_z2(r, n):
            nc.scalar.copy(
                out=z2_of(r, 0, ACT_DS[n], PASSES * P)
                .bitcast(F32)
                .rearrange("p (c b u) -> p c b u", c=PASSES, u=2),
                in_=z2_back[r, n].rearrange("p (c u b) -> p c b u", c=PASSES, u=2),
            )

        def pooled(r, blocks, first=False, last=False, halves=range(HALVES)):
            s = r // ROUNDS_PER_TILE
            for h in halves:
                if first:
                    sums[s, h] = bank.tile([P, N2], F32, name="sum_o2_%d" % h, tag="sum_%d" % ((2 * s + h) % 3))
                for n, (c, dl) in enumerate(blocks):
                    key = z2_key(r, dl)
                    block = slice(word_col(2, c, dl), word_col(2, c, dl) + P)
                    w_cols = slice(c * S2 + h * N2, c * S2 + (h + 1) * N2)
                    nc.tensor.matmul_mx(
                        out=sums[s, h][:],
                        lhsT=z_codes[key][:, block].bitcast(FP8X4),
                        lhsT_scale=z_scales[key][:, block],
                        rhs=w2_codes[:, w_cols].bitcast(FP8X4),
                        rhs_scale=w2_scales[:, w_cols],
                        start=(first and n == 0),
                        stop=(last and n == len(blocks) - 1),
                    )

        def pooled_o1(r):
            s, q = r // ROUNDS_PER_TILE, r % ROUNDS_PER_TILE
            if q == 0:
                sum_o1[s] = bank.tile([P, N2], F32, name="sum_o1")
            ds = [dl for dl in range(D_ROUND) if dl not in ACT_DS or r not in SUMMED_BY_VECTOR]
            for c in range(PASSES):
                for dl in ds:
                    block = slice(word_col(1, c, dl, r), word_col(1, c, dl, r) + P)
                    nc.tensor.matmul_mx(
                        out=sum_o1[s][:, 0:S1],
                        lhsT=z_codes[1, r][:, block].bitcast(FP8X4),
                        lhsT_scale=z_scales[1, r][:, block],
                        rhs=w1_codes[:, c * S1 : (c + 1) * S1].bitcast(FP8X4),
                        rhs_scale=w1_scales[:, c * S1 : (c + 1) * S1],
                        start=(q == 0 and c == 0 and dl == ds[0]),
                        stop=(q == ROUNDS_PER_TILE - 1 and c == PASSES - 1 and dl == ds[-1]),
                    )

        def finish(s, col, width, bias, total):
            if s not in result:
                result[s] = two.tile([P, S1 + S2], F32, name="result")
            nc.vector.scalar_tensor_tensor(
                out=result[s][:, col : col + width],
                in0=bias,
                scalar=float(D),
                in1=total,
                op0=MULT,
                op1=ADD,
            )
            nc.sync.dma_start(out=out[s * P : (s + 1) * P, col : col + width], in_=result[s][:, col : col + width])

        def finish_o1(s):
            if s not in result:
                finish(s, 0, S1, b1_rows[:], sum_o1[s][:, 0:S1])
                return
            nc.vector.tensor_tensor(
                out=result[s][:, 0:S1], in0=sum_o1[s][:, 0:S1], in1=result[s][:, 0:S1], op=ADD
            )
            nc.sync.dma_start(out=out[s * P : (s + 1) * P, 0:S1], in_=result[s][:, 0:S1])

        def finish_o2(s, h, pieces=1):
            width = N2 // pieces
            for col in range(0, N2, width):
                finish(
                    s, S1 + h * N2 + col, width, b2_rows[:, h * N2 + col : h * N2 + col + width], sums[s, h][:, col : col + width]
                )

        def regroup(copy, dst, src):
            copy(
                out=dst.rearrange("p (g i t) -> p g t i", i=4, t=PACK),
                in_=src.rearrange("p t (g i) -> p g t i", i=4),
            )

        def quantise_weights(codes, scales, grouped):
            nc.vector.quantize_mx(out=codes.bitcast(FP8X4), scales=scales, in_=grouped)

        def spread_b1():
            b1_ps = bank.tile([P, N2], F32, name="b1_ps", tag="o1")
            nc.tensor.matmul(out=b1_ps[:, 0:S1], lhsT=ones[:], rhs=b_row[:, 0:S1], start=True, stop=True)
            nc.tensor.matmul(out=b1_ps[:, S1 : 2 * S1], lhsT=b_row[:, 0:S1], rhs=ones[:], start=True, stop=True)
            nc.scalar.copy(out=b1_rows[:], in_=b1_ps[:, 0:S1])
            nc.scalar.copy(out=b1_col[:], in_=b1_ps[:, S1 : S1 + 1])

        def spread_b2(h):
            cols = slice(h * N2, (h + 1) * N2)
            b2_ps = bank.tile([P, N2], F32, name="b2_ps", tag="sum_2")
            nc.tensor.matmul(
                out=b2_ps[:], lhsT=ones[:], rhs=b_row[:, S1 + h * N2 : S1 + (h + 1) * N2], start=True, stop=True
            )
            nc.scalar.copy(out=b2_rows[:, cols], in_=b2_ps[:])

        w2_jobs = {}

        def regroup_w2(copies, c, h):
            if (c, h) == (0, 1):
                w2_grouped = keep_gp.tile([P, N2 * PACK], BF16, name="w2_last", tag="zg_in", align_bytes=64)
            else:
                w2_grouped = raw_pool.tile([P, N2 * PACK], BF16, name="w2_grouped", align_bytes=64)
            cols = slice(c * S2 + h * N2, c * S2 + (h + 1) * N2)
            w2_jobs[c, h] = (w2_codes[:, cols], w2_scales[:, cols], w2_grouped[:])
            for n, copy in enumerate(copies):
                regroup_part(copy, c, h, n, N2 // len(copies))

        def regroup_part(copy, c, h, n, width):
            regroup(
                copy,
                w2_jobs[c, h][2][:, n * width * PACK : (n + 1) * width * PACK],
                w2_raw[c, h].rearrange("p (t n) -> p t n", t=PACK)[:, :, n * width : (n + 1) * width],
            )

        v_copy, s_copy = nc.vector.tensor_copy, nc.scalar.copy

        w1_grouped = keep.tile([P, PASSES * S1 * PACK], BF16, name="w1_grouped", align_bytes=64)
        w1_codes = keep.tile([P, PASSES * S1], U32, name="w1_codes", align_bytes=64)
        w1_scales = keep.tile([P, PASSES * S1], U8, name="w1_scales", align_bytes=64)
        w2_codes = keep.tile([P, PASSES * S2], U32, name="w2_codes", align_bytes=64)
        w2_scales = keep.tile([P, PASSES * S2], U8, name="w2_scales", align_bytes=64)
        dve_blocks = [(c, dl) for c in range(PASSES) for dl in DVE_DS]
        act_blocks = [(c, dl) for dl in ACT_DS for c in range(PASSES)]
        gp_blocks = [(c, dl) for c in range(PASSES) for dl in GP_DS]
        per_pass = len(DVE_DS)
        act_words0 = DVE_WORDS

        def regroup_w1(c):
            part = slice(c * S1 * PACK, (c + 1) * S1 * PACK)
            nc.gpsimd.tensor_scalar(
                out=w1_grouped[:, part].rearrange("p (n t) -> p n t", t=PACK),
                in0=w1_raw[:, part].rearrange("p (t n) -> p n t", t=PACK),
                scalar1=1.0,
                scalar2=0.0,
                op0=MULT,
                op1=ADD,
            )

        def transposes(r):
            for n in range(len(ACT_DS) if (r in ROUTED) else 0):
                turn_z2(r, n)
            if r + 2 < ROUNDS:
                turn_x1(r + 2)
            for n in range(len(ACT_DS) if (r in ROUTED) else 0):
                collect_z2(r, n)

        def multiply2_act_d(r):
            if (r in ROUTED):
                add_b1_turned(r)
                multiply2_scalar(r)

        def multiply2_act_d_vector(r):
            if not (r in ROUTED):
                for n, dl in enumerate(ACT_DS):
                    for c in range(PASSES):
                        multiply2_vector(r, c, dl, dl * P, P)

        def quantise_act_d(r):
            quantise(2, r, act_words0, len(ACT_DS) * ACT_WORDS)

        sort_x()
        sort_x1(0, 0, 2)
        spread_x(0, (0,))
        collect_x(s_copy, 0, 0)
        sort_x1(0, 2, 2)
        turn_x()
        park_x()
        load_x()
        for c in range(PASSES):
            regroup_w1(c)
        spread_x(0, (1,))
        collect_x(v_copy, 0, 1)
        turn_x1(0, 0, 2)
        spread_x(0, (2, 3))
        collect_x(s_copy, 0, 2)
        collect_x(s_copy, 0, 3)
        spread_b1()
        spread_x(1, (3, 2))
        new_z(1, 0)
        new_z(2, 0)
        for c in range(PASSES):
            multiply1(0, c, 0, 2)
        turn_x1(0, 2, 2)
        spread_x(1, (1, 0))
        quantise_weights(w1_codes[:], w1_scales[:], w1_grouped[:])
        for dl in reversed(range(D_ROUND)):
            collect_x(s_copy, 1, dl)
        quantise(1, 0, 0, ROWS)
        layer1(0, 0)
        sort_x1(1)
        sort_x1(2)
        for c in range(PASSES):
            multiply1(0, c, 2, 2)
        regroup_w2([v_copy], 0, 0)
        quantise(1, 0, ROWS, ROWS)
        regroup_w2([s_copy], 1, 0)
        layer1(0, 1)
        pooled_o1(0)
        turn_x1(1)
        for c in range(PASSES):
            multiply2(0, c)
        multiply2_gpsimd_extra(0)
        regroup_w2([v_copy], 0, 1)
        for h in range(HALVES):
            quantise_weights(*w2_jobs[0, h])
        quantise(2, 0, 0, DVE_WORDS)
        pooled(0, dve_blocks[0:per_pass], first=True)
        multiply2_gpsimd_own(0)
        new_z(1, 1)
        multiply1(1, 0)
        regroup_w2([s_copy], 1, 1)
        nc.scalar.copy(out=x_f32[:], in_=x_sb[:])
        multiply2_act_d(0)
        multiply1(1, 1)
        turn_x1(2)
        for h in range(HALVES):
            quantise_weights(*w2_jobs[1, h])
        turn_z2(0, 0)
        collect_z2(0, 0)
        pooled(0, dve_blocks[per_pass:])
        quantise(1, 1, 0, PASSES * ROWS)
        layer1(1)
        pooled_o1(1)

        late = []
        for r in range(1, ROUNDS):
            s, q = r // ROUNDS_PER_TILE, r % ROUNDS_PER_TILE
            ahead = r + 1 < ROUNDS
            new_z(2, r)
            if ahead:
                new_z(1, r + 1)
                multiply1(r + 1, 0)
            if r == 1:
                quantise_act_d(0)
                pooled(0, act_blocks)
            multiply2_act_d(r)
            if r + 2 < ROUNDS:
                sort_x1(r + 2)
            if ahead:
                multiply1(r + 1, 1)
            if r in SUMMED_BY_VECTOR:
                sum_turned(r)
            if q == 1 and s > 0:
                finish_o2(s - 1, 0)
            if r > 1:
                multiply2_gpsimd_own(r - 1)
            if ahead:
                multiply2_gpsimd_extra(r)
            for c in range(PASSES):
                multiply2(r, c)
            transposes(r)
            if 0 < r <= HALVES:
                spread_b2(r - 1)
            if q == 1 and s > 0:
                pooled(r - 1, dve_blocks + act_blocks, first=True, halves=(1,))
            for g in late:
                pooled(g, gp_blocks)
            late = []
            if q == ROUNDS_PER_TILE - 1:
                finish_o1(s)
            if ahead:
                quantise(1, r + 1, 0, PASSES * ROWS)
                layer1(r + 1)
                pooled_o1(r + 1)
            if q == 0:
                quantise(2, r, 0, DVE_WORDS)
                quantise_act_d(r)
                quantise("gp", r - 1, 0, GP_WORDS)
                pooled(r - 1, gp_blocks, last=True)
                pooled(r, dve_blocks + act_blocks, first=True, halves=(0,))
            elif ahead:
                quantise(2, r, 0, DVE_WORDS)
                pooled(r, dve_blocks)
                quantise_act_d(r)
                pooled(r, act_blocks)
                quantise("gp", r - 1, 0, GP_WORDS)
                late.append(r - 1)
            else:
                quantise(2, r, 0, DVE_WORDS)
                quantise("gp", r - 1, 0, GP_WORDS)
                multiply2_act_d_vector(r)
                new_z_gp(r)
                for c in range(PASSES):
                    multiply2_vector(r, c, GP_DS[0], DVE_ROWS, P)
                pooled(r - 1, gp_blocks)
                pooled(r, dve_blocks)
                quantise_act_d(r)
                quantise("gp", r, 0, GP_WORDS)
                finish_o2(s - 1, 1)
                for h in range(HALVES):
                    pooled(r, act_blocks + gp_blocks, last=True, halves=(h,))
                    finish_o2(s, h, 2)
